import numpy as np
import ml_dtypes


def mxq(x, axis, fmt="e4m3"):
    dtype, down = {"e4m3": (ml_dtypes.float8_e4m3fn, 7), "e5m2": (ml_dtypes.float8_e5m2, 14)}[fmt]
    v = np.moveaxis(np.asarray(x, np.float32).astype(ml_dtypes.bfloat16).astype(np.float64), axis, -1)
    blocks = v.reshape(v.shape[:-1] + (-1, 32))
    amax = np.abs(blocks).max(-1, keepdims=True)
    byte = np.maximum(np.where(amax > 0, np.frexp(amax)[1] - 1 + 127, 0) - down, 1)
    scale = np.exp2(byte - 127.0)
    codes = (blocks / scale).astype(np.float32).astype(dtype).astype(np.float64)
    return np.moveaxis((codes * scale).reshape(v.shape), -1, axis)


WIDE = False


def mx_kscale(k):
    if not WIDE:
        return np.ones(k)
    levels = np.array([10, -10, 5, -5, 0])
    if k % 512:
        return np.exp2(np.random.permutation(np.resize(levels, k // 32))).repeat(32)
    a = np.empty((k // 512, 16))
    for p in range(k // 512):
        a[p, :8] = np.random.permutation(np.resize(levels, 8))
        for g in range(8):
            far = levels[np.abs(levels - a[p, g]) >= 10]
            a[p, g + 8] = far[np.random.randint(len(far))]
    return np.exp2(a.ravel()).repeat(32)


BF16 = ml_dtypes.bfloat16


def bf(x):
    return np.asarray(x, np.float32).astype(BF16)


def f64(x):
    return np.asarray(x).astype(np.float64)


B, T, D, DEPTH, F = 4, 1024, 1024, 4, 32
L = 2 ** DEPTH
N = L - 1
LF = L * F


def sigmoid(v):
    return 1.0 / (1.0 + np.exp(-v))


def leaf_probs(c):
    probs = np.ones(c.shape[:-1] + (1,))
    for m in range(DEPTH):
        start = 2 ** m - 1
        cl = c[..., start:start + 2 ** m]
        probs = np.stack([probs * cl, probs * (1.0 - cl)], axis=-1)
        probs = probs.reshape(probs.shape[:-2] + (-1,))
    return probs


def draw0():
    s = mx_kscale(D)
    t = mx_kscale(LF).reshape(L, F)
    return {"x": bf(np.random.standard_normal((B, T, D)) * s),
            "node_logits": bf(np.random.standard_normal((B, T, N)) * 1.5),
            "node_b": bf(np.random.standard_normal(N) * 0.5),
            "w1": bf(np.random.standard_normal((L, D, F)) / np.sqrt(D) / s[None, :, None] * t[:, None, :]),
            "b1": bf(np.random.standard_normal((L, F)) * 0.5 * t),
            "w2": bf(np.random.standard_normal((L, F, D)) * 2.0 / np.sqrt(F) / t[:, :, None])}


def core(x, node_logits, node_b, w1, b1, w2):
    probs = leaf_probs(sigmoid(f64(node_logits) + f64(node_b)))
    w1f = f64(w1).transpose(1, 0, 2).reshape(D, LF)
    a = mxq(f64(x), 2, "e4m3") @ mxq(w1f, 0, "e4m3")
    h = np.maximum(a.reshape(B, T, L, F) + f64(b1), 0.0) * probs[..., None]
    return mxq(h.reshape(B, T, LF), 2, "e4m3") @ mxq(f64(w2).reshape(LF, D), 0, "e4m3")


def e4m3fn_bytes(y):
    return np.clip(np.asarray(y, np.float64), -448.0, 448.0).astype(np.float32).astype(ml_dtypes.float8_e4m3fn).view(np.uint8)


def e4m3fn_values(b):
    return np.asarray(b, np.uint8).view(ml_dtypes.float8_e4m3fn).astype(np.float64)


def setup_inputs():
    d = draw0()
    x0 = np.asarray(d['x']).astype(np.float64)
    s = (np.max(np.abs(x0), axis=(0, 1), keepdims=True) / 448.0).astype(np.float32)
    out = {}
    for k, v in d.items():
        if k == 'x':
            out['x_bytes'] = e4m3fn_bytes(x0 / s.astype(np.float64))
            out['x_scale'] = s
        else:
            out[k] = v
    return out


def reference(x_bytes, x_scale, node_logits, node_b, w1, b1, w2):
    return core(e4m3fn_values(x_bytes) * x_scale.astype(np.float64), node_logits, node_b, w1, b1, w2)

@@ -1,0 +1,322 @@
+from contextlib import ExitStack
+
+import concourse.mybir as mybir
+from concourse.masks import make_identity
+
+F32 = mybir.dt.float32
+BF16 = mybir.dt.bfloat16
+U32 = mybir.dt.uint32
+U8 = mybir.dt.uint8
+FP8 = mybir.dt.float8_e4m3fn
+FP8X4 = mybir.dt.float8_e4m3fn_x4
+ACT = mybir.ActivationFunctionType
+OP = mybir.AluOpType
+
+P = 128
+TOKENS = 4096
+D = 1024
+LF = 512
+E = 1024
+LEAVES = 16
+NODES = 15
+TILES = TOKENS // P
+PAIRS = TILES // 2
+FLOPS = 2 * TOKENS * D * LF + 2 * TOKENS * LF * E
+
+X_CHUNKS = [(0, 1), (1, 2), (2, 4), (4, 8), (8, 12), (12, 16), (16, 20), (20, 24), (24, 28), (28, 32)]
+
+
+def tile_fastfeedforwardnetwork_pa_t_kernel(tc, x_bytes, x_scale, node_logits, node_b, w1, b1, w2, out):
+    nc = tc.nc
+    x_v = x_bytes.rearrange("b s k -> (b s) k").rearrange("(p i) k -> p i k", i=TILES)
+    out_v = out.rearrange("b s e -> (b s) e").rearrange("(p i) e -> p i e", i=TILES)
+    logits_v = node_logits.rearrange("b s v -> (b s) v").rearrange("(p i) v -> p (i v)", i=TILES)
+    scale_v = x_scale.rearrange("a b k -> (a b k)")
+    b1_v = b1.rearrange("l f -> (l f)").rearrange("(m t) -> m t", t=4)
+    w2_v = w2.rearrange("l f e -> (l f) e").rearrange("(p j) e -> p j e", j=4)
+
+    with ExitStack() as ctx:
+        keep = ctx.enter_context(tc.tile_pool(name="keep", bufs=1))
+        xs_pool = ctx.enter_context(tc.tile_pool(name="xs", bufs=4))
+        xg_pool = ctx.enter_context(tc.tile_pool(name="xg", bufs=2))
+        xq_pool = ctx.enter_context(tc.tile_pool(name="xq", bufs=2))
+        h_pool = ctx.enter_context(tc.tile_pool(name="h", bufs=2))
+        hq_pool = ctx.enter_context(tc.tile_pool(name="hq", bufs=3))
+        o_pool = ctx.enter_context(tc.tile_pool(name="o", bufs=4))
+        xt_psum = ctx.enter_context(tc.psum_pool(name="xt_psum", bufs=2))
+        a_psum = ctx.enter_context(tc.psum_pool(name="a_psum", bufs=2))
+        p_psum = ctx.enter_context(tc.psum_pool(name="p_psum", bufs=1))
+        o_psum = ctx.enter_context(tc.psum_pool(name="o_psum", bufs=3))
+        ctx.enter_context(tc.manual_schedule())
+
+        x8 = {}
+
+        def load_x(a, b):
+            t = keep.tile([P, b - a, D], U8, name=f"x8_{a}")
+            nc.sync.dma_start(out=t[:], in_=x_v[:, a:b, :])
+            for i in range(a, b):
+                x8[i] = t[:, i - a, :]
+
+        logits = keep.tile([P, TILES * NODES], BF16, name="logits")
+        nc.scalar.dma_start(out=logits[:], in_=logits_v)
+        bias_n = keep.tile([P, NODES], BF16, name="bias_n")
+        nc.scalar.dma_start(out=bias_n[:], in_=node_b.partition_broadcast(P))
+        bias_h = keep.tile([P, 4], BF16, name="bias_h")
+        nc.scalar.dma_start(out=bias_h[:], in_=b1_v)
+
+        load_x(0, 1)
+        scale = keep.tile([P, D], F32, name="scale")
+        nc.sync.dma_start(out=scale[:, 0:512], in_=scale_v[0:512].partition_broadcast(P))
+        nc.sync.dma_start(out=scale[:, 512:1024], in_=scale_v[512:1024].partition_broadcast(P))
+        w1_raw = keep.tile([P, 2, LEAVES, P], BF16, name="w1_raw")
+
+        def load_w1(g):
+            nc.sync.dma_start(
+                out=w1_raw[:, g, :, :],
+                in_=w1[:, 512 * g : 512 * (g + 1), :].rearrange("l (p j) f -> p l (j f)", j=4),
+            )
+
+        load_w1(0)
+        load_x(1, 2)
+        load_x(2, 4)
+        load_w1(1)
+        load_x(4, 8)
+        w2_raw = keep.tile([P, 4, E], BF16, name="w2_raw")
+        nc.sync.dma_start(out=w2_raw[:], in_=w2_v)
+        for a, b in X_CHUNKS[4:]:
+            load_x(a, b)
+
+        warm = keep.tile([P, 1], F32, name="warm")
+        nc.gpsimd.memset(warm[:], 0.0)
+        nc.scalar.activation(out=warm[:], in_=warm[:], func=ACT.Sigmoid)
+        ident = keep.tile([P, P], F32, name="ident")
+        make_identity(nc, ident[:])
+
+        z = keep.tile([P, TILES, NODES], F32, name="z")
+        nc.gpsimd.tensor_tensor(
+            out=z[:],
+            in0=logits[:].rearrange("p (i v) -> p i v", v=NODES),
+            in1=bias_n[:].unsqueeze(1).to_broadcast([P, TILES, NODES]),
+            op=OP.add,
+        )
+        gate = keep.tile([P, 2, TILES, NODES], F32, name="gate")
+        nc.scalar.activation(out=gate[:, 0, :, :], in_=z[:], func=ACT.Sigmoid)
+        nc.scalar.activation(out=gate[:, 1, :, :], in_=z[:], func=ACT.Sigmoid, scale=-1.0)
+        prob = gate[:, :, :, 0].rearrange("p s i -> p i s")
+        for level in range(1, 4):
+            n = 2**level
+            nxt = keep.tile([P, TILES, n, 2], F32, name=f"prob{level}")
+            nc.gpsimd.tensor_tensor(
+                out=nxt[:],
+                in0=prob.unsqueeze(3).to_broadcast([P, TILES, n, 2]),
+                in1=gate[:, :, :, n - 1 : 2 * n - 1].rearrange("p s i a -> p i a s"),
+                op=OP.mult,
+            )
+            prob = nxt[:].rearrange("p i a s -> p i (a s)")
+        leaf = prob
+
+        w1_g = keep.tile([P, 2, LF, 4], BF16, name="w1_g", align_bytes=64)
+        w1_c = keep.tile([P, 2, LF], U32, name="w1_c", align_bytes=64)
+        w1_s = keep.tile([P, 2, LF], U8, name="w1_s", align_bytes=64)
+        w2_g = keep.tile([P, E, 4], BF16, name="w2_g", align_bytes=64)
+        w2_c = keep.tile([P, E], U32, name="w2_c", align_bytes=64)
+        w2_s = keep.tile([P, E], U8, name="w2_s", align_bytes=64)
+
+        def w1_interleave(copy, g, t):
+            copy(
+                out=w1_g[:, g, P * t : P * (t + 1), :].rearrange("p (l h) j -> p l h j", h=8),
+                in_=w1_raw[:, g, :, :].rearrange("p l (j h t) -> p l h j t", h=8, t=4)[:, :, :, :, t],
+            )
+
+        def w1_quantize(g):
+            nc.vector.quantize_mx(
+                out=w1_c[:, g, :].bitcast(FP8X4),
+                scales=w1_s[:, g, :],
+                in_=w1_g[:, g, :, :].rearrange("p n j -> p (n j)"),
+            )
+
+        def w2_interleave(copy, a, b):
+            copy(
+                out=w2_g[:, a:b, :].rearrange("p (c i) j -> p c j i", i=4),
+                in_=w2_raw[:, :, a:b].rearrange("p j (c i) -> p c j i", i=4),
+            )
+
+        def w2_quantize(a, b):
+            nc.vector.quantize_mx(
+                out=w2_c[:, a:b].bitcast(FP8X4),
+                scales=w2_s[:, a:b],
+                in_=w2_g[:, a:b, :].rearrange("p e j -> p (e j)"),
+            )
+
+        xs, xt, xg, xq, hp, pt, a_bank, h1, hg, hq, o_bank, o_sb, prep = ({} for unused in range(13))
+
+        def widen(i, parts=1):
+            xs[i] = xs_pool.tile([P, D], BF16, name="xs")
+            w = D // parts
+            for c in range(parts):
+                cols = slice(c * w, (c + 1) * w)
+                nc.vector.tensor_tensor(
+                    out=xs[i][:, cols], in0=x8[i][:, cols].bitcast(FP8), in1=scale[:, cols], op=OP.mult
+                )
+
+        def turn_x(i):
+            xt[i] = xt_psum.tile([P, 2, 2, P], F32, name="xt")
+            words = xs[i][:].bitcast(F32)
+            for g in range(2):
+                for u in range(2):
+                    nc.tensor.transpose(
+                        xt[i][:, g, u, :], words[:, 256 * g + u : 256 * (g + 1) : 2], ident[:]
+                    )
+
+        def leave_x(i):
+            m, j = i // 2, i % 2
+            if j == 0:
+                xg[m] = xg_pool.tile([P, 2, 256, 4], BF16, name="xg", align_bytes=64)
+            words = xg[m][:].rearrange("p g n t -> p g (n t)").bitcast(F32)
+            nc.scalar.copy(
+                out=words[:, :, 256 * j : 256 * (j + 1)].rearrange("p g (n u) -> p g n u", u=2),
+                in_=xt[i][:].rearrange("p g u n -> p g n u"),
+            )
+
+        def quant_x(m):
+            xq[m] = (
+                xq_pool.tile([P, 512], U32, name="xq_c", align_bytes=64),
+                xq_pool.tile([P, 512], U8, name="xq_s", align_bytes=64),
+            )
+            nc.vector.quantize_mx(
+                out=xq[m][0][:].bitcast(FP8X4),
+                scales=xq[m][1][:],
+                in_=xg[m][:].rearrange("p g n t -> p (g n t)"),
+            )
+
+        def mm1(m, half):
+            a_bank[m, half] = a_psum.tile([P, 2, 256], F32, name="a")
+            for s in range(2):
+                t = 2 * half + s
+                for g in range(2):
+                    nc.tensor.matmul_mx(
+                        out=a_bank[m, half][:, s, :],
+                        lhsT=w1_c[:, g, P * t : P * (t + 1)].bitcast(FP8X4),
+                        lhsT_scale=w1_s[:, g, P * t : P * (t + 1)],
+                        rhs=xq[m][0][:, 256 * g : 256 * (g + 1)].bitcast(FP8X4),
+                        rhs_scale=xq[m][1][:, 256 * g : 256 * (g + 1)],
+                        start=(g == 0),
+                        stop=(g == 1),
+                    )
+
+        def leave_h(m, half):
+            if half == 0:
+                h1[m] = h_pool.tile([P, 64, 4, 4], F32, name="h1", align_bytes=64)
+            for s in range(2):
+                t = 2 * half + s
+                nc.scalar.activation(
+                    out=h1[m][:, :, t, :],
+                    in_=a_bank[m, half][:, s, :].rearrange("p (c i) -> p c i", i=4),
+                    func=ACT.Relu,
+                    bias=bias_h[:, t : t + 1],
+                )
+
+        def spread_p(g4):
+            prep[g4] = h_pool.tile([P, 512], F32, name="prep")
+            nc.vector.tensor_copy(
+                out=prep[g4][:].rearrange("p (c r) -> p c r", r=8),
+                in_=leaf[:, 4 * g4 : 4 * (g4 + 1), :]
+                .rearrange("p i l -> p (i l)")
+                .unsqueeze(2)
+                .to_broadcast([P, 64, 8]),
+            )
+
+        def turn_p(m):
+            pt[m] = p_psum.tile([P, 256], F32, name="pt")
+            for j in range(2):
+                c = 2 * (m % 2) + j
+                nc.tensor.transpose(
+                    pt[m][:, P * j : P * (j + 1)], prep[m // 2][:, P * c : P * (c + 1)], ident[:]
+                )
+
+        def weigh_h(m):
+            hg[m] = h_pool.tile([P, 1024], BF16, name="hg", align_bytes=64)
+            nc.vector.tensor_tensor(
+                out=hg[m][:].rearrange("p (c i t) -> p c i t", i=4, t=4),
+                in0=h1[m][:].rearrange("p c t i -> p c i t"),
+                in1=pt[m][:].rearrange("p (c i) -> p c i", i=4).unsqueeze(3).to_broadcast([P, 64, 4, 4]),
+                op=OP.mult,
+            )
+
+        def quant_h(m):
+            hq[m] = (
+                hq_pool.tile([P, 256], U32, name="hq_c", align_bytes=64),
+                hq_pool.tile([P, 256], U8, name="hq_s", align_bytes=64),
+            )
+            nc.vector.quantize_mx(out=hq[m][0][:].bitcast(FP8X4), scales=hq[m][1][:], in_=hg[m][:])
+
+        def mm2(i, e):
+            m, j = i // 2, i % 2
+            o_bank[i, e] = o_psum.tile([P, 512], F32, name="ob")
+            nc.tensor.matmul_mx(
+                out=o_bank[i, e][:],
+                lhsT=hq[m][0][:, P * j : P * (j + 1)].bitcast(FP8X4),
+                lhsT_scale=hq[m][1][:, P * j : P * (j + 1)],
+                rhs=w2_c[:, 512 * e : 512 * (e + 1)].bitcast(FP8X4),
+                rhs_scale=w2_s[:, 512 * e : 512 * (e + 1)],
+                start=True,
+                stop=True,
+            )
+
+        def leave_o(copy, i, e):
+            if e == 0:
+                o_sb[i] = o_pool.tile([P, E], F32, name="osb")
+            copy(out=o_sb[i][:, 512 * e : 512 * (e + 1)], in_=o_bank[i, e][:])
+            if e == 1:
+                nc.sync.dma_start(out=out_v[:, i, :], in_=o_sb[i][:])
+
+        for k in range(TILES + 10):
+            if k < TILES:
+                widen(k, 2 if k == 0 else 1)
+            if k in (2, 3):
+                w1_interleave(nc.vector.tensor_copy, 1, 2 * (k - 2))
+                w1_interleave(nc.vector.tensor_copy, 1, 2 * (k - 2) + 1)
+            if k % 2 == 1:
+                m = (k - 3) // 2
+                if 0 <= m < PAIRS:
+                    quant_x(m)
+                if k == 3:
+                    w1_quantize(0)
+                    w1_quantize(1)
+                if k % 4 == 3 and (k - 3) // 4 < 8:
+                    spread_p((k - 3) // 4)
+                m = (k - 7) // 2
+                if 0 <= m < PAIRS:
+                    quant_h(m)
+                if k == 7:
+                    w2_quantize(0, 512)
+            else:
+                if k == 8:
+                    w2_quantize(512, 1024)
+                m = k // 2 - 3
+                if 0 <= m < PAIRS:
+                    weigh_h(m)
+            if 0 <= k - 8 < TILES:
+                mm2(k - 8, 0)
+                mm2(k - 8, 1)
+            m = (k - 4) // 2
+            if 0 <= m < PAIRS:
+                mm1(m, k % 2)
+            if 0 <= k - 1 < TILES:
+                turn_x(k - 1)
+            if k % 2 == 1 and 0 <= (k - 5) // 2 < PAIRS:
+                turn_p((k - 5) // 2)
+            if k in (1, 2):
+                w1_interleave(nc.scalar.copy, 0, 2 * (k - 1))
+                w1_interleave(nc.scalar.copy, 0, 2 * (k - 1) + 1)
+            if 0 <= k - 8 < TILES:
+                leave_o(nc.scalar.copy, k - 8, 0)
+            if 0 <= m < PAIRS:
+                leave_h(m, k % 2)
+            if 0 <= k - 1 < TILES:
+                leave_x(k - 1)
+            if 4 <= k < 8:
+                w2_interleave(nc.scalar.copy, 256 * (k - 4), 256 * (k - 3))
+            if 0 <= k - 8 < TILES:
+                late = k >= TILES
+                leave_o(nc.vector.tensor_copy if late else nc.scalar.copy, k - 8, 1)

@@ -21,9 +21,10 @@ LEAVES = 16
 NODES = 15
 TILES = TOKENS // P
 PAIRS = TILES // 2
+QUADS = TILES // 4
 FLOPS = 2 * TOKENS * D * LF + 2 * TOKENS * LF * E
-
-X_CHUNKS = [(0, 1), (1, 2), (2, 4), (4, 8), (8, 12), (12, 16), (16, 20), (20, 24), (24, 28), (28, 32)]
+BF16_MAX = 3.3895313892515355e38
+LAG = 3
 
 
 def tile_fastfeedforwardnetwork_pa_t_kernel(tc, x_bytes, x_scale, node_logits, node_b, w1, b1, w2, out):
@@ -31,166 +32,192 @@ def tile_fastfeedforwardnetwork_pa_t_kernel(tc, x_bytes, x_scale, node_logits, n
     x_v = x_bytes.rearrange("b s k -> (b s) k").rearrange("(p i) k -> p i k", i=TILES)
     out_v = out.rearrange("b s e -> (b s) e").rearrange("(p i) e -> p i e", i=TILES)
     logits_v = node_logits.rearrange("b s v -> (b s) v").rearrange("(p i) v -> p (i v)", i=TILES)
-    scale_v = x_scale.rearrange("a b k -> (a b k)")
+    scale_v = x_scale.rearrange("a b (g p t) -> p (a b g) t", p=P, t=4)
     b1_v = b1.rearrange("l f -> (l f)").rearrange("(m t) -> m t", t=4)
     w2_v = w2.rearrange("l f e -> (l f) e").rearrange("(p j) e -> p j e", j=4)
 
     with ExitStack() as ctx:
         keep = ctx.enter_context(tc.tile_pool(name="keep", bufs=1))
-        xs_pool = ctx.enter_context(tc.tile_pool(name="xs", bufs=4))
+        xs_pool = ctx.enter_context(tc.tile_pool(name="xs", bufs=3))
         xg_pool = ctx.enter_context(tc.tile_pool(name="xg", bufs=2))
-        xq_pool = ctx.enter_context(tc.tile_pool(name="xq", bufs=2))
-        h_pool = ctx.enter_context(tc.tile_pool(name="h", bufs=2))
+        xq_pool = ctx.enter_context(tc.tile_pool(name="xq", bufs=LAG + 1))
+        h_pool = ctx.enter_context(tc.tile_pool(name="h", bufs=3))
         hq_pool = ctx.enter_context(tc.tile_pool(name="hq", bufs=3))
-        o_pool = ctx.enter_context(tc.tile_pool(name="o", bufs=4))
+        o_pool = ctx.enter_context(tc.tile_pool(name="o", bufs=8))
         xt_psum = ctx.enter_context(tc.psum_pool(name="xt_psum", bufs=2))
         a_psum = ctx.enter_context(tc.psum_pool(name="a_psum", bufs=2))
-        p_psum = ctx.enter_context(tc.psum_pool(name="p_psum", bufs=1))
-        o_psum = ctx.enter_context(tc.psum_pool(name="o_psum", bufs=3))
+        o_psum = ctx.enter_context(tc.psum_pool(name="o_psum", bufs=4))
         ctx.enter_context(tc.manual_schedule())
 
         x8 = {}
 
         def load_x(a, b):
-            t = keep.tile([P, b - a, D], U8, name=f"x8_{a}")
-            nc.sync.dma_start(out=t[:], in_=x_v[:, a:b, :])
+            t = keep.tile([P, (b - a) * D], U8, name=f"x8_{a}")
+            nc.sync.dma_start(out=t[:], in_=x_v[:, a:b, :].rearrange("p i k -> p (i k)"))
             for i in range(a, b):
-                x8[i] = t[:, i - a, :]
+                x8[i] = (t, (i - a) * D)
 
+        scale = keep.tile([P, 2, 4], F32, name="scale")
+        nc.scalar.dma_start(out=scale[:], in_=scale_v)
         logits = keep.tile([P, TILES * NODES], BF16, name="logits")
         nc.scalar.dma_start(out=logits[:], in_=logits_v)
         bias_n = keep.tile([P, NODES], BF16, name="bias_n")
         nc.scalar.dma_start(out=bias_n[:], in_=node_b.partition_broadcast(P))
-        bias_h = keep.tile([P, 4], BF16, name="bias_h")
-        nc.scalar.dma_start(out=bias_h[:], in_=b1_v)
 
-        load_x(0, 1)
-        scale = keep.tile([P, D], F32, name="scale")
-        nc.sync.dma_start(out=scale[:, 0:512], in_=scale_v[0:512].partition_broadcast(P))
-        nc.sync.dma_start(out=scale[:, 512:1024], in_=scale_v[512:1024].partition_broadcast(P))
-        w1_raw = keep.tile([P, 2, LEAVES, P], BF16, name="w1_raw")
+        w1_raw = {}
 
         def load_w1(g):
+            w1_raw[g] = keep.tile([P, LEAVES, P], BF16, name=f"w1_raw{g}")
             nc.sync.dma_start(
-                out=w1_raw[:, g, :, :],
+                out=w1_raw[g][:],
                 in_=w1[:, 512 * g : 512 * (g + 1), :].rearrange("l (p j) f -> p l (j f)", j=4),
             )
 
-        load_w1(0)
+        load_x(0, 1)
         load_x(1, 2)
         load_x(2, 4)
+        load_w1(0)
         load_w1(1)
         load_x(4, 8)
+        bias_h = keep.tile([P, 4], BF16, name="bias_h")
+        nc.sync.dma_start(out=bias_h[:], in_=b1_v)
         w2_raw = keep.tile([P, 4, E], BF16, name="w2_raw")
         nc.sync.dma_start(out=w2_raw[:], in_=w2_v)
-        for a, b in X_CHUNKS[4:]:
-            load_x(a, b)
+        for a in range(8, TILES, 4):
+            load_x(a, a + 4)
 
-        warm = keep.tile([P, 1], F32, name="warm")
-        nc.gpsimd.memset(warm[:], 0.0)
-        nc.scalar.activation(out=warm[:], in_=warm[:], func=ACT.Sigmoid)
         ident = keep.tile([P, P], F32, name="ident")
         make_identity(nc, ident[:])
+        ident16 = keep.tile([P, P], BF16, name="ident16")
+        make_identity(nc, ident16[:])
 
         z = keep.tile([P, TILES, NODES], F32, name="z")
-        nc.gpsimd.tensor_tensor(
-            out=z[:],
-            in0=logits[:].rearrange("p (i v) -> p i v", v=NODES),
-            in1=bias_n[:].unsqueeze(1).to_broadcast([P, TILES, NODES]),
-            op=OP.add,
-        )
         gate = keep.tile([P, 2, TILES, NODES], F32, name="gate")
-        nc.scalar.activation(out=gate[:, 0, :, :], in_=z[:], func=ACT.Sigmoid)
-        nc.scalar.activation(out=gate[:, 1, :, :], in_=z[:], func=ACT.Sigmoid, scale=-1.0)
-        prob = gate[:, :, :, 0].rearrange("p s i -> p i s")
-        for level in range(1, 4):
-            n = 2**level
-            nxt = keep.tile([P, TILES, n, 2], F32, name=f"prob{level}")
+        prep, p_bank, p_sb = {}, {}, {}
+
+        def gates_sum():
             nc.gpsimd.tensor_tensor(
-                out=nxt[:],
-                in0=prob.unsqueeze(3).to_broadcast([P, TILES, n, 2]),
-                in1=gate[:, :, :, n - 1 : 2 * n - 1].rearrange("p s i a -> p i a s"),
-                op=OP.mult,
-            )
-            prob = nxt[:].rearrange("p i a s -> p i (a s)")
-        leaf = prob
-
-        w1_g = keep.tile([P, 2, LF, 4], BF16, name="w1_g", align_bytes=64)
-        w1_c = keep.tile([P, 2, LF], U32, name="w1_c", align_bytes=64)
-        w1_s = keep.tile([P, 2, LF], U8, name="w1_s", align_bytes=64)
-        w2_g = keep.tile([P, E, 4], BF16, name="w2_g", align_bytes=64)
-        w2_c = keep.tile([P, E], U32, name="w2_c", align_bytes=64)
-        w2_s = keep.tile([P, E], U8, name="w2_s", align_bytes=64)
-
-        def w1_interleave(copy, g, t):
-            copy(
-                out=w1_g[:, g, P * t : P * (t + 1), :].rearrange("p (l h) j -> p l h j", h=8),
-                in_=w1_raw[:, g, :, :].rearrange("p l (j h t) -> p l h j t", h=8, t=4)[:, :, :, :, t],
+                out=z[:],
+                in0=logits[:].rearrange("p (i v) -> p i v", v=NODES),
+                in1=bias_n[:].unsqueeze(1).to_broadcast([P, TILES, NODES]),
+                op=OP.add,
             )
 
-        def w1_quantize(g):
-            nc.vector.quantize_mx(
-                out=w1_c[:, g, :].bitcast(FP8X4),
-                scales=w1_s[:, g, :],
-                in_=w1_g[:, g, :, :].rearrange("p n j -> p (n j)"),
-            )
+        def gates_sigmoid():
+            nc.scalar.activation(out=gate[:, 0, :, :], in_=z[:], func=ACT.Sigmoid)
+            nc.scalar.activation(out=gate[:, 1, :, :], in_=z[:], func=ACT.Sigmoid, scale=-1.0)
 
-        def w2_interleave(copy, a, b):
-            copy(
-                out=w2_g[:, a:b, :].rearrange("p (c i) j -> p c j i", i=4),
-                in_=w2_raw[:, :, a:b].rearrange("p j (c i) -> p c j i", i=4),
-            )
-
-        def w2_quantize(a, b):
-            nc.vector.quantize_mx(
-                out=w2_c[:, a:b].bitcast(FP8X4),
-                scales=w2_s[:, a:b],
-                in_=w2_g[:, a:b, :].rearrange("p e j -> p (e j)"),
-            )
-
-        xs, xt, xg, xq, hp, pt, a_bank, h1, hg, hq, o_bank, o_sb, prep = ({} for unused in range(13))
-
-        def widen(i, parts=1):
-            xs[i] = xs_pool.tile([P, D], BF16, name="xs")
-            w = D // parts
-            for c in range(parts):
-                cols = slice(c * w, (c + 1) * w)
-                nc.vector.tensor_tensor(
-                    out=xs[i][:, cols], in0=x8[i][:, cols].bitcast(FP8), in1=scale[:, cols], op=OP.mult
+        def leaf_probabilities():
+            prob = gate[:, :, :, 0].rearrange("p s i -> p i s")
+            for level in range(1, 4):
+                n = 2**level
+                nxt = keep.tile([P, TILES, n, 2], F32, name=f"prob{level}")
+                nc.gpsimd.tensor_tensor(
+                    out=nxt[:],
+                    in0=prob.unsqueeze(3).to_broadcast([P, TILES, n, 2]),
+                    in1=gate[:, :, :, n - 1 : 2 * n - 1].rearrange("p s i a -> p i a s"),
+                    op=OP.mult,
+                )
+                prob = nxt[:].rearrange("p i a s -> p i (a s)")
+            for q in range(QUADS):
+                prep[q] = keep.tile([P, 512], F32, name=f"prep{q}")
+                nc.gpsimd.tensor_scalar(
+                    out=prep[q][:].rearrange("p (c r) -> p c r", r=8),
+                    in0=prob[:, 4 * q : 4 * (q + 1), :]
+                    .rearrange("p i l -> p (i l)")
+                    .unsqueeze(2)
+                    .to_broadcast([P, 64, 8]),
+                    scalar1=1.0,
+                    scalar2=0.0,
+                    op0=OP.mult,
+                    op1=OP.add,
                 )
 
-        def turn_x(i):
-            xt[i] = xt_psum.tile([P, 2, 2, P], F32, name="xt")
-            words = xs[i][:].bitcast(F32)
-            for g in range(2):
+        def turn_p(q):
+            p_bank[q] = o_psum.tile([P, 512], F32, name="ob")
+            for c in range(4):
+                cols = slice(P * c, P * (c + 1))
+                nc.tensor.transpose(p_bank[q][:, cols], prep[q][:, cols], ident[:])
+
+        def leave_p(q):
+            p_sb[q] = keep.tile([P, 512], F32, name=f"p_sb{q}")
+            nc.scalar.copy(out=p_sb[q][:], in_=p_bank[q][:])
+
+        w1_c = keep.tile([P, 2, LF], U32, name="w1_c", align_bytes=64)
+        w1_s = keep.tile([P, 2, LF], U8, name="w1_s", align_bytes=64)
+        w2_c = keep.tile([P, E], U32, name="w2_c", align_bytes=64)
+        w2_s = keep.tile([P, E], U8, name="w2_s", align_bytes=64)
+        w_bank, w_g = {}, {}
+
+        def weave_w(n):
+            w_bank[n] = o_psum.tile([P, 1024], BF16, name="ob")
+            for s in range(2):
+                if n < 4:
+                    t = 2 * (n % 2) + s
+                    src = w1_raw[n // 2][:].rearrange("p l (j h t) -> p l h j t", h=8, t=4)[:, :, :, :, t]
+                else:
+                    e0 = 256 * (n - 4) + P * s
+                    src = w2_raw[:, :, e0 : e0 + P].rearrange("p j e -> p e j")
+                nc.tensor.matmul(
+                    out=w_bank[n][:, 512 * s : 512 * (s + 1)], lhsT=ident16[:], rhs=src, start=True, stop=True
+                )
+
+        def leave_w(n):
+            if n % 2 == 0:
+                w_g[n // 2] = keep.tile([P, 2048], BF16, name=f"w_g{n // 2}", align_bytes=64)
+            nc.scalar.copy(out=w_g[n // 2][:, 1024 * (n % 2) : 1024 * (n % 2 + 1)], in_=w_bank[n][:])
+
+        def quant_w(h):
+            if h < 2:
+                codes, scales = w1_c[:, h, :], w1_s[:, h, :]
+            else:
+                cols = slice(512 * (h - 2), 512 * (h - 1))
+                codes, scales = w2_c[:, cols], w2_s[:, cols]
+            nc.vector.quantize_mx(out=codes.bitcast(FP8X4), scales=scales, in_=w_g[h][:])
+
+        xs, xt, xg, xq, a_bank, hp, hg, hq, o_bank, o_sb = ({} for unused in range(10))
+
+        def widen(k):
+            if k == 0:
+                for j in range(2):
+                    xs[k, j] = keep.tile([P, D], BF16, name=f"xs_first{j}")[:]
+                    t, c = x8[j]
+                    nc.scalar.copy(out=xs[k, j], in_=t[:, c : c + D].bitcast(FP8))
+            else:
+                both = xs_pool.tile([P, 2 * D], BF16, name="xs")
+                t, c = x8[2 * k]
+                nc.scalar.copy(out=both[:], in_=t[:, c : c + 2 * D].bitcast(FP8))
+                for j in range(2):
+                    xs[k, j] = both[:, D * j : D * (j + 1)]
+
+        def turn_x(k, g):
+            xt[k, g] = xt_psum.tile([P, 2, 256], F32, name="xt")
+            for j in range(2):
+                words = xs[k, j].bitcast(F32)
                 for u in range(2):
                     nc.tensor.transpose(
-                        xt[i][:, g, u, :], words[:, 256 * g + u : 256 * (g + 1) : 2], ident[:]
+                        xt[k, g][:, u, P * j : P * (j + 1)], words[:, 256 * g + u : 256 * (g + 1) : 2], ident[:]
                     )
 
-        def leave_x(i):
-            m, j = i // 2, i % 2
-            if j == 0:
-                xg[m] = xg_pool.tile([P, 2, 256, 4], BF16, name="xg", align_bytes=64)
-            words = xg[m][:].rearrange("p g n t -> p g (n t)").bitcast(F32)
-            nc.scalar.copy(
-                out=words[:, :, 256 * j : 256 * (j + 1)].rearrange("p g (n u) -> p g n u", u=2),
-                in_=xt[i][:].rearrange("p g u n -> p g n u"),
+        def scale_x(k, g):
+            if g == 0:
+                xg[k] = xg_pool.tile([P, 2048], BF16, name="xg", align_bytes=64)
+            nc.vector.tensor_tensor(
+                out=xg[k][:, 1024 * g : 1024 * (g + 1)].rearrange("p (n u e) -> p n u e", u=2, e=2),
+                in0=xt[k, g][:].bitcast(BF16).rearrange("p u (n e) -> p n u e", e=2),
+                in1=scale[:, g, :].rearrange("p (u e) -> p u e", e=2).unsqueeze(1).to_broadcast([P, 256, 2, 2]),
+                op=OP.mult,
             )
 
-        def quant_x(m):
-            xq[m] = (
+        def quant_x(k):
+            xq[k] = (
                 xq_pool.tile([P, 512], U32, name="xq_c", align_bytes=64),
                 xq_pool.tile([P, 512], U8, name="xq_s", align_bytes=64),
             )
-            nc.vector.quantize_mx(
-                out=xq[m][0][:].bitcast(FP8X4),
-                scales=xq[m][1][:],
-                in_=xg[m][:].rearrange("p g n t -> p (g n t)"),
-            )
+            nc.vector.quantize_mx(out=xq[k][0][:].bitcast(FP8X4), scales=xq[k][1][:], in_=xg[k][:])
 
-        def mm1(m, half):
-            a_bank[m, half] = a_psum.tile([P, 2, 256], F32, name="a")
+        def mm1(m, half, pool, tag):
+            a_bank[m, half] = pool.tile([P, 2, 256], F32, name=tag)
             for s in range(2):
                 t = 2 * half + s
                 for g in range(2):
@@ -204,43 +231,27 @@ def tile_fastfeedforwardnetwork_pa_t_kernel(tc, x_bytes, x_scale, node_logits, n
                         stop=(g == 1),
                     )
 
-        def leave_h(m, half):
-            if half == 0:
-                h1[m] = h_pool.tile([P, 64, 4, 4], F32, name="h1", align_bytes=64)
-            for s in range(2):
-                t = 2 * half + s
-                nc.scalar.activation(
-                    out=h1[m][:, :, t, :],
-                    in_=a_bank[m, half][:, s, :].rearrange("p (c i) -> p c i", i=4),
-                    func=ACT.Relu,
-                    bias=bias_h[:, t : t + 1],
-                )
-
-        def spread_p(g4):
-            prep[g4] = h_pool.tile([P, 512], F32, name="prep")
-            nc.vector.tensor_copy(
-                out=prep[g4][:].rearrange("p (c r) -> p c r", r=8),
-                in_=leaf[:, 4 * g4 : 4 * (g4 + 1), :]
-                .rearrange("p i l -> p (i l)")
-                .unsqueeze(2)
-                .to_broadcast([P, 64, 8]),
-            )
-
-        def turn_p(m):
-            pt[m] = p_psum.tile([P, 256], F32, name="pt")
-            for j in range(2):
-                c = 2 * (m % 2) + j
-                nc.tensor.transpose(
-                    pt[m][:, P * j : P * (j + 1)], prep[m // 2][:, P * c : P * (c + 1)], ident[:]
-                )
-
         def weigh_h(m):
+            hp[m] = h_pool.tile([P, 4, 256], BF16, name="hp", align_bytes=64)
+            for t in range(4):
+                nc.vector.scalar_tensor_tensor(
+                    out=hp[m][:, t, :],
+                    in0=a_bank[m, t // 2][:, t % 2, :],
+                    scalar=bias_h[:, t : t + 1],
+                    in1=p_sb[m // 2][:, 256 * (m % 2) : 256 * (m % 2 + 1)],
+                    op0=OP.add,
+                    op1=OP.mult,
+                )
+
+        def relu_h(engine, m):
             hg[m] = h_pool.tile([P, 1024], BF16, name="hg", align_bytes=64)
-            nc.vector.tensor_tensor(
-                out=hg[m][:].rearrange("p (c i t) -> p c i t", i=4, t=4),
-                in0=h1[m][:].rearrange("p c t i -> p c i t"),
-                in1=pt[m][:].rearrange("p (c i) -> p c i", i=4).unsqueeze(3).to_broadcast([P, 64, 4, 4]),
-                op=OP.mult,
+            engine.tensor_scalar(
+                out=hg[m][:].rearrange("p (n t) -> p n t", t=4),
+                in0=hp[m][:].rearrange("p t n -> p n t"),
+                scalar1=BF16_MAX,
+                scalar2=0.0,
+                op0=OP.min,
+                op1=OP.max,
             )
 
         def quant_h(m):
@@ -250,11 +261,10 @@ def tile_fastfeedforwardnetwork_pa_t_kernel(tc, x_bytes, x_scale, node_logits, n
             )
             nc.vector.quantize_mx(out=hq[m][0][:].bitcast(FP8X4), scales=hq[m][1][:], in_=hg[m][:])
 
-        def mm2(i, e):
-            m, j = i // 2, i % 2
-            o_bank[i, e] = o_psum.tile([P, 512], F32, name="ob")
+        def mm2(m, j, e, pool, tag):
+            o_bank[m, j, e] = pool.tile([P, 512], F32, name=tag)
             nc.tensor.matmul_mx(
-                out=o_bank[i, e][:],
+                out=o_bank[m, j, e][:],
                 lhsT=hq[m][0][:, P * j : P * (j + 1)].bitcast(FP8X4),
                 lhsT_scale=hq[m][1][:, P * j : P * (j + 1)],
                 rhs=w2_c[:, 512 * e : 512 * (e + 1)].bitcast(FP8X4),
@@ -263,60 +273,91 @@ def tile_fastfeedforwardnetwork_pa_t_kernel(tc, x_bytes, x_scale, node_logits, n
                 stop=True,
             )
 
-        def leave_o(copy, i, e):
+        def leave_o(copy, m, j, e):
+            i = 2 * m + j
             if e == 0:
                 o_sb[i] = o_pool.tile([P, E], F32, name="osb")
-            copy(out=o_sb[i][:, 512 * e : 512 * (e + 1)], in_=o_bank[i, e][:])
+            copy(out=o_sb[i][:, 512 * e : 512 * (e + 1)], in_=o_bank[m, j, e][:])
             if e == 1:
                 nc.sync.dma_start(out=out_v[:, i, :], in_=o_sb[i][:])
 
-        for k in range(TILES + 10):
-            if k < TILES:
-                widen(k, 2 if k == 0 else 1)
-            if k in (2, 3):
-                w1_interleave(nc.vector.tensor_copy, 1, 2 * (k - 2))
-                w1_interleave(nc.vector.tensor_copy, 1, 2 * (k - 2) + 1)
-            if k % 2 == 1:
-                m = (k - 3) // 2
-                if 0 <= m < PAIRS:
-                    quant_x(m)
-                if k == 3:
-                    w1_quantize(0)
-                    w1_quantize(1)
-                if k % 4 == 3 and (k - 3) // 4 < 8:
-                    spread_p((k - 3) // 4)
-                m = (k - 7) // 2
-                if 0 <= m < PAIRS:
-                    quant_h(m)
-                if k == 7:
-                    w2_quantize(0, 512)
-            else:
-                if k == 8:
-                    w2_quantize(512, 1024)
-                m = k // 2 - 3
-                if 0 <= m < PAIRS:
-                    weigh_h(m)
-            if 0 <= k - 8 < TILES:
-                mm2(k - 8, 0)
-                mm2(k - 8, 1)
-            m = (k - 4) // 2
-            if 0 <= m < PAIRS:
-                mm1(m, k % 2)
-            if 0 <= k - 1 < TILES:
-                turn_x(k - 1)
-            if k % 2 == 1 and 0 <= (k - 5) // 2 < PAIRS:
-                turn_p((k - 5) // 2)
-            if k in (1, 2):
-                w1_interleave(nc.scalar.copy, 0, 2 * (k - 1))
-                w1_interleave(nc.scalar.copy, 0, 2 * (k - 1) + 1)
-            if 0 <= k - 8 < TILES:
-                leave_o(nc.scalar.copy, k - 8, 0)
-            if 0 <= m < PAIRS:
-                leave_h(m, k % 2)
-            if 0 <= k - 1 < TILES:
-                leave_x(k - 1)
-            if 4 <= k < 8:
-                w2_interleave(nc.scalar.copy, 256 * (k - 4), 256 * (k - 3))
-            if 0 <= k - 8 < TILES:
-                late = k >= TILES
-                leave_o(nc.vector.tensor_copy if late else nc.scalar.copy, k - 8, 1)
+        def mm2_pair(m, pools):
+            for n in range(4):
+                mm2(m, n // 2, n % 2, *pools[n])
+
+        O4 = [(o_psum, "ob")] * 4
+
+        gates_sum()
+        widen(0)
+        turn_x(0, 0)
+        turn_x(0, 1)
+        widen(1)
+        gates_sigmoid()
+        leaf_probabilities()
+
+        for k in range(PAIRS):
+            m = k - LAG
+            if m >= 1:
+                for n in range(4):
+                    leave_o(nc.scalar.copy, m - 1, n // 2, n % 2)
+            if m >= 0:
+                weigh_h(m)
+                relu_h(nc.gpsimd, m)
+            if k == 0:
+                for n in range(4):
+                    weave_w(n)
+                    leave_w(n)
+            if k + 2 < PAIRS:
+                widen(k + 2)
+            if k == 1:
+                for n in range(4, 8):
+                    weave_w(n)
+                    leave_w(n)
+            if k == LAG - 1:
+                quant_w(0)
+                quant_w(1)
+            if m + 1 >= 0:
+                mm1(m + 1, 0, a_psum, "a")
+                mm1(m + 1, 1, a_psum, "a")
+            for g in range(2):
+                scale_x(k, g)
+                if k + 1 < PAIRS:
+                    turn_x(k + 1, g)
+                else:
+                    mm1(m + 2, g, xt_psum, "xt")
+                q = (m + 2) // 2
+                if g == 0 and (m == -1 or (m >= 0 and m % 2 == 0)) and q < QUADS:
+                    turn_p(q)
+                    leave_p(q)
+            if m == 0:
+                quant_w(2)
+                quant_w(3)
+            if m >= 0:
+                quant_h(m)
+            quant_x(k)
+            if m >= 0:
+                mm2_pair(m, O4)
+
+        last = PAIRS - 1
+        for n in range(4):
+            leave_o(nc.scalar.copy, last - 3, n // 2, n % 2)
+        weigh_h(last - 2)
+        relu_h(nc.gpsimd, last - 2)
+        mm1(last, 0, a_psum, "a")
+        mm1(last, 1, a_psum, "a")
+        weigh_h(last - 1)
+        weigh_h(last)
+        quant_h(last - 2)
+        mm2_pair(last - 2, O4)
+        relu_h(nc.vector, last - 1)
+        relu_h(nc.vector, last)
+        quant_h(last - 1)
+        mm2_pair(last - 1, [(xt_psum, "xt")] * 2 + [(a_psum, "a")] * 2)
+        quant_h(last)
+        for n in range(4):
+            leave_o(nc.scalar.copy, last - 2, n // 2, n % 2)
+        mm2_pair(last, O4)
+        for m in (last - 1, last):
+            for j in range(2):
+                leave_o(nc.vector.tensor_copy, m, j, 0)
+                leave_o(nc.scalar.copy, m, j, 1)

@@ -39,7 +39,7 @@ def tile_fastfeedforwardnetwork_pa_t_kernel(tc, x_bytes, x_scale, node_logits, n
     with ExitStack() as ctx:
         keep = ctx.enter_context(tc.tile_pool(name="keep", bufs=1))
         xs_pool = ctx.enter_context(tc.tile_pool(name="xs", bufs=3))
-        xg_pool = ctx.enter_context(tc.tile_pool(name="xg", bufs=2))
+        xg_pool = ctx.enter_context(tc.tile_pool(name="xg", bufs=1))
         xq_pool = ctx.enter_context(tc.tile_pool(name="xq", bufs=LAG + 1))
         h_pool = ctx.enter_context(tc.tile_pool(name="h", bufs=3))
         hq_pool = ctx.enter_context(tc.tile_pool(name="hq", bufs=3))
@@ -96,7 +96,7 @@ def tile_fastfeedforwardnetwork_pa_t_kernel(tc, x_bytes, x_scale, node_logits, n
         prep, p_bank, p_sb = {}, {}, {}
 
         def gates_sum():
-            nc.gpsimd.tensor_tensor(
+            nc.vector.tensor_tensor(
                 out=z[:],
                 in0=logits[:].rearrange("p (i v) -> p i v", v=NODES),
                 in1=bias_n[:].unsqueeze(1).to_broadcast([P, TILES, NODES]),
@@ -119,19 +119,18 @@ def tile_fastfeedforwardnetwork_pa_t_kernel(tc, x_bytes, x_scale, node_logits, n
                     op=OP.mult,
                 )
                 prob = nxt[:].rearrange("p i a s -> p i (a s)")
-            for q in range(QUADS):
-                prep[q] = keep.tile([P, 512], F32, name=f"prep{q}")
-                nc.gpsimd.tensor_scalar(
-                    out=prep[q][:].rearrange("p (c r) -> p c r", r=8),
-                    in0=prob[:, 4 * q : 4 * (q + 1), :]
-                    .rearrange("p i l -> p (i l)")
-                    .unsqueeze(2)
-                    .to_broadcast([P, 64, 8]),
-                    scalar1=1.0,
-                    scalar2=0.0,
-                    op0=OP.mult,
-                    op1=OP.add,
-                )
+            return prob
+
+        def spread_p(q, pool, tag):
+            prep[q] = pool.tile([P, 512], F32, name=tag, align_bytes=64)
+            nc.gpsimd.tensor_scalar(
+                out=prep[q][:].rearrange("p (c r) -> p c r", r=8),
+                in0=leaf[:, 4 * q : 4 * (q + 1), :].rearrange("p i l -> p (i l)").unsqueeze(2).to_broadcast([P, 64, 8]),
+                scalar1=1.0,
+                scalar2=0.0,
+                op0=OP.mult,
+                op1=OP.add,
+            )
 
         def turn_p(q):
             p_bank[q] = o_psum.tile([P, 512], F32, name="ob")
@@ -177,18 +176,17 @@ def tile_fastfeedforwardnetwork_pa_t_kernel(tc, x_bytes, x_scale, node_logits, n
 
         xs, xt, xg, xq, a_bank, hp, hg, hq, o_bank, o_sb = ({} for unused in range(10))
 
+        def widen_first(j):
+            xs[0, j] = keep.tile([P, D], BF16, name=f"xs_first{j}")[:]
+            t, c = x8[j]
+            nc.vector.tensor_copy(out=xs[0, j], in_=t[:, c : c + D].bitcast(FP8))
+
         def widen(k):
-            if k == 0:
-                for j in range(2):
-                    xs[k, j] = keep.tile([P, D], BF16, name=f"xs_first{j}")[:]
-                    t, c = x8[j]
-                    nc.scalar.copy(out=xs[k, j], in_=t[:, c : c + D].bitcast(FP8))
-            else:
-                both = xs_pool.tile([P, 2 * D], BF16, name="xs")
-                t, c = x8[2 * k]
-                nc.scalar.copy(out=both[:], in_=t[:, c : c + 2 * D].bitcast(FP8))
-                for j in range(2):
-                    xs[k, j] = both[:, D * j : D * (j + 1)]
+            both = xs_pool.tile([P, 2 * D], BF16, name="xs")
+            t, c = x8[2 * k]
+            nc.scalar.copy(out=both[:], in_=t[:, c : c + 2 * D].bitcast(FP8))
+            for j in range(2):
+                xs[k, j] = both[:, D * j : D * (j + 1)]
 
         def turn_x(k, g):
             xt[k, g] = xt_psum.tile([P, 2, 256], F32, name="xt")
@@ -201,7 +199,7 @@ def tile_fastfeedforwardnetwork_pa_t_kernel(tc, x_bytes, x_scale, node_logits, n
 
         def scale_x(k, g):
             if g == 0:
-                xg[k] = xg_pool.tile([P, 2048], BF16, name="xg", align_bytes=64)
+                xg[k] = xg_pool.tile([P, 2048], BF16, name=f"xg{k % 2}", align_bytes=64)
             nc.vector.tensor_tensor(
                 out=xg[k][:, 1024 * g : 1024 * (g + 1)].rearrange("p (n u e) -> p n u e", u=2, e=2),
                 in0=xt[k, g][:].bitcast(BF16).rearrange("p u (n e) -> p n u e", e=2),
@@ -287,56 +285,80 @@ def tile_fastfeedforwardnetwork_pa_t_kernel(tc, x_bytes, x_scale, node_logits, n
 
         O4 = [(o_psum, "ob")] * 4
 
+        widen_first(0)
         gates_sum()
-        widen(0)
+        widen_first(1)
         turn_x(0, 0)
         turn_x(0, 1)
-        widen(1)
         gates_sigmoid()
-        leaf_probabilities()
+        leaf = leaf_probabilities()
+        spread_p(0, keep, "prep0")
+        widen(1)
+        widen(2)
+        scale_x(0, 0)
+        turn_x(1, 0)
+        scale_x(0, 1)
+        weave_w(0)
+        leave_w(0)
+        turn_x(1, 1)
+        weave_w(1)
+        leave_w(1)
+        quant_x(0)
+        scale_x(1, 0)
+        weave_w(2)
+        leave_w(2)
+        turn_x(2, 0)
+        scale_x(1, 1)
+        weave_w(3)
+        leave_w(3)
+        turn_x(2, 1)
+        widen(3)
+        quant_x(1)
+        quant_w(0)
+        scale_x(2, 0)
+        quant_w(1)
+        turn_p(0)
+        leave_p(0)
+        turn_x(3, 0)
+        mm1(0, 0, a_psum, "a")
+        mm1(0, 1, a_psum, "a")
+        scale_x(2, 1)
+        turn_x(3, 1)
+        for n in range(4, 8):
+            weave_w(n)
+            leave_w(n)
+        widen(4)
+        quant_x(2)
 
-        for k in range(PAIRS):
+        for k in range(LAG, PAIRS):
             m = k - LAG
+            q = m // 2 + 1
             if m >= 1:
                 for n in range(4):
                     leave_o(nc.scalar.copy, m - 1, n // 2, n % 2)
-            if m >= 0:
-                weigh_h(m)
-                relu_h(nc.gpsimd, m)
-            if k == 0:
-                for n in range(4):
-                    weave_w(n)
-                    leave_w(n)
+            if m % 2 == 0:
+                spread_p(q, xg_pool, f"xg{(k - 1) % 2}")
+            weigh_h(m)
+            relu_h(nc.gpsimd, m)
             if k + 2 < PAIRS:
                 widen(k + 2)
-            if k == 1:
-                for n in range(4, 8):
-                    weave_w(n)
-                    leave_w(n)
-            if k == LAG - 1:
-                quant_w(0)
-                quant_w(1)
-            if m + 1 >= 0:
-                mm1(m + 1, 0, a_psum, "a")
-                mm1(m + 1, 1, a_psum, "a")
+            mm1(m + 1, 0, a_psum, "a")
+            mm1(m + 1, 1, a_psum, "a")
             for g in range(2):
                 scale_x(k, g)
                 if k + 1 < PAIRS:
                     turn_x(k + 1, g)
                 else:
                     mm1(m + 2, g, xt_psum, "xt")
-                q = (m + 2) // 2
-                if g == 0 and (m == -1 or (m >= 0 and m % 2 == 0)) and q < QUADS:
+                if g == 0 and m % 2 == 0:
                     turn_p(q)
                     leave_p(q)
             if m == 0:
                 quant_w(2)
                 quant_w(3)
-            if m >= 0:
-                quant_h(m)
+            quant_h(m)
             quant_x(k)
-            if m >= 0:
-                mm2_pair(m, O4)
+            mm2_pair(m, O4)
 
         last = PAIRS - 1
         for n in range(4):

@@ -24,7 +24,8 @@ PAIRS = TILES // 2
 QUADS = TILES // 4
 FLOPS = 2 * TOKENS * D * LF + 2 * TOKENS * LF * E
 BF16_MAX = 3.3895313892515355e38
-LAG = 3
+LAG = 2
+AHEAD = 3
 
 
 def tile_fastfeedforwardnetwork_pa_t_kernel(tc, x_bytes, x_scale, node_logits, node_b, w1, b1, w2, out):
@@ -38,9 +39,11 @@ def tile_fastfeedforwardnetwork_pa_t_kernel(tc, x_bytes, x_scale, node_logits, n
 
     with ExitStack() as ctx:
         keep = ctx.enter_context(tc.tile_pool(name="keep", bufs=1))
-        xs_pool = ctx.enter_context(tc.tile_pool(name="xs", bufs=3))
+        xs_pool = ctx.enter_context(tc.tile_pool(name="xs", bufs=6))
+        hg_pool = ctx.enter_context(tc.tile_pool(name="hg", bufs=1))
+        prep_pool = ctx.enter_context(tc.tile_pool(name="prep", bufs=2))
         xg_pool = ctx.enter_context(tc.tile_pool(name="xg", bufs=1))
-        xq_pool = ctx.enter_context(tc.tile_pool(name="xq", bufs=LAG + 1))
+        xq_pool = ctx.enter_context(tc.tile_pool(name="xq", bufs=AHEAD + 1))
         h_pool = ctx.enter_context(tc.tile_pool(name="h", bufs=3))
         hq_pool = ctx.enter_context(tc.tile_pool(name="hq", bufs=3))
         o_pool = ctx.enter_context(tc.tile_pool(name="o", bufs=8))
@@ -77,8 +80,9 @@ def tile_fastfeedforwardnetwork_pa_t_kernel(tc, x_bytes, x_scale, node_logits, n
         load_x(1, 2)
         load_x(2, 4)
         load_w1(0)
+        load_x(4, 6)
         load_w1(1)
-        load_x(4, 8)
+        load_x(6, 8)
         bias_h = keep.tile([P, 4], BF16, name="bias_h")
         nc.sync.dma_start(out=bias_h[:], in_=b1_v)
         w2_raw = keep.tile([P, 4, E], BF16, name="w2_raw")
@@ -121,15 +125,11 @@ def tile_fastfeedforwardnetwork_pa_t_kernel(tc, x_bytes, x_scale, node_logits, n
                 prob = nxt[:].rearrange("p i a s -> p i (a s)")
             return prob
 
-        def spread_p(q, pool, tag):
-            prep[q] = pool.tile([P, 512], F32, name=tag, align_bytes=64)
-            nc.gpsimd.tensor_scalar(
+        def spread_p(q):
+            prep[q] = prep_pool.tile([P, 512], F32, name="prep")
+            nc.scalar.copy(
                 out=prep[q][:].rearrange("p (c r) -> p c r", r=8),
-                in0=leaf[:, 4 * q : 4 * (q + 1), :].rearrange("p i l -> p (i l)").unsqueeze(2).to_broadcast([P, 64, 8]),
-                scalar1=1.0,
-                scalar2=0.0,
-                op0=OP.mult,
-                op1=OP.add,
+                in_=leaf[:, 4 * q : 4 * (q + 1), :].rearrange("p i l -> p (i l)").unsqueeze(2).to_broadcast([P, 64, 8]),
             )
 
         def turn_p(q):
@@ -176,22 +176,20 @@ def tile_fastfeedforwardnetwork_pa_t_kernel(tc, x_bytes, x_scale, node_logits, n
 
         xs, xt, xg, xq, a_bank, hp, hg, hq, o_bank, o_sb = ({} for unused in range(10))
 
-        def widen_first(j):
-            xs[0, j] = keep.tile([P, D], BF16, name=f"xs_first{j}")[:]
-            t, c = x8[j]
-            nc.vector.tensor_copy(out=xs[0, j], in_=t[:, c : c + D].bitcast(FP8))
+        def widen(copy, i):
+            xs[i] = xs_pool.tile([P, D], BF16, name="xs")
+            t, c = x8[i]
+            copy(out=xs[i][:], in_=t[:, c : c + D].bitcast(FP8))
 
-        def widen(k):
-            both = xs_pool.tile([P, 2 * D], BF16, name="xs")
-            t, c = x8[2 * k]
-            nc.scalar.copy(out=both[:], in_=t[:, c : c + 2 * D].bitcast(FP8))
-            for j in range(2):
-                xs[k, j] = both[:, D * j : D * (j + 1)]
+        def widen_in_window(i, pool, tag):
+            xs[i] = pool.tile([P, D], BF16, name=tag, align_bytes=64)
+            t, c = x8[i]
+            nc.gpsimd.tensor_copy(out=xs[i][:], in_=t[:, c : c + D].bitcast(FP8))
 
         def turn_x(k, g):
             xt[k, g] = xt_psum.tile([P, 2, 256], F32, name="xt")
             for j in range(2):
-                words = xs[k, j].bitcast(F32)
+                words = xs[2 * k + j][:].bitcast(F32)
                 for u in range(2):
                     nc.tensor.transpose(
                         xt[k, g][:, u, P * j : P * (j + 1)], words[:, 256 * g + u : 256 * (g + 1) : 2], ident[:]
@@ -229,9 +227,10 @@ def tile_fastfeedforwardnetwork_pa_t_kernel(tc, x_bytes, x_scale, node_logits, n
                         stop=(g == 1),
                     )
 
-        def weigh_h(m):
-            hp[m] = h_pool.tile([P, 4, 256], BF16, name="hp", align_bytes=64)
-            for t in range(4):
+        def weigh_h(m, planes=range(4)):
+            if 0 in planes:
+                hp[m] = h_pool.tile([P, 4, 256], BF16, name="hp", align_bytes=64)
+            for t in planes:
                 nc.vector.scalar_tensor_tensor(
                     out=hp[m][:, t, :],
                     in0=a_bank[m, t // 2][:, t % 2, :],
@@ -242,7 +241,7 @@ def tile_fastfeedforwardnetwork_pa_t_kernel(tc, x_bytes, x_scale, node_logits, n
                 )
 
         def relu_h(engine, m):
-            hg[m] = h_pool.tile([P, 1024], BF16, name="hg", align_bytes=64)
+            hg[m] = hg_pool.tile([P, 1024], BF16, name=f"hg{m % 4}", align_bytes=64)
             engine.tensor_scalar(
                 out=hg[m][:].rearrange("p (n t) -> p n t", t=4),
                 in0=hp[m][:].rearrange("p t n -> p n t"),
@@ -276,7 +275,10 @@ def tile_fastfeedforwardnetwork_pa_t_kernel(tc, x_bytes, x_scale, node_logits, n
             if e == 0:
                 o_sb[i] = o_pool.tile([P, E], F32, name="osb")
             copy(out=o_sb[i][:, 512 * e : 512 * (e + 1)], in_=o_bank[m, j, e][:])
-            if e == 1:
+            if m >= PAIRS - 2:
+                cols = slice(512 * e, 512 * (e + 1))
+                nc.sync.dma_start(out=out_v[:, i, cols], in_=o_sb[i][:, cols])
+            elif e == 1:
                 nc.sync.dma_start(out=out_v[:, i, :], in_=o_sb[i][:])
 
         def mm2_pair(m, pools):
@@ -285,101 +287,113 @@ def tile_fastfeedforwardnetwork_pa_t_kernel(tc, x_bytes, x_scale, node_logits, n
 
         O4 = [(o_psum, "ob")] * 4
 
-        widen_first(0)
+        widen(nc.vector.tensor_copy, 0)
         gates_sum()
-        widen_first(1)
+        widen(nc.vector.tensor_copy, 1)
         turn_x(0, 0)
         turn_x(0, 1)
         gates_sigmoid()
+        widen(nc.gpsimd.tensor_copy, 3)
         leaf = leaf_probabilities()
-        spread_p(0, keep, "prep0")
-        widen(1)
-        widen(2)
+        widen(nc.scalar.copy, 2)
+        widen(nc.scalar.copy, 4)
+        widen(nc.scalar.copy, 5)
         scale_x(0, 0)
         turn_x(1, 0)
         scale_x(0, 1)
-        weave_w(0)
-        leave_w(0)
         turn_x(1, 1)
-        weave_w(1)
-        leave_w(1)
-        quant_x(0)
         scale_x(1, 0)
-        weave_w(2)
-        leave_w(2)
-        turn_x(2, 0)
-        scale_x(1, 1)
-        weave_w(3)
-        leave_w(3)
-        turn_x(2, 1)
-        widen(3)
-        quant_x(1)
-        quant_w(0)
-        scale_x(2, 0)
-        quant_w(1)
-        turn_p(0)
-        leave_p(0)
-        turn_x(3, 0)
-        mm1(0, 0, a_psum, "a")
-        mm1(0, 1, a_psum, "a")
-        scale_x(2, 1)
-        turn_x(3, 1)
-        for n in range(4, 8):
+        for n in range(2):
             weave_w(n)
             leave_w(n)
-        widen(4)
+        turn_x(2, 0)
+        scale_x(1, 1)
+        for n in range(2, 4):
+            weave_w(n)
+            leave_w(n)
+        turn_x(2, 1)
+        quant_x(0)
+        quant_x(1)
+        widen_in_window(6, xg_pool, "xg1")
+        scale_x(2, 0)
+        quant_w(0)
+        quant_w(1)
+        spread_p(0)
+        for n in range(4, 6):
+            weave_w(n)
+            leave_w(n)
+        weave_w(6)
+        turn_p(0)
+        leave_p(0)
+        mm1(0, 0, a_psum, "a")
+        mm1(0, 1, a_psum, "a")
+        leave_w(6)
+        weave_w(7)
+        leave_w(7)
+        scale_x(2, 1)
+        widen(nc.scalar.copy, 7)
         quant_x(2)
+        weigh_h(0)
+        mm1(1, 0, a_psum, "a")
+        mm1(1, 1, a_psum, "a")
+        turn_x(3, 0)
+        turn_x(3, 1)
+        spread_p(1)
+        turn_p(1)
+        widen(nc.scalar.copy, 8)
+        leave_p(1)
+        quant_w(2)
+        relu_h(nc.vector, 0)
+        quant_w(3)
+        quant_h(0)
+        mm2_pair(0, O4)
 
-        for k in range(LAG, PAIRS):
+        for k in range(AHEAD, PAIRS):
             m = k - LAG
-            q = m // 2 + 1
-            if m >= 1:
-                for n in range(4):
-                    leave_o(nc.scalar.copy, m - 1, n // 2, n % 2)
-            if m % 2 == 0:
-                spread_p(q, xg_pool, f"xg{(k - 1) % 2}")
+            q = (m + 3) // 2
+            for n in range(4):
+                leave_o(nc.scalar.copy, m - 1, n // 2, n % 2)
+            if k + 1 < PAIRS:
+                widen_in_window(2 * k + 3, hg_pool, f"hg{(m - 1) % 4}")
             weigh_h(m)
             relu_h(nc.gpsimd, m)
-            if k + 2 < PAIRS:
-                widen(k + 2)
             mm1(m + 1, 0, a_psum, "a")
             mm1(m + 1, 1, a_psum, "a")
             for g in range(2):
                 scale_x(k, g)
                 if k + 1 < PAIRS:
                     turn_x(k + 1, g)
-                else:
-                    mm1(m + 2, g, xt_psum, "xt")
-                if g == 0 and m % 2 == 0:
+                if g == 0 and m % 2 == 0 and q < QUADS:
                     turn_p(q)
-                    leave_p(q)
-            if m == 0:
-                quant_w(2)
-                quant_w(3)
+            if k + 2 < PAIRS:
+                widen(nc.scalar.copy, 2 * k + 4)
+            if m % 2 == 0 and q < QUADS:
+                leave_p(q)
+            if m % 2 == 1 and q < QUADS:
+                spread_p(q)
             quant_h(m)
             quant_x(k)
             mm2_pair(m, O4)
 
         last = PAIRS - 1
-        for n in range(4):
-            leave_o(nc.scalar.copy, last - 3, n // 2, n % 2)
-        weigh_h(last - 2)
-        relu_h(nc.gpsimd, last - 2)
-        mm1(last, 0, a_psum, "a")
-        mm1(last, 1, a_psum, "a")
-        weigh_h(last - 1)
-        weigh_h(last)
-        quant_h(last - 2)
-        mm2_pair(last - 2, O4)
-        relu_h(nc.vector, last - 1)
-        relu_h(nc.vector, last)
-        quant_h(last - 1)
-        mm2_pair(last - 1, [(xt_psum, "xt")] * 2 + [(a_psum, "a")] * 2)
-        quant_h(last)
+        mm1(last, 0, xt_psum, "xt")
+        mm1(last, 1, xt_psum, "xt")
         for n in range(4):
             leave_o(nc.scalar.copy, last - 2, n // 2, n % 2)
-        mm2_pair(last, O4)
-        for m in (last - 1, last):
-            for j in range(2):
-                leave_o(nc.vector.tensor_copy, m, j, 0)
-                leave_o(nc.scalar.copy, m, j, 1)
+        weigh_h(last - 1)
+        weigh_h(last, [0])
+        relu_h(nc.vector, last - 1)
+        weigh_h(last, [1])
+        quant_h(last - 1)
+        mm2_pair(last - 1, O4)
+        weigh_h(last, [2, 3])
+        leave_o(nc.vector.tensor_copy, last - 1, 0, 0)
+        relu_h(nc.vector, last)
+        leave_o(nc.scalar.copy, last - 1, 0, 1)
+        leave_o(nc.vector.tensor_copy, last - 1, 1, 0)
+        quant_h(last)
+        leave_o(nc.scalar.copy, last - 1, 1, 1)
+        mm2_pair(last, [(a_psum, "a")] * 2 + [(xt_psum, "xt")] * 2)
+        for j in range(2):
+            leave_o(nc.vector.tensor_copy, last, j, 0)
+            leave_o(nc.scalar.copy, last, j, 1)

@@ -142,6 +142,27 @@ def tile_fastfeedforwardnetwork_pa_t_kernel(tc, x_bytes, x_scale, node_logits, n
             p_sb[q] = keep.tile([P, 512], F32, name=f"p_sb{q}")
             nc.scalar.copy(out=p_sb[q][:], in_=p_bank[q][:])
 
+        p_far = keep.tile([P, 8, 3 * P], F32, name="p_far")
+
+        def park_p():
+            bank = o_psum.tile([P, 3 * P], F32, name="ob")
+            for c in range(3):
+                rows = leaf[:, 8 * (c + 1) : 8 * (c + 2), :].rearrange("p i l -> p (i l)")
+                nc.tensor.transpose(bank[:, P * c : P * (c + 1)], rows, ident[:])
+            turned = keep.tile([P, 3 * P], F32, name="turned")
+            nc.scalar.copy(out=turned[:], in_=bank[:])
+            parked = out_v[:, TILES - 1, 0 : 3 * P]
+            nc.sync.dma_start(out=parked, in_=turned[:])
+            for r in range(8):
+                start = 4 * (r % 2) + r // 2
+                nc.sync.dma_start(out=p_far[start:P:8, :, :], in_=parked.rearrange("(i l) n -> l i n", l=LEAVES))
+
+        def p_of(m):
+            if m < 4:
+                return p_sb[m // 2][:, 256 * (m % 2) : 256 * (m % 2 + 1)].rearrange("p (j n) -> p j n", j=2)
+            c, i = m // 4 - 1, 2 * (m % 4)
+            return p_far[:, i : i + 2, P * c : P * (c + 1)]
+
         w1_c = keep.tile([P, 2, LF], U32, name="w1_c", align_bytes=64)
         w1_s = keep.tile([P, 2, LF], U8, name="w1_s", align_bytes=64)
         w2_c = keep.tile([P, E], U32, name="w2_c", align_bytes=64)
@@ -176,23 +197,21 @@ def tile_fastfeedforwardnetwork_pa_t_kernel(tc, x_bytes, x_scale, node_logits, n
 
         xs, xt, xg, xq, a_bank, hp, hg, hq, o_bank, o_sb = ({} for unused in range(10))
 
-        def widen(copy, i):
-            xs[i] = xs_pool.tile([P, D], BF16, name="xs")
-            t, c = x8[i]
-            copy(out=xs[i][:], in_=t[:, c : c + D].bitcast(FP8))
-
-        def widen_in_window(i, pool, tag):
-            xs[i] = pool.tile([P, D], BF16, name=tag, align_bytes=64)
-            t, c = x8[i]
-            nc.gpsimd.tensor_copy(out=xs[i][:], in_=t[:, c : c + D].bitcast(FP8))
+        def widen(copy, first, count, pool=xs_pool, tag="xs"):
+            wide = pool.tile([P, 512 * count], BF16, name=tag, align_bytes=64)
+            t, c = x8[first // 2]
+            c += 512 * (first % 2)
+            copy(out=wide[:], in_=t[:, c : c + 512 * count].bitcast(FP8))
+            for n in range(count):
+                xs[first + n] = wide[:, 512 * n : 512 * (n + 1)]
 
         def turn_x(k, g):
             xt[k, g] = xt_psum.tile([P, 2, 256], F32, name="xt")
             for j in range(2):
-                words = xs[2 * k + j][:].bitcast(F32)
+                words = xs[4 * k + 2 * j + g].bitcast(F32)
                 for u in range(2):
                     nc.tensor.transpose(
-                        xt[k, g][:, u, P * j : P * (j + 1)], words[:, 256 * g + u : 256 * (g + 1) : 2], ident[:]
+                        xt[k, g][:, u, P * j : P * (j + 1)], words[:, u:256:2], ident[:]
                     )
 
         def scale_x(k, g):
@@ -232,10 +251,10 @@ def tile_fastfeedforwardnetwork_pa_t_kernel(tc, x_bytes, x_scale, node_logits, n
                 hp[m] = h_pool.tile([P, 4, 256], BF16, name="hp", align_bytes=64)
             for t in planes:
                 nc.vector.scalar_tensor_tensor(
-                    out=hp[m][:, t, :],
-                    in0=a_bank[m, t // 2][:, t % 2, :],
+                    out=hp[m][:, t, :].rearrange("p (j n) -> p j n", j=2),
+                    in0=a_bank[m, t // 2][:, t % 2, :].rearrange("p (j n) -> p j n", j=2),
                     scalar=bias_h[:, t : t + 1],
-                    in1=p_sb[m // 2][:, 256 * (m % 2) : 256 * (m % 2 + 1)],
+                    in1=p_of(m),
                     op0=OP.add,
                     op1=OP.mult,
                 )
@@ -287,17 +306,17 @@ def tile_fastfeedforwardnetwork_pa_t_kernel(tc, x_bytes, x_scale, node_logits, n
 
         O4 = [(o_psum, "ob")] * 4
 
-        widen(nc.vector.tensor_copy, 0)
+        widen(nc.vector.tensor_copy, 0, 2)
         gates_sum()
-        widen(nc.vector.tensor_copy, 1)
+        widen(nc.vector.tensor_copy, 2, 2)
         turn_x(0, 0)
         turn_x(0, 1)
         gates_sigmoid()
-        widen(nc.gpsimd.tensor_copy, 3)
+        widen(nc.gpsimd.tensor_copy, 6, 2)
         leaf = leaf_probabilities()
-        widen(nc.scalar.copy, 2)
-        widen(nc.scalar.copy, 4)
-        widen(nc.scalar.copy, 5)
+        widen(nc.scalar.copy, 4, 2)
+        widen(nc.scalar.copy, 8, 2)
+        widen(nc.scalar.copy, 10, 2)
         scale_x(0, 0)
         turn_x(1, 0)
         scale_x(0, 1)
@@ -314,11 +333,12 @@ def tile_fastfeedforwardnetwork_pa_t_kernel(tc, x_bytes, x_scale, node_logits, n
         turn_x(2, 1)
         quant_x(0)
         quant_x(1)
-        widen_in_window(6, xg_pool, "xg1")
+        widen(nc.gpsimd.tensor_copy, 12, 2, xg_pool, "xg1")
         scale_x(2, 0)
         quant_w(0)
         quant_w(1)
         spread_p(0)
+        park_p()
         for n in range(4, 6):
             weave_w(n)
             leave_w(n)
@@ -331,7 +351,7 @@ def tile_fastfeedforwardnetwork_pa_t_kernel(tc, x_bytes, x_scale, node_logits, n
         weave_w(7)
         leave_w(7)
         scale_x(2, 1)
-        widen(nc.scalar.copy, 7)
+        widen(nc.scalar.copy, 14, 2)
         quant_x(2)
         weigh_h(0)
         mm1(1, 0, a_psum, "a")
@@ -340,60 +360,60 @@ def tile_fastfeedforwardnetwork_pa_t_kernel(tc, x_bytes, x_scale, node_logits, n
         turn_x(3, 1)
         spread_p(1)
         turn_p(1)
-        widen(nc.scalar.copy, 8)
         leave_p(1)
+        widen(nc.scalar.copy, 17, 3)
         quant_w(2)
         relu_h(nc.vector, 0)
         quant_w(3)
         quant_h(0)
         mm2_pair(0, O4)
 
-        for k in range(AHEAD, PAIRS):
+        for k in range(AHEAD, PAIRS - 1):
             m = k - LAG
-            q = (m + 3) // 2
             for n in range(4):
                 leave_o(nc.scalar.copy, m - 1, n // 2, n % 2)
-            if k + 1 < PAIRS:
-                widen_in_window(2 * k + 3, hg_pool, f"hg{(m - 1) % 4}")
+            widen(nc.gpsimd.tensor_copy, 4 * (k + 1), 1, hg_pool, f"hg{(m - 1) % 4}")
             weigh_h(m)
             relu_h(nc.gpsimd, m)
             mm1(m + 1, 0, a_psum, "a")
             mm1(m + 1, 1, a_psum, "a")
             for g in range(2):
                 scale_x(k, g)
-                if k + 1 < PAIRS:
-                    turn_x(k + 1, g)
-                if g == 0 and m % 2 == 0 and q < QUADS:
-                    turn_p(q)
+                turn_x(k + 1, g)
             if k + 2 < PAIRS:
-                widen(nc.scalar.copy, 2 * k + 4)
-            if m % 2 == 0 and q < QUADS:
-                leave_p(q)
-            if m % 2 == 1 and q < QUADS:
-                spread_p(q)
+                widen(nc.scalar.copy, 4 * (k + 2) + 1, 3)
             quant_h(m)
             quant_x(k)
             mm2_pair(m, O4)
 
         last = PAIRS - 1
-        mm1(last, 0, xt_psum, "xt")
-        mm1(last, 1, xt_psum, "xt")
         for n in range(4):
-            leave_o(nc.scalar.copy, last - 2, n // 2, n % 2)
+            leave_o(nc.scalar.copy, last - 3, n // 2, n % 2)
+        weigh_h(last - 2)
+        relu_h(nc.gpsimd, last - 2)
+        mm1(last - 1, 0, a_psum, "a")
+        mm1(last - 1, 1, a_psum, "a")
+        scale_x(last, 0)
         weigh_h(last - 1)
-        weigh_h(last, [0])
-        relu_h(nc.vector, last - 1)
-        weigh_h(last, [1])
+        quant_h(last - 2)
+        relu_h(nc.gpsimd, last - 1)
+        mm2_pair(last - 2, O4)
+        scale_x(last, 1)
+        leave_o(nc.vector.tensor_copy, last - 2, 0, 0)
+        for n in range(1, 4):
+            leave_o(nc.scalar.copy, last - 2, n // 2, n % 2)
+        quant_x(last)
+        mm1(last, 0, a_psum, "a")
+        mm1(last, 1, a_psum, "a")
         quant_h(last - 1)
-        mm2_pair(last - 1, O4)
-        weigh_h(last, [2, 3])
-        leave_o(nc.vector.tensor_copy, last - 1, 0, 0)
+        mm2_pair(last - 1, [(xt_psum, "xt")] * 2 + [(o_psum, "ob")] * 2)
+        weigh_h(last)
+        for n in range(3):
+            leave_o(nc.scalar.copy, last - 1, n // 2, n % 2)
         relu_h(nc.vector, last)
-        leave_o(nc.scalar.copy, last - 1, 0, 1)
-        leave_o(nc.vector.tensor_copy, last - 1, 1, 0)
+        leave_o(nc.vector.tensor_copy, last - 1, 1, 1)
         quant_h(last)
-        leave_o(nc.scalar.copy, last - 1, 1, 1)
-        mm2_pair(last, [(a_psum, "a")] * 2 + [(xt_psum, "xt")] * 2)
+        mm2_pair(last, [(o_psum, "ob")] * 2 + [(a_psum, "a")] * 2)
         for j in range(2):
             leave_o(nc.vector.tensor_copy, last, j, 0)
             leave_o(nc.scalar.copy, last, j, 1)

@@ -28,6 +28,10 @@ LAG = 2
 AHEAD = 3
 
 
+def shared(m):
+    return m % 3 == 0 and 0 < m < PAIRS - 3
+
+
 def tile_fastfeedforwardnetwork_pa_t_kernel(tc, x_bytes, x_scale, node_logits, node_b, w1, b1, w2, out):
     nc = tc.nc
     x_v = x_bytes.rearrange("b s k -> (b s) k").rearrange("(p i) k -> p i k", i=TILES)
@@ -40,6 +44,7 @@ def tile_fastfeedforwardnetwork_pa_t_kernel(tc, x_bytes, x_scale, node_logits, n
     with ExitStack() as ctx:
         keep = ctx.enter_context(tc.tile_pool(name="keep", bufs=1))
         xs_pool = ctx.enter_context(tc.tile_pool(name="xs", bufs=6))
+        h1_pool = ctx.enter_context(tc.tile_pool(name="h1", bufs=1))
         hg_pool = ctx.enter_context(tc.tile_pool(name="hg", bufs=1))
         prep_pool = ctx.enter_context(tc.tile_pool(name="prep", bufs=2))
         xg_pool = ctx.enter_context(tc.tile_pool(name="xg", bufs=1))
@@ -195,7 +200,7 @@ def tile_fastfeedforwardnetwork_pa_t_kernel(tc, x_bytes, x_scale, node_logits, n
                 codes, scales = w2_c[:, cols], w2_s[:, cols]
             nc.vector.quantize_mx(out=codes.bitcast(FP8X4), scales=scales, in_=w_g[h][:])
 
-        xs, xt, xg, xq, a_bank, hp, hg, hq, o_bank, o_sb = ({} for unused in range(10))
+        xs, xt, xg, xq, a_bank, hp, h1, hg, hg_tag, hq, o_bank, o_sb = ({} for unused in range(12))
 
         def widen(copy, first, count, pool=xs_pool, tag="xs"):
             wide = pool.tile([P, 512 * count], BF16, name=tag, align_bytes=64)
@@ -260,7 +265,8 @@ def tile_fastfeedforwardnetwork_pa_t_kernel(tc, x_bytes, x_scale, node_logits, n
                 )
 
         def relu_h(engine, m):
-            hg[m] = hg_pool.tile([P, 1024], BF16, name=f"hg{m % 4}", align_bytes=64)
+            hg_tag[m] = f"hg{m % 4}"
+            hg[m] = hg_pool.tile([P, 1024], BF16, name=hg_tag[m], align_bytes=64)
             engine.tensor_scalar(
                 out=hg[m][:].rearrange("p (n t) -> p n t", t=4),
                 in0=hp[m][:].rearrange("p t n -> p n t"),
@@ -268,6 +274,26 @@ def tile_fastfeedforwardnetwork_pa_t_kernel(tc, x_bytes, x_scale, node_logits, n
                 scalar2=0.0,
                 op0=OP.min,
                 op1=OP.max,
+            )
+
+        def leave_h(m):
+            h1[m] = h1_pool.tile([P, 4, 256], F32, name="h1")
+            for t in range(4):
+                nc.scalar.activation(
+                    out=h1[m][:, t, :],
+                    in_=a_bank[m, t // 2][:, t % 2, :],
+                    func=ACT.Relu,
+                    bias=bias_h[:, t : t + 1],
+                )
+
+        def weigh_on_gpsimd(m):
+            hg[m] = hg_pool.tile([P, 1024], BF16, name=hg_tag[m - 1], align_bytes=64)
+            hg_tag[m] = hg_tag[m - 1]
+            nc.gpsimd.tensor_tensor(
+                out=hg[m][:].rearrange("p (j n t) -> p j n t", j=2, t=4),
+                in0=h1[m][:].rearrange("p t (j n) -> p j n t", j=2),
+                in1=p_of(m).unsqueeze(3).to_broadcast([P, 2, P, 4]),
+                op=OP.mult,
             )
 
         def quant_h(m):
@@ -361,7 +387,7 @@ def tile_fastfeedforwardnetwork_pa_t_kernel(tc, x_bytes, x_scale, node_logits, n
         spread_p(1)
         turn_p(1)
         leave_p(1)
-        widen(nc.scalar.copy, 17, 3)
+        widen(nc.scalar.copy, 18, 2)
         quant_w(2)
         relu_h(nc.vector, 0)
         quant_w(3)
@@ -370,18 +396,27 @@ def tile_fastfeedforwardnetwork_pa_t_kernel(tc, x_bytes, x_scale, node_logits, n
 
         for k in range(AHEAD, PAIRS - 1):
             m = k - LAG
-            for n in range(4):
-                leave_o(nc.scalar.copy, m - 1, n // 2, n % 2)
-            widen(nc.gpsimd.tensor_copy, 4 * (k + 1), 1, hg_pool, f"hg{(m - 1) % 4}")
-            weigh_h(m)
-            relu_h(nc.gpsimd, m)
+            for e in range(2):
+                leave_o(nc.scalar.copy, m - 1, 0, e)
+            if shared(m):
+                weigh_on_gpsimd(m)
+            else:
+                widen(nc.gpsimd.tensor_copy, 4 * (k + 1), 2, hg_pool, hg_tag[m - 1])
+                weigh_h(m)
+                relu_h(nc.gpsimd, m)
             mm1(m + 1, 0, a_psum, "a")
             mm1(m + 1, 1, a_psum, "a")
+            if shared(m + 1):
+                leave_h(m + 1)
+            for e in range(2):
+                leave_o(nc.scalar.copy, m - 1, 1, e)
             for g in range(2):
                 scale_x(k, g)
                 turn_x(k + 1, g)
             if k + 2 < PAIRS:
-                widen(nc.scalar.copy, 4 * (k + 2) + 1, 3)
+                widen(nc.scalar.copy, 4 * (k + 2) + 2, 2)
+            if shared(m + 2):
+                widen(nc.scalar.copy, 4 * (k + 3), 2)
             quant_h(m)
             quant_x(k)
             mm2_pair(m, O4)

@@ -29,7 +29,7 @@ AHEAD = 3
 
 
 def shared(m):
-    return m % 3 == 0 and 0 < m < PAIRS - 3
+    return m % 4 == 3 and 0 < m < PAIRS - 4
 
 
 def tile_fastfeedforwardnetwork_pa_t_kernel(tc, x_bytes, x_scale, node_logits, node_b, w1, b1, w2, out):
@@ -65,12 +65,12 @@ def tile_fastfeedforwardnetwork_pa_t_kernel(tc, x_bytes, x_scale, node_logits, n
             for i in range(a, b):
                 x8[i] = (t, (i - a) * D)
 
+        bias_n = keep.tile([P, NODES], BF16, name="bias_n")
+        nc.scalar.dma_start(out=bias_n[:], in_=node_b.partition_broadcast(P))
         scale = keep.tile([P, 2, 4], F32, name="scale")
         nc.scalar.dma_start(out=scale[:], in_=scale_v)
         logits = keep.tile([P, TILES * NODES], BF16, name="logits")
-        nc.scalar.dma_start(out=logits[:], in_=logits_v)
-        bias_n = keep.tile([P, NODES], BF16, name="bias_n")
-        nc.scalar.dma_start(out=bias_n[:], in_=node_b.partition_broadcast(P))
+        nc.sync.dma_start(out=logits[:], in_=logits_v)
 
         w1_raw = {}
 
@@ -81,11 +81,12 @@ def tile_fastfeedforwardnetwork_pa_t_kernel(tc, x_bytes, x_scale, node_logits, n
                 in_=w1[:, 512 * g : 512 * (g + 1), :].rearrange("l (p j) f -> p l (j f)", j=4),
             )
 
-        load_x(0, 1)
-        load_x(1, 2)
+        x8_first = keep.tile([P, 2, 2, 512], U8, name="x8_first")
+        for g in range(2):
+            nc.sync.dma_start(out=x8_first[:, g, :, :], in_=x_v[:, 0:2, 512 * g : 512 * (g + 1)])
         load_x(2, 4)
-        load_w1(0)
         load_x(4, 6)
+        load_w1(0)
         load_w1(1)
         load_x(6, 8)
         bias_h = keep.tile([P, 4], BF16, name="bias_h")
@@ -221,7 +222,7 @@ def tile_fastfeedforwardnetwork_pa_t_kernel(tc, x_bytes, x_scale, node_logits, n
 
         def scale_x(k, g):
             if g == 0:
-                xg[k] = xg_pool.tile([P, 2048], BF16, name=f"xg{k % 2}", align_bytes=64)
+                xg[k] = xg_pool.tile([P, 2048], BF16, name=f"xg{k % 3}", align_bytes=64)
             nc.vector.tensor_tensor(
                 out=xg[k][:, 1024 * g : 1024 * (g + 1)].rearrange("p (n u e) -> p n u e", u=2, e=2),
                 in0=xt[k, g][:].bitcast(BF16).rearrange("p u (n e) -> p n u e", e=2),
@@ -265,7 +266,7 @@ def tile_fastfeedforwardnetwork_pa_t_kernel(tc, x_bytes, x_scale, node_logits, n
                 )
 
         def relu_h(engine, m):
-            hg_tag[m] = f"hg{m % 4}"
+            hg_tag[m] = hg_tag[m - 1] if shared(m - 1) else f"hg{m % 4}"
             hg[m] = hg_pool.tile([P, 1024], BF16, name=hg_tag[m], align_bytes=64)
             engine.tensor_scalar(
                 out=hg[m][:].rearrange("p (n t) -> p n t", t=4),
@@ -332,13 +333,15 @@ def tile_fastfeedforwardnetwork_pa_t_kernel(tc, x_bytes, x_scale, node_logits, n
 
         O4 = [(o_psum, "ob")] * 4
 
-        widen(nc.vector.tensor_copy, 0, 2)
         gates_sum()
-        widen(nc.vector.tensor_copy, 2, 2)
-        turn_x(0, 0)
-        turn_x(0, 1)
+        for g in range(2):
+            wide = keep.tile([P, 1024], BF16, name=f"xs_first{g}", align_bytes=64)
+            nc.vector.tensor_copy(out=wide[:], in_=x8_first[:, g, :, :].rearrange("p j k -> p (j k)").bitcast(FP8))
+            for j in range(2):
+                xs[2 * j + g] = wide[:, 512 * j : 512 * (j + 1)]
+            turn_x(0, g)
         gates_sigmoid()
-        widen(nc.gpsimd.tensor_copy, 6, 2)
+        widen(nc.gpsimd.tensor_copy, 6, 2, keep, "xs_first0")
         leaf = leaf_probabilities()
         widen(nc.scalar.copy, 4, 2)
         widen(nc.scalar.copy, 8, 2)
@@ -348,19 +351,19 @@ def tile_fastfeedforwardnetwork_pa_t_kernel(tc, x_bytes, x_scale, node_logits, n
         scale_x(0, 1)
         turn_x(1, 1)
         scale_x(1, 0)
-        for n in range(2):
-            weave_w(n)
-            leave_w(n)
+        weave_w(0)
+        leave_w(0)
         turn_x(2, 0)
+        weave_w(1)
+        leave_w(1)
         scale_x(1, 1)
         for n in range(2, 4):
             weave_w(n)
             leave_w(n)
         turn_x(2, 1)
+        scale_x(2, 0)
         quant_x(0)
         quant_x(1)
-        widen(nc.gpsimd.tensor_copy, 12, 2, xg_pool, "xg1")
-        scale_x(2, 0)
         quant_w(0)
         quant_w(1)
         spread_p(0)
@@ -379,6 +382,7 @@ def tile_fastfeedforwardnetwork_pa_t_kernel(tc, x_bytes, x_scale, node_logits, n
         scale_x(2, 1)
         widen(nc.scalar.copy, 14, 2)
         quant_x(2)
+        widen(nc.gpsimd.tensor_copy, 12, 2, xg_pool, "xg2")
         weigh_h(0)
         mm1(1, 0, a_psum, "a")
         mm1(1, 1, a_psum, "a")
@@ -400,6 +404,8 @@ def tile_fastfeedforwardnetwork_pa_t_kernel(tc, x_bytes, x_scale, node_logits, n
                 leave_o(nc.scalar.copy, m - 1, 0, e)
             if shared(m):
                 weigh_on_gpsimd(m)
+            elif shared(m - 1):
+                relu_h(nc.gpsimd, m)
             else:
                 widen(nc.gpsimd.tensor_copy, 4 * (k + 1), 2, hg_pool, hg_tag[m - 1])
                 weigh_h(m)
@@ -413,7 +419,10 @@ def tile_fastfeedforwardnetwork_pa_t_kernel(tc, x_bytes, x_scale, node_logits, n
             for g in range(2):
                 scale_x(k, g)
                 turn_x(k + 1, g)
-            if k + 2 < PAIRS:
+            if shared(m):
+                weigh_h(m + 1)
+                widen(nc.scalar.copy, 4 * (k + 2), 4)
+            elif k + 2 < PAIRS:
                 widen(nc.scalar.copy, 4 * (k + 2) + 2, 2)
             if shared(m + 2):
                 widen(nc.scalar.copy, 4 * (k + 3), 2)
@@ -441,14 +450,16 @@ def tile_fastfeedforwardnetwork_pa_t_kernel(tc, x_bytes, x_scale, node_logits, n
         mm1(last, 0, a_psum, "a")
         mm1(last, 1, a_psum, "a")
         quant_h(last - 1)
-        mm2_pair(last - 1, [(xt_psum, "xt")] * 2 + [(o_psum, "ob")] * 2)
+        for e in range(2):
+            mm2(last - 1, 0, e, xt_psum, "xt")
+            leave_o(nc.scalar.copy, last - 1, 0, e)
         weigh_h(last)
-        for n in range(3):
-            leave_o(nc.scalar.copy, last - 1, n // 2, n % 2)
+        for e in range(2):
+            mm2(last - 1, 1, e, a_psum, "a")
+            leave_o(nc.scalar.copy, last - 1, 1, e)
         relu_h(nc.vector, last)
-        leave_o(nc.vector.tensor_copy, last - 1, 1, 1)
         quant_h(last)
-        mm2_pair(last, [(o_psum, "ob")] * 2 + [(a_psum, "a")] * 2)
+        mm2_pair(last, O4)
         for j in range(2):
             leave_o(nc.vector.tensor_copy, last, j, 0)
             leave_o(nc.scalar.copy, last, j, 1)

@@ -29,7 +29,7 @@ AHEAD = 3
 
 
 def shared(m):
-    return m % 4 == 3 and 0 < m < PAIRS - 4
+    return m in (3, 7, 11, 13)
 
 
 def tile_fastfeedforwardnetwork_pa_t_kernel(tc, x_bytes, x_scale, node_logits, node_b, w1, b1, w2, out):
@@ -43,7 +43,7 @@ def tile_fastfeedforwardnetwork_pa_t_kernel(tc, x_bytes, x_scale, node_logits, n
 
     with ExitStack() as ctx:
         keep = ctx.enter_context(tc.tile_pool(name="keep", bufs=1))
-        xs_pool = ctx.enter_context(tc.tile_pool(name="xs", bufs=6))
+        xs_pool = ctx.enter_context(tc.tile_pool(name="xs", bufs=7))
         h1_pool = ctx.enter_context(tc.tile_pool(name="h1", bufs=1))
         hg_pool = ctx.enter_context(tc.tile_pool(name="hg", bufs=1))
         prep_pool = ctx.enter_context(tc.tile_pool(name="prep", bufs=2))
@@ -85,10 +85,9 @@ def tile_fastfeedforwardnetwork_pa_t_kernel(tc, x_bytes, x_scale, node_logits, n
         for g in range(2):
             nc.sync.dma_start(out=x8_first[:, g, :, :], in_=x_v[:, 0:2, 512 * g : 512 * (g + 1)])
         load_x(2, 4)
-        load_x(4, 6)
+        load_x(4, 8)
         load_w1(0)
         load_w1(1)
-        load_x(6, 8)
         bias_h = keep.tile([P, 4], BF16, name="bias_h")
         nc.sync.dma_start(out=bias_h[:], in_=b1_v)
         w2_raw = keep.tile([P, 4, E], BF16, name="w2_raw")
@@ -321,7 +320,7 @@ def tile_fastfeedforwardnetwork_pa_t_kernel(tc, x_bytes, x_scale, node_logits, n
             if e == 0:
                 o_sb[i] = o_pool.tile([P, E], F32, name="osb")
             copy(out=o_sb[i][:, 512 * e : 512 * (e + 1)], in_=o_bank[m, j, e][:])
-            if m >= PAIRS - 2:
+            if m >= PAIRS - 3:
                 cols = slice(512 * e, 512 * (e + 1))
                 nc.sync.dma_start(out=out_v[:, i, cols], in_=o_sb[i][:, cols])
             elif e == 1:
@@ -330,6 +329,10 @@ def tile_fastfeedforwardnetwork_pa_t_kernel(tc, x_bytes, x_scale, node_logits, n
         def mm2_pair(m, pools):
             for n in range(4):
                 mm2(m, n // 2, n % 2, *pools[n])
+
+        def mm2_tile(m, j):
+            for e in range(2):
+                mm2(m, j, e, o_psum, "ob")
 
         O4 = [(o_psum, "ob")] * 4
 
@@ -346,6 +349,7 @@ def tile_fastfeedforwardnetwork_pa_t_kernel(tc, x_bytes, x_scale, node_logits, n
         widen(nc.scalar.copy, 4, 2)
         widen(nc.scalar.copy, 8, 2)
         widen(nc.scalar.copy, 10, 2)
+        widen(nc.scalar.copy, 14, 2)
         scale_x(0, 0)
         turn_x(1, 0)
         scale_x(0, 1)
@@ -378,9 +382,9 @@ def tile_fastfeedforwardnetwork_pa_t_kernel(tc, x_bytes, x_scale, node_logits, n
         mm1(0, 1, a_psum, "a")
         leave_w(6)
         weave_w(7)
+        widen(nc.scalar.copy, 18, 2)
         leave_w(7)
         scale_x(2, 1)
-        widen(nc.scalar.copy, 14, 2)
         quant_x(2)
         widen(nc.gpsimd.tensor_copy, 12, 2, xg_pool, "xg2")
         weigh_h(0)
@@ -390,13 +394,13 @@ def tile_fastfeedforwardnetwork_pa_t_kernel(tc, x_bytes, x_scale, node_logits, n
         turn_x(3, 1)
         spread_p(1)
         turn_p(1)
+        widen(nc.scalar.copy, 22, 2)
         leave_p(1)
-        widen(nc.scalar.copy, 18, 2)
         quant_w(2)
         relu_h(nc.vector, 0)
         quant_w(3)
         quant_h(0)
-        mm2_pair(0, O4)
+        mm2_tile(0, 0)
 
         for k in range(AHEAD, PAIRS - 1):
             m = k - LAG
@@ -414,46 +418,55 @@ def tile_fastfeedforwardnetwork_pa_t_kernel(tc, x_bytes, x_scale, node_logits, n
             mm1(m + 1, 1, a_psum, "a")
             if shared(m + 1):
                 leave_h(m + 1)
-            for e in range(2):
-                leave_o(nc.scalar.copy, m - 1, 1, e)
+            if shared(m) and k + 2 < PAIRS:
+                widen(nc.scalar.copy, 4 * (k + 2), 2)
+            if shared(m + 2) and k + 3 < PAIRS:
+                widen(nc.scalar.copy, 4 * (k + 3), 4)
+            elif k + 3 < PAIRS:
+                widen(nc.scalar.copy, 4 * (k + 3) + 2, 2)
             for g in range(2):
                 scale_x(k, g)
                 turn_x(k + 1, g)
+                if g == 0:
+                    mm2_tile(m - 1, 1)
+                    for e in range(2):
+                        leave_o(nc.scalar.copy, m - 1, 1, e)
             if shared(m):
                 weigh_h(m + 1)
-                widen(nc.scalar.copy, 4 * (k + 2), 4)
-            elif k + 2 < PAIRS:
-                widen(nc.scalar.copy, 4 * (k + 2) + 2, 2)
-            if shared(m + 2):
-                widen(nc.scalar.copy, 4 * (k + 3), 2)
             quant_h(m)
             quant_x(k)
-            mm2_pair(m, O4)
+            mm2_tile(m, 0)
 
         last = PAIRS - 1
-        for n in range(4):
-            leave_o(nc.scalar.copy, last - 3, n // 2, n % 2)
-        weigh_h(last - 2)
-        relu_h(nc.gpsimd, last - 2)
+        weigh_on_gpsimd(last - 2)
         mm1(last - 1, 0, a_psum, "a")
         mm1(last - 1, 1, a_psum, "a")
+        for e in range(2):
+            mm2(last - 3, 1, e, o_psum, "ob")
+        for n in range(4):
+            leave_o(nc.scalar.copy, last - 3, n // 2, n % 2)
         scale_x(last, 0)
+        scale_x(last, 1)
         weigh_h(last - 1)
         quant_h(last - 2)
-        relu_h(nc.gpsimd, last - 1)
-        mm2_pair(last - 2, O4)
-        scale_x(last, 1)
-        leave_o(nc.vector.tensor_copy, last - 2, 0, 0)
-        for n in range(1, 4):
-            leave_o(nc.scalar.copy, last - 2, n // 2, n % 2)
         quant_x(last)
+        relu_h(nc.gpsimd, last - 1)
+        for e in range(2):
+            mm2(last - 2, 0, e, o_psum, "ob")
         mm1(last, 0, a_psum, "a")
+        for e in range(2):
+            mm2(last - 2, 1, e, o_psum, "ob")
         mm1(last, 1, a_psum, "a")
+        leave_o(nc.scalar.copy, last - 2, 0, 0)
+        leave_o(nc.vector.tensor_copy, last - 2, 0, 1)
+        for e in range(2):
+            leave_o(nc.scalar.copy, last - 2, 1, e)
+        weigh_h(last, [0, 1])
         quant_h(last - 1)
         for e in range(2):
             mm2(last - 1, 0, e, xt_psum, "xt")
             leave_o(nc.scalar.copy, last - 1, 0, e)
-        weigh_h(last)
+        weigh_h(last, [2, 3])
         for e in range(2):
             mm2(last - 1, 1, e, a_psum, "a")
             leave_o(nc.scalar.copy, last - 1, 1, e)

@@ -211,21 +211,21 @@ def tile_fastfeedforwardnetwork_pa_t_kernel(tc, x_bytes, x_scale, node_logits, n
                 xs[first + n] = wide[:, 512 * n : 512 * (n + 1)]
 
         def turn_x(k, g):
-            xt[k, g] = xt_psum.tile([P, 2, 256], F32, name="xt")
+            xt[k, g] = xt_psum.tile([P, 256, 2], F32, name="xt")
             for j in range(2):
                 words = xs[4 * k + 2 * j + g].bitcast(F32)
                 for u in range(2):
                     nc.tensor.transpose(
-                        xt[k, g][:, u, P * j : P * (j + 1)], words[:, u:256:2], ident[:]
+                        xt[k, g][:, P * j : P * (j + 1), u], words[:, u:256:2], ident[:]
                     )
 
         def scale_x(k, g):
             if g == 0:
                 xg[k] = xg_pool.tile([P, 2048], BF16, name=f"xg{k % 3}", align_bytes=64)
             nc.vector.tensor_tensor(
-                out=xg[k][:, 1024 * g : 1024 * (g + 1)].rearrange("p (n u e) -> p n u e", u=2, e=2),
-                in0=xt[k, g][:].bitcast(BF16).rearrange("p u (n e) -> p n u e", e=2),
-                in1=scale[:, g, :].rearrange("p (u e) -> p u e", e=2).unsqueeze(1).to_broadcast([P, 256, 2, 2]),
+                out=xg[k][:, 1024 * g : 1024 * (g + 1)].rearrange("p (a b) -> p a b", b=64),
+                in0=xt[k, g][:].rearrange("p n u -> p (n u)").bitcast(BF16).rearrange("p (a b) -> p a b", b=64),
+                in1=scale_row[:, g, :].unsqueeze(1).to_broadcast([P, 16, 64]),
                 op=OP.mult,
             )
 
@@ -336,6 +336,11 @@ def tile_fastfeedforwardnetwork_pa_t_kernel(tc, x_bytes, x_scale, node_logits, n
 
         O4 = [(o_psum, "ob")] * 4
 
+        scale_row = keep.tile([P, 2, 64], F32, name="scale_row")
+        nc.vector.tensor_copy(
+            out=scale_row[:].rearrange("p g (n t) -> p g n t", t=4),
+            in_=scale[:].unsqueeze(2).to_broadcast([P, 2, 16, 4]),
+        )
         gates_sum()
         for g in range(2):
             wide = keep.tile([P, 1024], BF16, name=f"xs_first{g}", align_bytes=64)

@@ -21,7 +21,6 @@ LEAVES = 16
 NODES = 15
 TILES = TOKENS // P
 PAIRS = TILES // 2
-QUADS = TILES // 4
 FLOPS = 2 * TOKENS * D * LF + 2 * TOKENS * LF * E
 BF16_MAX = 3.3895313892515355e38
 LAG = 2
@@ -29,7 +28,7 @@ AHEAD = 3
 
 
 def shared(m):
-    return m in (3, 7, 11, 13)
+    return (m % 4 == 3 and 0 < m < PAIRS - 1) or m == PAIRS - 3
 
 
 def tile_fastfeedforwardnetwork_pa_t_kernel(tc, x_bytes, x_scale, node_logits, node_b, w1, b1, w2, out):
@@ -211,21 +210,24 @@ def tile_fastfeedforwardnetwork_pa_t_kernel(tc, x_bytes, x_scale, node_logits, n
                 xs[first + n] = wide[:, 512 * n : 512 * (n + 1)]
 
         def turn_x(k, g):
-            xt[k, g] = xt_psum.tile([P, 256, 2], F32, name="xt")
+            xt[k, g] = xt_psum.tile([P, 512], F32, name="xt")
+            places = xt[k, g][:].rearrange("p (u n) -> p u n" if g == 0 else "p (n u) -> p u n", u=2)
             for j in range(2):
                 words = xs[4 * k + 2 * j + g].bitcast(F32)
                 for u in range(2):
-                    nc.tensor.transpose(
-                        xt[k, g][:, P * j : P * (j + 1), u], words[:, u:256:2], ident[:]
-                    )
+                    nc.tensor.transpose(places[:, u, P * j : P * (j + 1)], words[:, u:256:2], ident[:])
 
         def scale_x(k, g):
             if g == 0:
                 xg[k] = xg_pool.tile([P, 2048], BF16, name=f"xg{k % 3}", align_bytes=64)
+            order = "p (u a n e) -> p a n u e" if g == 0 else "p (a n u e) -> p a n u e"
             nc.vector.tensor_tensor(
-                out=xg[k][:, 1024 * g : 1024 * (g + 1)].rearrange("p (a b) -> p a b", b=64),
-                in0=xt[k, g][:].rearrange("p n u -> p (n u)").bitcast(BF16).rearrange("p (a b) -> p a b", b=64),
-                in1=scale_row[:, g, :].unsqueeze(1).to_broadcast([P, 16, 64]),
+                out=xg[k][:, 1024 * g : 1024 * (g + 1)].rearrange("p (a n u e) -> p a n u e", n=16, u=2, e=2),
+                in0=xt[k, g][:].bitcast(BF16).rearrange(order, n=16, u=2, e=2),
+                in1=scale_row[:, g, :]
+                .rearrange("p (n u e) -> p n u e", u=2, e=2)
+                .unsqueeze(1)
+                .to_broadcast([P, 16, 16, 2, 2]),
                 op=OP.mult,
             )
 
@@ -236,8 +238,8 @@ def tile_fastfeedforwardnetwork_pa_t_kernel(tc, x_bytes, x_scale, node_logits, n
             )
             nc.vector.quantize_mx(out=xq[k][0][:].bitcast(FP8X4), scales=xq[k][1][:], in_=xg[k][:])
 
-        def mm1(m, half, pool, tag):
-            a_bank[m, half] = pool.tile([P, 2, 256], F32, name=tag)
+        def mm1(m, half):
+            a_bank[m, half] = a_psum.tile([P, 2, 256], F32, name="a")
             for s in range(2):
                 t = 2 * half + s
                 for g in range(2):
@@ -326,15 +328,9 @@ def tile_fastfeedforwardnetwork_pa_t_kernel(tc, x_bytes, x_scale, node_logits, n
             elif e == 1:
                 nc.sync.dma_start(out=out_v[:, i, :], in_=o_sb[i][:])
 
-        def mm2_pair(m, pools):
-            for n in range(4):
-                mm2(m, n // 2, n % 2, *pools[n])
-
         def mm2_tile(m, j):
             for e in range(2):
                 mm2(m, j, e, o_psum, "ob")
-
-        O4 = [(o_psum, "ob")] * 4
 
         scale_row = keep.tile([P, 2, 64], F32, name="scale_row")
         nc.vector.tensor_copy(
@@ -383,8 +379,8 @@ def tile_fastfeedforwardnetwork_pa_t_kernel(tc, x_bytes, x_scale, node_logits, n
         weave_w(6)
         turn_p(0)
         leave_p(0)
-        mm1(0, 0, a_psum, "a")
-        mm1(0, 1, a_psum, "a")
+        mm1(0, 0)
+        mm1(0, 1)
         leave_w(6)
         weave_w(7)
         widen(nc.scalar.copy, 18, 2)
@@ -393,8 +389,8 @@ def tile_fastfeedforwardnetwork_pa_t_kernel(tc, x_bytes, x_scale, node_logits, n
         quant_x(2)
         widen(nc.gpsimd.tensor_copy, 12, 2, xg_pool, "xg2")
         weigh_h(0)
-        mm1(1, 0, a_psum, "a")
-        mm1(1, 1, a_psum, "a")
+        mm1(1, 0)
+        mm1(1, 1)
         turn_x(3, 0)
         turn_x(3, 1)
         spread_p(1)
@@ -419,8 +415,8 @@ def tile_fastfeedforwardnetwork_pa_t_kernel(tc, x_bytes, x_scale, node_logits, n
                 widen(nc.gpsimd.tensor_copy, 4 * (k + 1), 2, hg_pool, hg_tag[m - 1])
                 weigh_h(m)
                 relu_h(nc.gpsimd, m)
-            mm1(m + 1, 0, a_psum, "a")
-            mm1(m + 1, 1, a_psum, "a")
+            mm1(m + 1, 0)
+            mm1(m + 1, 1)
             if shared(m + 1):
                 leave_h(m + 1)
             if shared(m) and k + 2 < PAIRS:
@@ -444,10 +440,9 @@ def tile_fastfeedforwardnetwork_pa_t_kernel(tc, x_bytes, x_scale, node_logits, n
 
         last = PAIRS - 1
         weigh_on_gpsimd(last - 2)
-        mm1(last - 1, 0, a_psum, "a")
-        mm1(last - 1, 1, a_psum, "a")
-        for e in range(2):
-            mm2(last - 3, 1, e, o_psum, "ob")
+        mm1(last - 1, 0)
+        mm1(last - 1, 1)
+        mm2_tile(last - 3, 1)
         for n in range(4):
             leave_o(nc.scalar.copy, last - 3, n // 2, n % 2)
         scale_x(last, 0)
@@ -456,12 +451,10 @@ def tile_fastfeedforwardnetwork_pa_t_kernel(tc, x_bytes, x_scale, node_logits, n
         quant_h(last - 2)
         quant_x(last)
         relu_h(nc.gpsimd, last - 1)
-        for e in range(2):
-            mm2(last - 2, 0, e, o_psum, "ob")
-        mm1(last, 0, a_psum, "a")
-        for e in range(2):
-            mm2(last - 2, 1, e, o_psum, "ob")
-        mm1(last, 1, a_psum, "a")
+        mm2_tile(last - 2, 0)
+        mm1(last, 0)
+        mm2_tile(last - 2, 1)
+        mm1(last, 1)
         leave_o(nc.scalar.copy, last - 2, 0, 0)
         leave_o(nc.vector.tensor_copy, last - 2, 0, 1)
         for e in range(2):
@@ -477,7 +470,8 @@ def tile_fastfeedforwardnetwork_pa_t_kernel(tc, x_bytes, x_scale, node_logits, n
             leave_o(nc.scalar.copy, last - 1, 1, e)
         relu_h(nc.vector, last)
         quant_h(last)
-        mm2_pair(last, O4)
+        mm2_tile(last, 0)
+        mm2_tile(last, 1)
         for j in range(2):
             leave_o(nc.vector.tensor_copy, last, j, 0)
             leave_o(nc.scalar.copy, last, j, 1)

@@ -23,12 +23,8 @@ TILES = TOKENS // P
 PAIRS = TILES // 2
 FLOPS = 2 * TOKENS * D * LF + 2 * TOKENS * LF * E
 BF16_MAX = 3.3895313892515355e38
-LAG = 2
-AHEAD = 3
-
-
-def shared(m):
-    return (m % 4 == 3 and 0 < m < PAIRS - 1) or m == PAIRS - 3
+GROUPS = [(2 * k, 2) for k in range(PAIRS - 1)] + [(TILES - 2, 1), (TILES - 1, 1)]
+SHARED = ()
 
 
 def tile_fastfeedforwardnetwork_pa_t_kernel(tc, x_bytes, x_scale, node_logits, node_b, w1, b1, w2, out):
@@ -44,10 +40,10 @@ def tile_fastfeedforwardnetwork_pa_t_kernel(tc, x_bytes, x_scale, node_logits, n
         keep = ctx.enter_context(tc.tile_pool(name="keep", bufs=1))
         xs_pool = ctx.enter_context(tc.tile_pool(name="xs", bufs=7))
         h1_pool = ctx.enter_context(tc.tile_pool(name="h1", bufs=1))
-        hg_pool = ctx.enter_context(tc.tile_pool(name="hg", bufs=1))
+        hg_pool = ctx.enter_context(tc.tile_pool(name="hg", bufs=2))
         prep_pool = ctx.enter_context(tc.tile_pool(name="prep", bufs=2))
         xg_pool = ctx.enter_context(tc.tile_pool(name="xg", bufs=1))
-        xq_pool = ctx.enter_context(tc.tile_pool(name="xq", bufs=AHEAD + 1))
+        xq_pool = ctx.enter_context(tc.tile_pool(name="xq", bufs=4))
         h_pool = ctx.enter_context(tc.tile_pool(name="h", bufs=3))
         hq_pool = ctx.enter_context(tc.tile_pool(name="hq", bufs=3))
         o_pool = ctx.enter_context(tc.tile_pool(name="o", bufs=8))
@@ -80,13 +76,12 @@ def tile_fastfeedforwardnetwork_pa_t_kernel(tc, x_bytes, x_scale, node_logits, n
                 in_=w1[:, 512 * g : 512 * (g + 1), :].rearrange("l (p j) f -> p l (j f)", j=4),
             )
 
-        x8_first = keep.tile([P, 2, 2, 512], U8, name="x8_first")
-        for g in range(2):
-            nc.sync.dma_start(out=x8_first[:, g, :, :], in_=x_v[:, 0:2, 512 * g : 512 * (g + 1)])
+        load_x(0, 2)
         load_x(2, 4)
-        load_x(4, 8)
         load_w1(0)
+        load_x(4, 6)
         load_w1(1)
+        load_x(6, 8)
         bias_h = keep.tile([P, 4], BF16, name="bias_h")
         nc.sync.dma_start(out=bias_h[:], in_=b1_v)
         w2_raw = keep.tile([P, 4, E], BF16, name="w2_raw")
@@ -162,10 +157,12 @@ def tile_fastfeedforwardnetwork_pa_t_kernel(tc, x_bytes, x_scale, node_logits, n
                 nc.sync.dma_start(out=p_far[start:P:8, :, :], in_=parked.rearrange("(i l) n -> l i n", l=LEAVES))
 
         def p_of(m):
-            if m < 4:
-                return p_sb[m // 2][:, 256 * (m % 2) : 256 * (m % 2 + 1)].rearrange("p (j n) -> p j n", j=2)
-            c, i = m // 4 - 1, 2 * (m % 4)
-            return p_far[:, i : i + 2, P * c : P * (c + 1)]
+            first, n = GROUPS[m]
+            if first < 8:
+                near = p_sb[first // 4][:].rearrange("p (j n) -> p j n", j=4)
+                return near[:, first % 4 : first % 4 + n, :]
+            c, i = first // 8 - 1, first % 8
+            return p_far[:, i : i + n, P * c : P * (c + 1)]
 
         w1_c = keep.tile([P, 2, LF], U32, name="w1_c", align_bytes=64)
         w1_s = keep.tile([P, 2, LF], U8, name="w1_s", align_bytes=64)
@@ -199,76 +196,77 @@ def tile_fastfeedforwardnetwork_pa_t_kernel(tc, x_bytes, x_scale, node_logits, n
                 codes, scales = w2_c[:, cols], w2_s[:, cols]
             nc.vector.quantize_mx(out=codes.bitcast(FP8X4), scales=scales, in_=w_g[h][:])
 
-        xs, xt, xg, xq, a_bank, hp, h1, hg, hg_tag, hq, o_bank, o_sb = ({} for unused in range(12))
+        xs, xt, xg, xq, a_bank, hp, h1, hg, hq, o_bank, o_sb = ({} for unused in range(11))
 
-        def widen(copy, first, count, pool=xs_pool, tag="xs"):
-            wide = pool.tile([P, 512 * count], BF16, name=tag, align_bytes=64)
-            t, c = x8[first // 2]
-            c += 512 * (first % 2)
-            copy(out=wide[:], in_=t[:, c : c + 512 * count].bitcast(FP8))
-            for n in range(count):
-                xs[first + n] = wide[:, 512 * n : 512 * (n + 1)]
+        def widen(copy, i, pool=xs_pool, tag="xs"):
+            xs[i] = pool.tile([P, D], BF16, name=tag, align_bytes=64)
+            t, c = x8[i]
+            copy(out=xs[i][:], in_=t[:, c : c + D].bitcast(FP8))
 
-        def turn_x(k, g):
-            xt[k, g] = xt_psum.tile([P, 512], F32, name="xt")
-            places = xt[k, g][:].rearrange("p (u n) -> p u n" if g == 0 else "p (n u) -> p u n", u=2)
-            for j in range(2):
-                words = xs[4 * k + 2 * j + g].bitcast(F32)
+        def turn_x(i, pool=xt_psum, tag="xt"):
+            xt[i] = pool.tile([P, 2, 2, P], F32, name=tag)
+            words = xs[i][:].bitcast(F32)
+            for g in range(2):
                 for u in range(2):
-                    nc.tensor.transpose(places[:, u, P * j : P * (j + 1)], words[:, u:256:2], ident[:])
+                    nc.tensor.transpose(xt[i][:, u, g, :], words[:, 256 * g + u : 256 * (g + 1) : 2], ident[:])
 
-        def scale_x(k, g):
-            if g == 0:
-                xg[k] = xg_pool.tile([P, 2048], BF16, name=f"xg{k % 3}", align_bytes=64)
-            order = "p (u a n e) -> p a n u e" if g == 0 else "p (a n u e) -> p a n u e"
+        def scale_x(m, j):
+            first, n = GROUPS[m]
+            if j == 0:
+                xg[m] = xg_pool.tile([P, 2, n, 512], BF16, name=f"xg{m % 3}", align_bytes=64)
             nc.vector.tensor_tensor(
-                out=xg[k][:, 1024 * g : 1024 * (g + 1)].rearrange("p (a n u e) -> p a n u e", n=16, u=2, e=2),
-                in0=xt[k, g][:].bitcast(BF16).rearrange(order, n=16, u=2, e=2),
-                in1=scale_row[:, g, :]
-                .rearrange("p (n u e) -> p n u e", u=2, e=2)
-                .unsqueeze(1)
-                .to_broadcast([P, 16, 16, 2, 2]),
+                out=xg[m][:, :, j, :].rearrange("p g (a n u e) -> p g a n u e", n=16, u=2, e=2),
+                in0=xt[first + j][:].bitcast(BF16).rearrange("p u g (a n e) -> p g a n u e", n=16, e=2),
+                in1=scale_row[:]
+                .rearrange("p g (n u e) -> p g n u e", u=2, e=2)
+                .unsqueeze(2)
+                .to_broadcast([P, 2, 8, 16, 2, 2]),
                 op=OP.mult,
             )
 
-        def quant_x(k):
-            xq[k] = (
-                xq_pool.tile([P, 512], U32, name="xq_c", align_bytes=64),
-                xq_pool.tile([P, 512], U8, name="xq_s", align_bytes=64),
+        def quant_x(m):
+            n = GROUPS[m][1]
+            xq[m] = (
+                xq_pool.tile([P, 256 * n], U32, name="xq_c", align_bytes=64),
+                xq_pool.tile([P, 256 * n], U8, name="xq_s", align_bytes=64),
             )
-            nc.vector.quantize_mx(out=xq[k][0][:].bitcast(FP8X4), scales=xq[k][1][:], in_=xg[k][:])
+            nc.vector.quantize_mx(
+                out=xq[m][0][:].bitcast(FP8X4), scales=xq[m][1][:], in_=xg[m][:].rearrange("p g j c -> p (g j c)")
+            )
 
-        def mm1(m, half):
-            a_bank[m, half] = a_psum.tile([P, 2, 256], F32, name="a")
-            for s in range(2):
-                t = 2 * half + s
+        def mm1(m, pool=a_psum, tag="a"):
+            n = GROUPS[m][1]
+            width = P * n
+            for t in range(4):
+                if t * width % 512 == 0:
+                    bank = pool.tile([P, 512], F32, name=tag)
+                a_bank[m, t] = bank[:, t * width % 512 : t * width % 512 + width]
                 for g in range(2):
                     nc.tensor.matmul_mx(
-                        out=a_bank[m, half][:, s, :],
+                        out=a_bank[m, t],
                         lhsT=w1_c[:, g, P * t : P * (t + 1)].bitcast(FP8X4),
                         lhsT_scale=w1_s[:, g, P * t : P * (t + 1)],
-                        rhs=xq[m][0][:, 256 * g : 256 * (g + 1)].bitcast(FP8X4),
-                        rhs_scale=xq[m][1][:, 256 * g : 256 * (g + 1)],
+                        rhs=xq[m][0][:, width * g : width * (g + 1)].bitcast(FP8X4),
+                        rhs_scale=xq[m][1][:, width * g : width * (g + 1)],
                         start=(g == 0),
                         stop=(g == 1),
                     )
 
-        def weigh_h(m, planes=range(4)):
-            if 0 in planes:
-                hp[m] = h_pool.tile([P, 4, 256], BF16, name="hp", align_bytes=64)
-            for t in planes:
+        def weigh_h(m):
+            n = GROUPS[m][1]
+            hp[m] = h_pool.tile([P, 4, P * n], BF16, name="hp", align_bytes=64)
+            for t in range(4):
                 nc.vector.scalar_tensor_tensor(
-                    out=hp[m][:, t, :].rearrange("p (j n) -> p j n", j=2),
-                    in0=a_bank[m, t // 2][:, t % 2, :].rearrange("p (j n) -> p j n", j=2),
+                    out=hp[m][:, t, :].rearrange("p (j n) -> p j n", j=n),
+                    in0=a_bank[m, t].rearrange("p (j n) -> p j n", j=n),
                     scalar=bias_h[:, t : t + 1],
                     in1=p_of(m),
                     op0=OP.add,
                     op1=OP.mult,
                 )
 
-        def relu_h(engine, m):
-            hg_tag[m] = hg_tag[m - 1] if shared(m - 1) else f"hg{m % 4}"
-            hg[m] = hg_pool.tile([P, 1024], BF16, name=hg_tag[m], align_bytes=64)
+        def relu_h(engine, m, pool=hg_pool, tag="hg"):
+            hg[m] = pool.tile([P, 512 * GROUPS[m][1]], BF16, name=tag, align_bytes=64)
             engine.tensor_scalar(
                 out=hg[m][:].rearrange("p (n t) -> p n t", t=4),
                 in0=hp[m][:].rearrange("p t n -> p n t"),
@@ -279,199 +277,197 @@ def tile_fastfeedforwardnetwork_pa_t_kernel(tc, x_bytes, x_scale, node_logits, n
             )
 
         def leave_h(m):
-            h1[m] = h1_pool.tile([P, 4, 256], F32, name="h1")
+            h1[m] = h1_pool.tile([P, 4, P * GROUPS[m][1]], F32, name="h1")
             for t in range(4):
-                nc.scalar.activation(
-                    out=h1[m][:, t, :],
-                    in_=a_bank[m, t // 2][:, t % 2, :],
-                    func=ACT.Relu,
-                    bias=bias_h[:, t : t + 1],
-                )
+                nc.scalar.activation(out=h1[m][:, t, :], in_=a_bank[m, t], func=ACT.Relu, bias=bias_h[:, t : t + 1])
 
-        def weigh_on_gpsimd(m):
-            hg[m] = hg_pool.tile([P, 1024], BF16, name=hg_tag[m - 1], align_bytes=64)
-            hg_tag[m] = hg_tag[m - 1]
+        def weigh_on_gpsimd(m, pool, tag):
+            n = GROUPS[m][1]
+            hg[m] = pool.tile([P, 512 * n], BF16, name=tag, align_bytes=64)
             nc.gpsimd.tensor_tensor(
-                out=hg[m][:].rearrange("p (j n t) -> p j n t", j=2, t=4),
-                in0=h1[m][:].rearrange("p t (j n) -> p j n t", j=2),
-                in1=p_of(m).unsqueeze(3).to_broadcast([P, 2, P, 4]),
+                out=hg[m][:].rearrange("p (j n t) -> p j n t", j=n, t=4),
+                in0=h1[m][:].rearrange("p t (j n) -> p j n t", j=n),
+                in1=p_of(m).unsqueeze(3).to_broadcast([P, n, P, 4]),
                 op=OP.mult,
             )
 
         def quant_h(m):
+            n = GROUPS[m][1]
             hq[m] = (
-                hq_pool.tile([P, 256], U32, name="hq_c", align_bytes=64),
-                hq_pool.tile([P, 256], U8, name="hq_s", align_bytes=64),
+                hq_pool.tile([P, P * n], U32, name="hq_c", align_bytes=64),
+                hq_pool.tile([P, P * n], U8, name="hq_s", align_bytes=64),
             )
             nc.vector.quantize_mx(out=hq[m][0][:].bitcast(FP8X4), scales=hq[m][1][:], in_=hg[m][:])
 
-        def mm2(m, j, e, pool, tag):
-            o_bank[m, j, e] = pool.tile([P, 512], F32, name=tag)
-            nc.tensor.matmul_mx(
-                out=o_bank[m, j, e][:],
-                lhsT=hq[m][0][:, P * j : P * (j + 1)].bitcast(FP8X4),
-                lhsT_scale=hq[m][1][:, P * j : P * (j + 1)],
-                rhs=w2_c[:, 512 * e : 512 * (e + 1)].bitcast(FP8X4),
-                rhs_scale=w2_s[:, 512 * e : 512 * (e + 1)],
-                start=True,
-                stop=True,
-            )
+        def mm2(m, j, pool=o_psum, tag="ob"):
+            for e in range(2):
+                o_bank[m, j, e] = pool.tile([P, 512], F32, name=tag)
+                nc.tensor.matmul_mx(
+                    out=o_bank[m, j, e][:],
+                    lhsT=hq[m][0][:, P * j : P * (j + 1)].bitcast(FP8X4),
+                    lhsT_scale=hq[m][1][:, P * j : P * (j + 1)],
+                    rhs=w2_c[:, 512 * e : 512 * (e + 1)].bitcast(FP8X4),
+                    rhs_scale=w2_s[:, 512 * e : 512 * (e + 1)],
+                    start=True,
+                    stop=True,
+                )
 
-        def leave_o(copy, m, j, e):
-            i = 2 * m + j
-            if e == 0:
-                o_sb[i] = o_pool.tile([P, E], F32, name="osb")
-            copy(out=o_sb[i][:, 512 * e : 512 * (e + 1)], in_=o_bank[m, j, e][:])
-            if m >= PAIRS - 3:
+        def leave_o(m, j, copies=(nc.scalar.copy, nc.scalar.copy), halves=False):
+            i = GROUPS[m][0] + j
+            o_sb[i] = o_pool.tile([P, E], F32, name="osb")
+            for e in range(2):
                 cols = slice(512 * e, 512 * (e + 1))
-                nc.sync.dma_start(out=out_v[:, i, cols], in_=o_sb[i][:, cols])
-            elif e == 1:
+                copies[e](out=o_sb[i][:, cols], in_=o_bank[m, j, e][:])
+                if halves:
+                    nc.sync.dma_start(out=out_v[:, i, cols], in_=o_sb[i][:, cols])
+            if not halves:
                 nc.sync.dma_start(out=out_v[:, i, :], in_=o_sb[i][:])
 
-        def mm2_tile(m, j):
-            for e in range(2):
-                mm2(m, j, e, o_psum, "ob")
-
         scale_row = keep.tile([P, 2, 64], F32, name="scale_row")
+        gates_sum()
+        widen(nc.vector.tensor_copy, 0)
+        turn_x(0)
+        widen(nc.vector.tensor_copy, 1)
+        turn_x(1)
         nc.vector.tensor_copy(
             out=scale_row[:].rearrange("p g (n t) -> p g n t", t=4),
             in_=scale[:].unsqueeze(2).to_broadcast([P, 2, 16, 4]),
         )
-        gates_sum()
-        for g in range(2):
-            wide = keep.tile([P, 1024], BF16, name=f"xs_first{g}", align_bytes=64)
-            nc.vector.tensor_copy(out=wide[:], in_=x8_first[:, g, :, :].rearrange("p j k -> p (j k)").bitcast(FP8))
-            for j in range(2):
-                xs[2 * j + g] = wide[:, 512 * j : 512 * (j + 1)]
-            turn_x(0, g)
+        widen(nc.vector.tensor_copy, 2)
+        turn_x(2, a_psum, "a")
         gates_sigmoid()
-        widen(nc.gpsimd.tensor_copy, 6, 2, keep, "xs_first0")
+        widen(nc.scalar.copy, 3)
         leaf = leaf_probabilities()
-        widen(nc.scalar.copy, 4, 2)
-        widen(nc.scalar.copy, 8, 2)
-        widen(nc.scalar.copy, 10, 2)
-        widen(nc.scalar.copy, 14, 2)
+        widen(nc.gpsimd.tensor_copy, 4)
         scale_x(0, 0)
-        turn_x(1, 0)
         scale_x(0, 1)
-        turn_x(1, 1)
-        scale_x(1, 0)
         weave_w(0)
-        leave_w(0)
-        turn_x(2, 0)
+        turn_x(3, a_psum, "a")
         weave_w(1)
+        leave_w(0)
         leave_w(1)
-        scale_x(1, 1)
-        for n in range(2, 4):
-            weave_w(n)
-            leave_w(n)
-        turn_x(2, 1)
-        scale_x(2, 0)
-        quant_x(0)
-        quant_x(1)
-        quant_w(0)
-        quant_w(1)
+        widen(nc.scalar.copy, 5)
+        weave_w(2)
+        weave_w(3)
+        turn_x(4)
         spread_p(0)
+        leave_w(2)
+        leave_w(3)
+        turn_x(5)
         park_p()
-        for n in range(4, 6):
-            weave_w(n)
-            leave_w(n)
-        weave_w(6)
         turn_p(0)
         leave_p(0)
-        mm1(0, 0)
-        mm1(0, 1)
-        leave_w(6)
+        scale_x(1, 0)
+        scale_x(1, 1)
+        quant_x(0)
+        quant_w(0)
+        widen(nc.gpsimd.tensor_copy, 6, xg_pool, "xg0")
+        scale_x(2, 0)
+        quant_w(1)
+        quant_x(1)
+        weave_w(4)
+        weave_w(5)
+        mm1(0)
+        leave_w(4)
+        leave_w(5)
+        weave_w(6)
         weave_w(7)
-        widen(nc.scalar.copy, 18, 2)
+        widen(nc.gpsimd.tensor_copy, 8, xg_pool, "xg1")
+        leave_w(6)
         leave_w(7)
-        scale_x(2, 1)
-        quant_x(2)
-        widen(nc.gpsimd.tensor_copy, 12, 2, xg_pool, "xg2")
-        weigh_h(0)
-        mm1(1, 0)
-        mm1(1, 1)
-        turn_x(3, 0)
-        turn_x(3, 1)
+        widen(nc.scalar.copy, 7)
         spread_p(1)
+        scale_x(2, 1)
+        turn_x(6)
+        weigh_h(0)
+        mm1(1)
+        turn_x(7)
         turn_p(1)
-        widen(nc.scalar.copy, 22, 2)
         leave_p(1)
+        widen(nc.scalar.copy, 9)
+        quant_x(2)
         quant_w(2)
-        relu_h(nc.vector, 0)
         quant_w(3)
+        relu_h(nc.gpsimd, 0, keep, "w_g2")
+        weigh_h(1)
+        mm1(2)
+        widen(nc.scalar.copy, 10)
+        widen(nc.scalar.copy, 11)
+        scale_x(3, 0)
+        turn_x(8)
         quant_h(0)
-        mm2_tile(0, 0)
-
-        for k in range(AHEAD, PAIRS - 1):
-            m = k - LAG
-            for e in range(2):
-                leave_o(nc.scalar.copy, m - 1, 0, e)
-            if shared(m):
-                weigh_on_gpsimd(m)
-            elif shared(m - 1):
-                relu_h(nc.gpsimd, m)
-            else:
-                widen(nc.gpsimd.tensor_copy, 4 * (k + 1), 2, hg_pool, hg_tag[m - 1])
-                weigh_h(m)
-                relu_h(nc.gpsimd, m)
-            mm1(m + 1, 0)
-            mm1(m + 1, 1)
-            if shared(m + 1):
-                leave_h(m + 1)
-            if shared(m) and k + 2 < PAIRS:
-                widen(nc.scalar.copy, 4 * (k + 2), 2)
-            if shared(m + 2) and k + 3 < PAIRS:
-                widen(nc.scalar.copy, 4 * (k + 3), 4)
-            elif k + 3 < PAIRS:
-                widen(nc.scalar.copy, 4 * (k + 3) + 2, 2)
-            for g in range(2):
-                scale_x(k, g)
-                turn_x(k + 1, g)
-                if g == 0:
-                    mm2_tile(m - 1, 1)
-                    for e in range(2):
-                        leave_o(nc.scalar.copy, m - 1, 1, e)
-            if shared(m):
-                weigh_h(m + 1)
-            quant_h(m)
-            quant_x(k)
-            mm2_tile(m, 0)
-
+        relu_h(nc.gpsimd, 1, keep, "w_g2")
+        mm2(0, 0)
+        leave_o(0, 0)
+        scale_x(3, 1)
+        mm2(0, 1)
+        leave_o(0, 1)
+        turn_x(9)
+        weigh_h(2)
+        quant_x(3)
+        quant_h(1)
         last = PAIRS - 1
-        weigh_on_gpsimd(last - 2)
-        mm1(last - 1, 0)
-        mm1(last - 1, 1)
-        mm2_tile(last - 3, 1)
-        for n in range(4):
-            leave_o(nc.scalar.copy, last - 3, n // 2, n % 2)
+        for k in range(4, last):
+            gate_tag = f"xg{(k - 1) % 3}"
+            ahead = 2 * (k + 2)
+            if k - 1 in SHARED:
+                mm1(k - 1, o_psum, "ob")
+                leave_h(k - 1)
+            else:
+                mm1(k - 1)
+            mm2(k - 3, 0)
+            leave_o(k - 3, 0)
+            if k - 2 in SHARED:
+                weigh_on_gpsimd(k - 2, xg_pool, gate_tag)
+            elif k - 1 in SHARED or ahead >= TILES:
+                relu_h(nc.gpsimd, k - 2, xg_pool, gate_tag)
+            else:
+                widen(nc.gpsimd.tensor_copy, ahead, xg_pool, gate_tag)
+                relu_h(nc.gpsimd, k - 2)
+            for i in range(ahead, min(ahead + 2, TILES)):
+                if i not in xs:
+                    widen(nc.scalar.copy, i)
+            scale_x(k, 0)
+            turn_x(2 * k + 2)
+            mm2(k - 3, 1)
+            leave_o(k - 3, 1)
+            scale_x(k, 1)
+            turn_x(2 * k + 3)
+            if k - 1 not in SHARED:
+                weigh_h(k - 1)
+            quant_x(k)
+            quant_h(k - 2)
+        mm1(last - 1)
+        mm2(last - 3, 0)
+        leave_o(last - 3, 0)
+        relu_h(nc.gpsimd, last - 2, xg_pool, f"xg{(last - 1) % 3}")
         scale_x(last, 0)
-        scale_x(last, 1)
-        weigh_h(last - 1)
-        quant_h(last - 2)
+        mm2(last - 3, 1)
+        leave_o(last - 3, 1)
+        scale_x(last + 1, 0)
         quant_x(last)
+        quant_h(last - 2)
+        quant_x(last + 1)
+        weigh_h(last - 1)
+        mm2(last - 2, 0)
+        leave_o(last - 2, 0)
         relu_h(nc.gpsimd, last - 1)
-        mm2_tile(last - 2, 0)
-        mm1(last, 0)
-        mm2_tile(last - 2, 1)
-        mm1(last, 1)
-        leave_o(nc.scalar.copy, last - 2, 0, 0)
-        leave_o(nc.vector.tensor_copy, last - 2, 0, 1)
-        for e in range(2):
-            leave_o(nc.scalar.copy, last - 2, 1, e)
-        weigh_h(last, [0, 1])
+        mm1(last)
+        mm1(last + 1)
+        mm2(last - 2, 1)
+        leave_o(last - 2, 1)
+        weigh_h(last)
+        weigh_h(last + 1)
         quant_h(last - 1)
-        for e in range(2):
-            mm2(last - 1, 0, e, xt_psum, "xt")
-            leave_o(nc.scalar.copy, last - 1, 0, e)
-        weigh_h(last, [2, 3])
-        for e in range(2):
-            mm2(last - 1, 1, e, a_psum, "a")
-            leave_o(nc.scalar.copy, last - 1, 1, e)
         relu_h(nc.vector, last)
+        mm2(last - 1, 0, xt_psum, "xt")
+        leave_o(last - 1, 0, halves=True)
+        relu_h(nc.vector, last + 1)
         quant_h(last)
-        mm2_tile(last, 0)
-        mm2_tile(last, 1)
-        for j in range(2):
-            leave_o(nc.vector.tensor_copy, last, j, 0)
-            leave_o(nc.scalar.copy, last, j, 1)
+        mm2(last - 1, 1)
+        leave_o(last - 1, 1, halves=True)
+        quant_h(last + 1)
+        mm2(last, 0)
+        mm2(last + 1, 0, a_psum, "a")
+        leave_o(last, 0, (nc.vector.tensor_copy, nc.scalar.copy), True)
+        leave_o(last + 1, 0, (nc.vector.tensor_copy, nc.scalar.copy), True)

@@ -24,7 +24,8 @@ PAIRS = TILES // 2
 FLOPS = 2 * TOKENS * D * LF + 2 * TOKENS * LF * E
 BF16_MAX = 3.3895313892515355e38
 GROUPS = [(2 * k, 2) for k in range(PAIRS - 1)] + [(TILES - 2, 1), (TILES - 1, 1)]
-SHARED = ()
+SHARED = (6, 9, 12)
+CASTS = 3
 
 
 def tile_fastfeedforwardnetwork_pa_t_kernel(tc, x_bytes, x_scale, node_logits, node_b, w1, b1, w2, out):
@@ -38,13 +39,13 @@ def tile_fastfeedforwardnetwork_pa_t_kernel(tc, x_bytes, x_scale, node_logits, n
 
     with ExitStack() as ctx:
         keep = ctx.enter_context(tc.tile_pool(name="keep", bufs=1))
-        xs_pool = ctx.enter_context(tc.tile_pool(name="xs", bufs=7))
+        xs_pool = ctx.enter_context(tc.tile_pool(name="xs", bufs=12))
         h1_pool = ctx.enter_context(tc.tile_pool(name="h1", bufs=1))
         hg_pool = ctx.enter_context(tc.tile_pool(name="hg", bufs=2))
         prep_pool = ctx.enter_context(tc.tile_pool(name="prep", bufs=2))
         xg_pool = ctx.enter_context(tc.tile_pool(name="xg", bufs=1))
         xq_pool = ctx.enter_context(tc.tile_pool(name="xq", bufs=4))
-        h_pool = ctx.enter_context(tc.tile_pool(name="h", bufs=3))
+        h_pool = ctx.enter_context(tc.tile_pool(name="h", bufs=4))
         hq_pool = ctx.enter_context(tc.tile_pool(name="hq", bufs=3))
         o_pool = ctx.enter_context(tc.tile_pool(name="o", bufs=8))
         xt_psum = ctx.enter_context(tc.psum_pool(name="xt_psum", bufs=2))
@@ -77,16 +78,16 @@ def tile_fastfeedforwardnetwork_pa_t_kernel(tc, x_bytes, x_scale, node_logits, n
             )
 
         load_x(0, 2)
-        load_x(2, 4)
+        load_x(2, 6)
         load_w1(0)
-        load_x(4, 6)
-        load_w1(1)
         load_x(6, 8)
+        load_w1(1)
+        load_x(8, 12)
         bias_h = keep.tile([P, 4], BF16, name="bias_h")
         nc.sync.dma_start(out=bias_h[:], in_=b1_v)
         w2_raw = keep.tile([P, 4, E], BF16, name="w2_raw")
         nc.sync.dma_start(out=w2_raw[:], in_=w2_v)
-        for a in range(8, TILES, 4):
+        for a in range(12, TILES, 4):
             load_x(a, a + 4)
 
         ident = keep.tile([P, P], F32, name="ident")
@@ -198,22 +199,25 @@ def tile_fastfeedforwardnetwork_pa_t_kernel(tc, x_bytes, x_scale, node_logits, n
 
         xs, xt, xg, xq, a_bank, hp, h1, hg, hq, o_bank, o_sb = ({} for unused in range(11))
 
-        def widen(copy, i, pool=xs_pool, tag="xs"):
-            xs[i] = pool.tile([P, D], BF16, name=tag, align_bytes=64)
-            t, c = x8[i]
-            copy(out=xs[i][:], in_=t[:, c : c + D].bitcast(FP8))
+        def widen(copy, first, count, pool=xs_pool, tag="xs"):
+            wide = pool.tile([P, 512 * count], BF16, name=tag, align_bytes=64)
+            t, c = x8[first // 2]
+            c += 512 * (first % 2)
+            copy(out=wide[:], in_=t[:, c : c + 512 * count].bitcast(FP8))
+            for n in range(count):
+                xs[first + n] = wide[:, 512 * n : 512 * (n + 1)]
 
         def turn_x(i, pool=xt_psum, tag="xt"):
             xt[i] = pool.tile([P, 2, 2, P], F32, name=tag)
-            words = xs[i][:].bitcast(F32)
             for g in range(2):
+                words = xs[2 * i + g].bitcast(F32)
                 for u in range(2):
-                    nc.tensor.transpose(xt[i][:, u, g, :], words[:, 256 * g + u : 256 * (g + 1) : 2], ident[:])
+                    nc.tensor.transpose(xt[i][:, u, g, :], words[:, u:256:2], ident[:])
 
         def scale_x(m, j):
             first, n = GROUPS[m]
             if j == 0:
-                xg[m] = xg_pool.tile([P, 2, n, 512], BF16, name=f"xg{m % 3}", align_bytes=64)
+                xg[m] = xg_pool.tile([P, 2, n, 512], BF16, name=f"xg{m % 4}", align_bytes=64)
             nc.vector.tensor_tensor(
                 out=xg[m][:, :, j, :].rearrange("p g (a n u e) -> p g a n u e", n=16, u=2, e=2),
                 in0=xt[first + j][:].bitcast(BF16).rearrange("p u g (a n e) -> p g a n u e", n=16, e=2),
@@ -323,34 +327,52 @@ def tile_fastfeedforwardnetwork_pa_t_kernel(tc, x_bytes, x_scale, node_logits, n
             if not halves:
                 nc.sync.dma_start(out=out_v[:, i, :], in_=o_sb[i][:])
 
+        last = PAIRS - 1
+
+        def gpsimd_halves(k):
+            if k < 5 or k + 2 > last or k - 2 in SHARED or k - 1 in SHARED:
+                return 0
+            return 3
+
+        left = [23] + [h for k in range(5, last - 1) for h in range(4 * (k + 2) + gpsimd_halves(k), 4 * (k + 3))]
+
+        def scalar_casts(count):
+            while count > 0 and left:
+                run = 2 if left[0] % 2 == 0 else 1
+                widen(nc.scalar.copy, left[0], run)
+                for n in range(run):
+                    left.remove(left[0])
+                count -= run
+
         scale_row = keep.tile([P, 2, 64], F32, name="scale_row")
         gates_sum()
-        widen(nc.vector.tensor_copy, 0)
+        widen(nc.vector.tensor_copy, 0, 2)
         turn_x(0)
-        widen(nc.vector.tensor_copy, 1)
+        widen(nc.vector.tensor_copy, 2, 2)
         turn_x(1)
         nc.vector.tensor_copy(
             out=scale_row[:].rearrange("p g (n t) -> p g n t", t=4),
             in_=scale[:].unsqueeze(2).to_broadcast([P, 2, 16, 4]),
         )
-        widen(nc.vector.tensor_copy, 2)
+        widen(nc.vector.tensor_copy, 4, 2)
         turn_x(2, a_psum, "a")
         gates_sigmoid()
-        widen(nc.scalar.copy, 3)
+        for i in range(3, 7):
+            widen(nc.scalar.copy, 2 * i, 2)
         leaf = leaf_probabilities()
-        widen(nc.gpsimd.tensor_copy, 4)
+        widen(nc.gpsimd.tensor_copy, 14, 2, keep, "xs7")
+        turn_x(3, a_psum, "a")
         scale_x(0, 0)
         scale_x(0, 1)
         weave_w(0)
-        turn_x(3, a_psum, "a")
         weave_w(1)
         leave_w(0)
         leave_w(1)
-        widen(nc.scalar.copy, 5)
+        spread_p(0)
+        widen(nc.scalar.copy, 16, 2)
+        turn_x(4)
         weave_w(2)
         weave_w(3)
-        turn_x(4)
-        spread_p(0)
         leave_w(2)
         leave_w(3)
         turn_x(5)
@@ -361,113 +383,137 @@ def tile_fastfeedforwardnetwork_pa_t_kernel(tc, x_bytes, x_scale, node_logits, n
         scale_x(1, 1)
         quant_x(0)
         quant_w(0)
-        widen(nc.gpsimd.tensor_copy, 6, xg_pool, "xg0")
+        widen(nc.gpsimd.tensor_copy, 20, 3, keep, "w_g0")
         scale_x(2, 0)
-        quant_w(1)
-        quant_x(1)
+        turn_x(6)
         weave_w(4)
-        weave_w(5)
-        mm1(0)
+        widen(nc.scalar.copy, 18, 2)
         leave_w(4)
-        leave_w(5)
-        weave_w(6)
-        weave_w(7)
-        widen(nc.gpsimd.tensor_copy, 8, xg_pool, "xg1")
-        leave_w(6)
-        leave_w(7)
-        widen(nc.scalar.copy, 7)
         spread_p(1)
         scale_x(2, 1)
-        turn_x(6)
-        weigh_h(0)
-        mm1(1)
         turn_x(7)
+        quant_x(1)
+        quant_w(1)
+        widen(nc.gpsimd.tensor_copy, 24, 4, keep, "w_g1")
+        mm1(0)
+        mm1(1, o_psum, "ob")
+        scale_x(3, 0)
+        weave_w(5)
+        weave_w(6)
+        turn_x(8)
+        scalar_casts(3)
+        leave_w(5)
+        leave_w(6)
+        scalar_casts(2)
+        weigh_h(0)
+        relu_h(nc.gpsimd, 0)
+        weigh_h(1)
+        weave_w(7)
+        leave_w(7)
         turn_p(1)
         leave_p(1)
-        widen(nc.scalar.copy, 9)
+        scalar_casts(4)
+        scale_x(3, 1)
+        turn_x(9)
         quant_x(2)
+        quant_x(3)
         quant_w(2)
         quant_w(3)
-        relu_h(nc.gpsimd, 0, keep, "w_g2")
-        weigh_h(1)
-        mm1(2)
-        widen(nc.scalar.copy, 10)
-        widen(nc.scalar.copy, 11)
-        scale_x(3, 0)
-        turn_x(8)
         quant_h(0)
-        relu_h(nc.gpsimd, 1, keep, "w_g2")
+        mm1(2)
         mm2(0, 0)
         leave_o(0, 0)
-        scale_x(3, 1)
+        relu_h(nc.gpsimd, 1, keep, "w_g3")
+        scale_x(4, 0)
+        turn_x(10)
+        weigh_h(2)
+        mm1(3)
+        relu_h(nc.gpsimd, 2)
         mm2(0, 1)
         leave_o(0, 1)
-        turn_x(9)
-        weigh_h(2)
-        quant_x(3)
+        scale_x(4, 1)
+        turn_x(11)
+        scalar_casts(2)
+        weigh_h(3)
+        quant_x(4)
         quant_h(1)
-        last = PAIRS - 1
-        for k in range(4, last):
-            gate_tag = f"xg{(k - 1) % 3}"
-            ahead = 2 * (k + 2)
-            if k - 1 in SHARED:
+        quant_h(2)
+        for k in range(5, last):
+            gate_tag = f"xg{(k - 1) % 4}"
+            short = k - 1 in SHARED
+            if short:
                 mm1(k - 1, o_psum, "ob")
                 leave_h(k - 1)
             else:
                 mm1(k - 1)
-            mm2(k - 3, 0)
-            leave_o(k - 3, 0)
+            if k == 5:
+                mm2(1, 0)
+                leave_o(1, 0)
+                mm2(1, 1)
+                leave_o(1, 1)
             if k - 2 in SHARED:
                 weigh_on_gpsimd(k - 2, xg_pool, gate_tag)
-            elif k - 1 in SHARED or ahead >= TILES:
-                relu_h(nc.gpsimd, k - 2, xg_pool, gate_tag)
-            else:
-                widen(nc.gpsimd.tensor_copy, ahead, xg_pool, gate_tag)
+            elif gpsimd_halves(k):
+                widen(nc.gpsimd.tensor_copy, 4 * (k + 2), gpsimd_halves(k), xg_pool, gate_tag)
                 relu_h(nc.gpsimd, k - 2)
-            for i in range(ahead, min(ahead + 2, TILES)):
-                if i not in xs:
-                    widen(nc.scalar.copy, i)
+            else:
+                relu_h(nc.gpsimd, k - 2, xg_pool, gate_tag)
             scale_x(k, 0)
-            turn_x(2 * k + 2)
-            mm2(k - 3, 1)
-            leave_o(k - 3, 1)
-            scale_x(k, 1)
-            turn_x(2 * k + 3)
-            if k - 1 not in SHARED:
+            if short or k == 5:
+                turn_x(2 * k + 2)
+                mm2(k - 3, 0)
+                leave_o(k - 3, 0)
+                scale_x(k, 1)
+                turn_x(2 * k + 3)
+                mm2(k - 3, 1)
+                leave_o(k - 3, 1)
+            else:
+                mm2(k - 3, 0)
+                leave_o(k - 3, 0)
+                scalar_casts(CASTS)
+                turn_x(2 * k + 2)
+                mm2(k - 3, 1)
+                leave_o(k - 3, 1)
+                scale_x(k, 1)
+                turn_x(2 * k + 3)
+            if short:
+                quant_h(k - 2)
+                quant_x(k)
+            else:
                 weigh_h(k - 1)
-            quant_x(k)
-            quant_h(k - 2)
+                quant_x(k)
+                quant_h(k - 2)
         mm1(last - 1)
         mm2(last - 3, 0)
         leave_o(last - 3, 0)
-        relu_h(nc.gpsimd, last - 2, xg_pool, f"xg{(last - 1) % 3}")
-        scale_x(last, 0)
         mm2(last - 3, 1)
         leave_o(last - 3, 1)
-        scale_x(last + 1, 0)
+        relu_h(nc.gpsimd, last - 2, xg_pool, f"xg{(last - 1) % 4}")
+        scale_x(last, 0)
+        weigh_h(last - 1)
         quant_x(last)
         quant_h(last - 2)
-        quant_x(last + 1)
-        weigh_h(last - 1)
+        mm1(last)
         mm2(last - 2, 0)
         leave_o(last - 2, 0)
-        relu_h(nc.gpsimd, last - 1)
-        mm1(last)
-        mm1(last + 1)
         mm2(last - 2, 1)
         leave_o(last - 2, 1)
+        relu_h(nc.gpsimd, last - 1, xg_pool, f"xg{last % 4}")
+        scale_x(last + 1, 0)
         weigh_h(last)
-        weigh_h(last + 1)
+        quant_x(last + 1)
         quant_h(last - 1)
+        mm1(last + 1)
         relu_h(nc.vector, last)
-        mm2(last - 1, 0, xt_psum, "xt")
-        leave_o(last - 1, 0, halves=True)
-        relu_h(nc.vector, last + 1)
+        mm2(last - 1, 0)
+        leave_o(last - 1, 0)
         quant_h(last)
         mm2(last - 1, 1)
         leave_o(last - 1, 1, halves=True)
+        weigh_h(last + 1)
+        relu_h(nc.vector, last + 1)
         quant_h(last + 1)
-        mm2(last, 0)
+        mm2(last, 0, xt_psum, "xt")
+        leave_o(last, 0, halves=True)
         mm2(last + 1, 0, a_psum, "a")
-        leave_o(last, 0, (nc.vector.tensor_copy, nc.scalar.copy), True)
-        leave_o(last + 1, 0, (nc.vector.tensor_copy, nc.scalar.copy), True)
+        leave_o(last + 1, 0, (nc.vector.tensor_copy, nc.vector.tensor_copy), True)

@@ -23,9 +23,9 @@ TILES = TOKENS // P
 PAIRS = TILES // 2
 FLOPS = 2 * TOKENS * D * LF + 2 * TOKENS * LF * E
 BF16_MAX = 3.3895313892515355e38
-GROUPS = [(2 * k, 2) for k in range(PAIRS - 1)] + [(TILES - 2, 1), (TILES - 1, 1)]
-SHARED = (6, 9, 12)
-CASTS = 3
+GROUPS = [(2 * k, 2) for k in range(14)] + [(i, 1) for i in range(28, TILES)]
+SHARED = (5,8,11,15)
+CASTS = 4
 
 
 def tile_fastfeedforwardnetwork_pa_t_kernel(tc, x_bytes, x_scale, node_logits, node_b, w1, b1, w2, out):
@@ -39,7 +39,7 @@ def tile_fastfeedforwardnetwork_pa_t_kernel(tc, x_bytes, x_scale, node_logits, n
 
     with ExitStack() as ctx:
         keep = ctx.enter_context(tc.tile_pool(name="keep", bufs=1))
-        xs_pool = ctx.enter_context(tc.tile_pool(name="xs", bufs=12))
+        xs_pool = ctx.enter_context(tc.tile_pool(name="xs", bufs=16))
         h1_pool = ctx.enter_context(tc.tile_pool(name="h1", bufs=1))
         hg_pool = ctx.enter_context(tc.tile_pool(name="hg", bufs=2))
         prep_pool = ctx.enter_context(tc.tile_pool(name="prep", bufs=2))
@@ -65,6 +65,7 @@ def tile_fastfeedforwardnetwork_pa_t_kernel(tc, x_bytes, x_scale, node_logits, n
         nc.scalar.dma_start(out=bias_n[:], in_=node_b.partition_broadcast(P))
         scale = keep.tile([P, 2, 4], F32, name="scale")
         nc.scalar.dma_start(out=scale[:], in_=scale_v)
+        load_x(0, 1)
         logits = keep.tile([P, TILES * NODES], BF16, name="logits")
         nc.sync.dma_start(out=logits[:], in_=logits_v)
 
@@ -77,8 +78,8 @@ def tile_fastfeedforwardnetwork_pa_t_kernel(tc, x_bytes, x_scale, node_logits, n
                 in_=w1[:, 512 * g : 512 * (g + 1), :].rearrange("l (p j) f -> p l (j f)", j=4),
             )
 
-        load_x(0, 2)
-        load_x(2, 6)
+        load_x(1, 3)
+        load_x(3, 6)
         load_w1(0)
         load_x(6, 8)
         load_w1(1)
@@ -280,6 +281,12 @@ def tile_fastfeedforwardnetwork_pa_t_kernel(tc, x_bytes, x_scale, node_logits, n
                 op1=OP.max,
             )
 
+        def relu_on_scalar(m):
+            hg[m] = hg_pool.tile([P, 512 * GROUPS[m][1]], BF16, name="hg", align_bytes=64)
+            nc.scalar.activation(
+                out=hg[m][:].rearrange("p (n t) -> p n t", t=4), in_=hp[m][:].rearrange("p t n -> p n t"), func=ACT.Relu
+            )
+
         def leave_h(m):
             h1[m] = h1_pool.tile([P, 4, P * GROUPS[m][1]], F32, name="h1")
             for t in range(4):
@@ -327,14 +334,12 @@ def tile_fastfeedforwardnetwork_pa_t_kernel(tc, x_bytes, x_scale, node_logits, n
             if not halves:
                 nc.sync.dma_start(out=out_v[:, i, :], in_=o_sb[i][:])
 
-        last = PAIRS - 1
-
         def gpsimd_halves(k):
-            if k < 5 or k + 2 > last or k - 2 in SHARED or k - 1 in SHARED:
-                return 0
-            return 3
+            free = k >= 5 and GROUPS[k][1] == 2 and k - 2 not in SHARED and k - 1 not in SHARED
+            return 2 if free else 0
 
-        left = [23] + [h for k in range(5, last - 1) for h in range(4 * (k + 2) + gpsimd_halves(k), 4 * (k + 3))]
+        taken = [2 * GROUPS[k][0] + 8 + n for k in range(len(GROUPS)) for n in range(gpsimd_halves(k))]
+        left = [h for h in range(20, 2 * TILES) if h not in taken and not 24 <= h < 28]
 
         def scalar_casts(count):
             while count > 0 and left:
@@ -345,53 +350,52 @@ def tile_fastfeedforwardnetwork_pa_t_kernel(tc, x_bytes, x_scale, node_logits, n
                 count -= run
 
         scale_row = keep.tile([P, 2, 64], F32, name="scale_row")
-        gates_sum()
         widen(nc.vector.tensor_copy, 0, 2)
         turn_x(0)
-        widen(nc.vector.tensor_copy, 2, 2)
-        turn_x(1)
+        gates_sum()
         nc.vector.tensor_copy(
             out=scale_row[:].rearrange("p g (n t) -> p g n t", t=4),
             in_=scale[:].unsqueeze(2).to_broadcast([P, 2, 16, 4]),
         )
-        widen(nc.vector.tensor_copy, 4, 2)
+        widen(nc.vector.tensor_copy, 2, 2)
+        turn_x(1)
+        widen(nc.gpsimd.tensor_copy, 4, 2, keep, "xs2")
         turn_x(2, a_psum, "a")
         gates_sigmoid()
         for i in range(3, 7):
             widen(nc.scalar.copy, 2 * i, 2)
         leaf = leaf_probabilities()
-        widen(nc.gpsimd.tensor_copy, 14, 2, keep, "xs7")
         turn_x(3, a_psum, "a")
         scale_x(0, 0)
         scale_x(0, 1)
         weave_w(0)
-        weave_w(1)
-        leave_w(0)
-        leave_w(1)
-        spread_p(0)
-        widen(nc.scalar.copy, 16, 2)
         turn_x(4)
+        weave_w(1)
+        turn_x(5)
+        leave_w(0)
+        spread_p(0)
+        leave_w(1)
         weave_w(2)
         weave_w(3)
+        widen(nc.scalar.copy, 16, 2)
         leave_w(2)
         leave_w(3)
-        turn_x(5)
-        park_p()
-        turn_p(0)
-        leave_p(0)
         scale_x(1, 0)
         scale_x(1, 1)
         quant_x(0)
-        quant_w(0)
-        widen(nc.gpsimd.tensor_copy, 20, 3, keep, "w_g0")
+        widen(nc.gpsimd.tensor_copy, 14, 2, xg_pool, "xg0")
         scale_x(2, 0)
         turn_x(6)
+        park_p()
+        turn_p(0)
+        leave_p(0)
         weave_w(4)
         widen(nc.scalar.copy, 18, 2)
         leave_w(4)
         spread_p(1)
         scale_x(2, 1)
         turn_x(7)
+        quant_w(0)
         quant_x(1)
         quant_w(1)
         widen(nc.gpsimd.tensor_copy, 24, 4, keep, "w_g1")
@@ -401,16 +405,16 @@ def tile_fastfeedforwardnetwork_pa_t_kernel(tc, x_bytes, x_scale, node_logits, n
         weave_w(5)
         weave_w(6)
         turn_x(8)
-        scalar_casts(3)
+        scalar_casts(4)
         leave_w(5)
         leave_w(6)
-        scalar_casts(2)
         weigh_h(0)
         relu_h(nc.gpsimd, 0)
         weigh_h(1)
         weave_w(7)
         leave_w(7)
         turn_p(1)
+        scalar_casts(2)
         leave_p(1)
         scalar_casts(4)
         scale_x(3, 1)
@@ -424,6 +428,7 @@ def tile_fastfeedforwardnetwork_pa_t_kernel(tc, x_bytes, x_scale, node_logits, n
         mm2(0, 0)
         leave_o(0, 0)
         relu_h(nc.gpsimd, 1, keep, "w_g3")
+        scalar_casts(2)
         scale_x(4, 0)
         turn_x(10)
         weigh_h(2)
@@ -433,12 +438,13 @@ def tile_fastfeedforwardnetwork_pa_t_kernel(tc, x_bytes, x_scale, node_logits, n
         leave_o(0, 1)
         scale_x(4, 1)
         turn_x(11)
-        scalar_casts(2)
+        scalar_casts(4)
         weigh_h(3)
         quant_x(4)
         quant_h(1)
         quant_h(2)
-        for k in range(5, last):
+        for k in range(5, len(GROUPS)):
+            first, count = GROUPS[k]
             gate_tag = f"xg{(k - 1) % 4}"
             short = k - 1 in SHARED
             if short:
@@ -452,68 +458,43 @@ def tile_fastfeedforwardnetwork_pa_t_kernel(tc, x_bytes, x_scale, node_logits, n
                 mm2(1, 1)
                 leave_o(1, 1)
             if k - 2 in SHARED:
-                weigh_on_gpsimd(k - 2, xg_pool, gate_tag)
+                weigh_on_gpsimd(k - 2, xg_pool, f"xg{(k - 2) % 4}")
             elif gpsimd_halves(k):
-                widen(nc.gpsimd.tensor_copy, 4 * (k + 2), gpsimd_halves(k), xg_pool, gate_tag)
+                widen(nc.gpsimd.tensor_copy, 2 * first + 8, gpsimd_halves(k), xg_pool, gate_tag)
                 relu_h(nc.gpsimd, k - 2)
             else:
                 relu_h(nc.gpsimd, k - 2, xg_pool, gate_tag)
-            scale_x(k, 0)
-            if short or k == 5:
-                turn_x(2 * k + 2)
-                mm2(k - 3, 0)
-                leave_o(k - 3, 0)
-                scale_x(k, 1)
-                turn_x(2 * k + 3)
-                mm2(k - 3, 1)
-                leave_o(k - 3, 1)
-            else:
-                mm2(k - 3, 0)
-                leave_o(k - 3, 0)
-                scalar_casts(CASTS)
-                turn_x(2 * k + 2)
-                mm2(k - 3, 1)
-                leave_o(k - 3, 1)
-                scale_x(k, 1)
-                turn_x(2 * k + 3)
+            early = short or k == 5
+            for j in range(2):
+                if j < count:
+                    scale_x(k, j)
+                if early and j < count and first + j + 2 < TILES:
+                    turn_x(first + j + 2)
+                if j < GROUPS[k - 3][1]:
+                    mm2(k - 3, j)
+                    leave_o(k - 3, j)
+                if j == 0 and not early:
+                    scalar_casts(2 if k in SHARED else CASTS)
+                if not early and j < count and first + j + 2 < TILES:
+                    turn_x(first + j + 2)
             if short:
+                scalar_casts(2)
                 quant_h(k - 2)
                 quant_x(k)
             else:
                 weigh_h(k - 1)
                 quant_x(k)
                 quant_h(k - 2)
-        mm1(last - 1)
-        mm2(last - 3, 0)
-        leave_o(last - 3, 0)
-        mm2(last - 3, 1)
-        leave_o(last - 3, 1)
-        relu_h(nc.gpsimd, last - 2, xg_pool, f"xg{(last - 1) % 4}")
-        scale_x(last, 0)
-        weigh_h(last - 1)
-        quant_x(last)
-        quant_h(last - 2)
-        mm1(last)
-        mm2(last - 2, 0)
-        leave_o(last - 2, 0)
-        mm2(last - 2, 1)
-        leave_o(last - 2, 1)
-        relu_h(nc.gpsimd, last - 1, xg_pool, f"xg{last % 4}")
-        scale_x(last + 1, 0)
-        weigh_h(last)
-        quant_x(last + 1)
-        quant_h(last - 1)
-        mm1(last + 1)
-        relu_h(nc.vector, last)
-        mm2(last - 1, 0)
-        leave_o(last - 1, 0)
-        quant_h(last)
-        mm2(last - 1, 1)
-        leave_o(last - 1, 1, halves=True)
-        weigh_h(last + 1)
-        relu_h(nc.vector, last + 1)
-        quant_h(last + 1)
-        mm2(last, 0, xt_psum, "xt")
-        leave_o(last, 0, halves=True)
-        mm2(last + 1, 0, a_psum, "a")
-        leave_o(last + 1, 0, (nc.vector.tensor_copy, nc.vector.tensor_copy), True)
+        end = len(GROUPS) - 1
+        relu_h(nc.vector, end - 1)
+        mm1(end)
+        mm2(end - 2, 0)
+        leave_o(end - 2, 0, halves=True)
+        quant_h(end - 1)
+        weigh_h(end)
+        relu_h(nc.vector, end)
+        mm2(end - 1, 0)
+        leave_o(end - 1, 0, halves=True)
+        quant_h(end)
+        mm2(end, 0)
+        leave_o(end, 0, (nc.vector.tensor_copy, nc.scalar.copy), True)

@@ -24,7 +24,7 @@ PAIRS = TILES // 2
 FLOPS = 2 * TOKENS * D * LF + 2 * TOKENS * LF * E
 BF16_MAX = 3.3895313892515355e38
 GROUPS = [(2 * k, 2) for k in range(14)] + [(i, 1) for i in range(28, TILES)]
-SHARED = (5,8,11,15)
+SHARED = (5, 8, 11)
 CASTS = 4
 
 
@@ -369,8 +369,8 @@ def tile_fastfeedforwardnetwork_pa_t_kernel(tc, x_bytes, x_scale, node_logits, n
         scale_x(0, 0)
         scale_x(0, 1)
         weave_w(0)
-        turn_x(4)
         weave_w(1)
+        turn_x(4)
         turn_x(5)
         leave_w(0)
         spread_p(0)
@@ -389,12 +389,12 @@ def tile_fastfeedforwardnetwork_pa_t_kernel(tc, x_bytes, x_scale, node_logits, n
         park_p()
         turn_p(0)
         leave_p(0)
+        scale_x(2, 1)
+        turn_x(7)
         weave_w(4)
         widen(nc.scalar.copy, 18, 2)
         leave_w(4)
         spread_p(1)
-        scale_x(2, 1)
-        turn_x(7)
         quant_w(0)
         quant_x(1)
         quant_w(1)
@@ -404,7 +404,6 @@ def tile_fastfeedforwardnetwork_pa_t_kernel(tc, x_bytes, x_scale, node_logits, n
         scale_x(3, 0)
         weave_w(5)
         weave_w(6)
-        turn_x(8)
         scalar_casts(4)
         leave_w(5)
         leave_w(6)
@@ -413,6 +412,7 @@ def tile_fastfeedforwardnetwork_pa_t_kernel(tc, x_bytes, x_scale, node_logits, n
         weigh_h(1)
         weave_w(7)
         leave_w(7)
+        turn_x(8)
         turn_p(1)
         scalar_casts(2)
         leave_p(1)
@@ -443,7 +443,8 @@ def tile_fastfeedforwardnetwork_pa_t_kernel(tc, x_bytes, x_scale, node_logits, n
         quant_x(4)
         quant_h(1)
         quant_h(2)
-        for k in range(5, len(GROUPS)):
+        end = len(GROUPS) - 1
+        for k in range(5, end):
             first, count = GROUPS[k]
             gate_tag = f"xg{(k - 1) % 4}"
             short = k - 1 in SHARED
@@ -470,13 +471,16 @@ def tile_fastfeedforwardnetwork_pa_t_kernel(tc, x_bytes, x_scale, node_logits, n
                     scale_x(k, j)
                 if early and j < count and first + j + 2 < TILES:
                     turn_x(first + j + 2)
+                if not early and count == 2 and j == 1:
+                    turn_x(first + 2)
+                    turn_x(first + 3)
                 if j < GROUPS[k - 3][1]:
                     mm2(k - 3, j)
                     leave_o(k - 3, j)
                 if j == 0 and not early:
                     scalar_casts(2 if k in SHARED else CASTS)
-                if not early and j < count and first + j + 2 < TILES:
-                    turn_x(first + j + 2)
+                if not early and count == 1 and j == 0 and first + 2 < TILES:
+                    turn_x(first + 2)
             if short:
                 scalar_casts(2)
                 quant_h(k - 2)
@@ -485,16 +489,37 @@ def tile_fastfeedforwardnetwork_pa_t_kernel(tc, x_bytes, x_scale, node_logits, n
                 weigh_h(k - 1)
                 quant_x(k)
                 quant_h(k - 2)
-        end = len(GROUPS) - 1
+        mm1(end - 1)
+        relu_h(nc.gpsimd, end - 2, xg_pool, f"xg{(end - 1) % 4}")
+        mm2(end - 3, 0)
+        leave_o(end - 3, 0)
+        scale_x(end, 0)
+        quant_h(end - 2)
+        mm2(end - 2, 0)
+        leave_o(end - 2, 0)
+        weigh_h(end - 1)
+        quant_x(end)
         relu_h(nc.vector, end - 1)
         mm1(end)
-        mm2(end - 2, 0)
-        leave_o(end - 2, 0, halves=True)
         quant_h(end - 1)
         weigh_h(end)
         relu_h(nc.vector, end)
         mm2(end - 1, 0)
         leave_o(end - 1, 0, halves=True)
         quant_h(end)
-        mm2(end, 0)
-        leave_o(end, 0, (nc.vector.tensor_copy, nc.scalar.copy), True)
+        last = o_pool.tile([P, E], F32, name="osb")
+        for e in range(4):
+            cols = slice(256 * e, 256 * (e + 1))
+            bank = xt_psum.tile([P, 256], F32, name="xt") if e < 2 else a_psum.tile([P, 256], F32, name="a")
+            nc.tensor.matmul_mx(
+                out=bank[:],
+                lhsT=hq[end][0][:].bitcast(FP8X4),
+                lhsT_scale=hq[end][1][:],
+                rhs=w2_c[:, cols].bitcast(FP8X4),
+                rhs_scale=w2_s[:, cols],
+                start=True,
+                stop=True,
+            )
+            copy = nc.vector.tensor_copy if e % 2 == 0 else nc.scalar.copy
+            copy(out=last[:, cols], in_=bank[:])
+            nc.sync.dma_start(out=out_v[:, TILES - 1, cols], in_=last[:, cols])

@@ -24,7 +24,7 @@ PAIRS = TILES // 2
 FLOPS = 2 * TOKENS * D * LF + 2 * TOKENS * LF * E
 BF16_MAX = 3.3895313892515355e38
 GROUPS = [(2 * k, 2) for k in range(14)] + [(i, 1) for i in range(28, TILES)]
-SHARED = (5, 8, 11)
+SHARED = (6, 9, 11)
 CASTS = 4
 
 
@@ -243,9 +243,9 @@ def tile_fastfeedforwardnetwork_pa_t_kernel(tc, x_bytes, x_scale, node_logits, n
             n = GROUPS[m][1]
             width = P * n
             for t in range(4):
-                if t * width % 512 == 0:
+                if t % 2 == 0:
                     bank = pool.tile([P, 512], F32, name=tag)
-                a_bank[m, t] = bank[:, t * width % 512 : t * width % 512 + width]
+                a_bank[m, t] = bank[:, t % 2 * width : (t % 2 + 1) * width]
                 for g in range(2):
                     nc.tensor.matmul_mx(
                         out=a_bank[m, t],
@@ -434,10 +434,10 @@ def tile_fastfeedforwardnetwork_pa_t_kernel(tc, x_bytes, x_scale, node_logits, n
         weigh_h(2)
         mm1(3)
         relu_h(nc.gpsimd, 2)
-        mm2(0, 1)
-        leave_o(0, 1)
         scale_x(4, 1)
         turn_x(11)
+        mm2(0, 1)
+        leave_o(0, 1)
         scalar_casts(4)
         weigh_h(3)
         quant_x(4)

@@ -20,12 +20,13 @@ E = 1024
 LEAVES = 16
 NODES = 15
 TILES = TOKENS // P
-PAIRS = TILES // 2
 FLOPS = 2 * TOKENS * D * LF + 2 * TOKENS * LF * E
 BF16_MAX = 3.3895313892515355e38
 GROUPS = [(2 * k, 2) for k in range(14)] + [(i, 1) for i in range(28, TILES)]
-SHARED = (6, 9, 11)
-CASTS = 4
+SHARED = (7, 9, 11)
+LONG_HALVES = 5
+SHORT_HALVES = 3
+SCALAR_CASTS = (11, 13)
 
 
 def tile_fastfeedforwardnetwork_pa_t_kernel(tc, x_bytes, x_scale, node_logits, node_b, w1, b1, w2, out):
@@ -39,27 +40,24 @@ def tile_fastfeedforwardnetwork_pa_t_kernel(tc, x_bytes, x_scale, node_logits, n
 
     with ExitStack() as ctx:
         keep = ctx.enter_context(tc.tile_pool(name="keep", bufs=1))
-        xs_pool = ctx.enter_context(tc.tile_pool(name="xs", bufs=16))
-        h1_pool = ctx.enter_context(tc.tile_pool(name="h1", bufs=1))
-        hg_pool = ctx.enter_context(tc.tile_pool(name="hg", bufs=2))
-        prep_pool = ctx.enter_context(tc.tile_pool(name="prep", bufs=2))
-        xg_pool = ctx.enter_context(tc.tile_pool(name="xg", bufs=1))
-        xq_pool = ctx.enter_context(tc.tile_pool(name="xq", bufs=4))
-        h_pool = ctx.enter_context(tc.tile_pool(name="h", bufs=4))
+        xs_pool = ctx.enter_context(tc.tile_pool(name="xs", bufs=10))
+        two = ctx.enter_context(tc.tile_pool(name="two", bufs=2))
         hq_pool = ctx.enter_context(tc.tile_pool(name="hq", bufs=3))
         o_pool = ctx.enter_context(tc.tile_pool(name="o", bufs=8))
-        xt_psum = ctx.enter_context(tc.psum_pool(name="xt_psum", bufs=2))
-        a_psum = ctx.enter_context(tc.psum_pool(name="a_psum", bufs=2))
-        o_psum = ctx.enter_context(tc.psum_pool(name="o_psum", bufs=4))
+        psum = ctx.enter_context(tc.psum_pool(name="psum", bufs=1))
         ctx.enter_context(tc.manual_schedule())
 
-        x8 = {}
+        free_banks = list(range(8))
+
+        def take_bank(shape, dtype):
+            b = free_banks[0]
+            free_banks.remove(b)
+            return b, psum.tile(shape, dtype, name=f"bank{b}")
+
+        x8 = keep.tile([P, TILES * D], U8, name="x8")
 
         def load_x(a, b):
-            t = keep.tile([P, (b - a) * D], U8, name=f"x8_{a}")
-            nc.sync.dma_start(out=t[:], in_=x_v[:, a:b, :].rearrange("p i k -> p (i k)"))
-            for i in range(a, b):
-                x8[i] = (t, (i - a) * D)
+            nc.sync.dma_start(out=x8[:, a * D : b * D], in_=x_v[:, a:b, :].rearrange("p i k -> p (i k)"))
 
         bias_n = keep.tile([P, NODES], BF16, name="bias_n")
         nc.scalar.dma_start(out=bias_n[:], in_=node_b.partition_broadcast(P))
@@ -79,32 +77,32 @@ def tile_fastfeedforwardnetwork_pa_t_kernel(tc, x_bytes, x_scale, node_logits, n
             )
 
         load_x(1, 3)
-        load_x(3, 6)
+        load_x(3, 5)
         load_w1(0)
-        load_x(6, 8)
+        load_x(5, 8)
         load_w1(1)
-        load_x(8, 12)
         bias_h = keep.tile([P, 4], BF16, name="bias_h")
         nc.sync.dma_start(out=bias_h[:], in_=b1_v)
+        load_x(8, 12)
         w2_raw = keep.tile([P, 4, E], BF16, name="w2_raw")
         nc.sync.dma_start(out=w2_raw[:], in_=w2_v)
-        for a in range(12, TILES, 4):
-            load_x(a, a + 4)
+        load_x(12, 16)
 
         ident = keep.tile([P, P], F32, name="ident")
         make_identity(nc, ident[:])
         ident16 = keep.tile([P, P], BF16, name="ident16")
         make_identity(nc, ident16[:])
 
-        z = keep.tile([P, TILES, NODES], F32, name="z")
-        gate = keep.tile([P, 2, TILES, NODES], F32, name="gate")
+        z = keep.tile([P, NODES, TILES], F32, name="z")
+        gate = keep.tile([P, 2, NODES, TILES], F32, name="gate")
+        leaf = keep.tile([P, 4, LEAVES, 8], F32, name="leaf")
         prep, p_bank, p_sb = {}, {}, {}
 
         def gates_sum():
             nc.vector.tensor_tensor(
                 out=z[:],
-                in0=logits[:].rearrange("p (i v) -> p i v", v=NODES),
-                in1=bias_n[:].unsqueeze(1).to_broadcast([P, TILES, NODES]),
+                in0=logits[:].rearrange("p (i v) -> p v i", v=NODES),
+                in1=bias_n[:].unsqueeze(2).to_broadcast([P, NODES, TILES]),
                 op=OP.add,
             )
 
@@ -113,58 +111,66 @@ def tile_fastfeedforwardnetwork_pa_t_kernel(tc, x_bytes, x_scale, node_logits, n
             nc.scalar.activation(out=gate[:, 1, :, :], in_=z[:], func=ACT.Sigmoid, scale=-1.0)
 
         def leaf_probabilities():
-            prob = gate[:, :, :, 0].rearrange("p s i -> p i s")
+            prob = gate[:, :, 0, :]
             for level in range(1, 4):
                 n = 2**level
-                nxt = keep.tile([P, TILES, n, 2], F32, name=f"prob{level}")
-                nc.gpsimd.tensor_tensor(
-                    out=nxt[:],
-                    in0=prob.unsqueeze(3).to_broadcast([P, TILES, n, 2]),
-                    in1=gate[:, :, :, n - 1 : 2 * n - 1].rearrange("p s i a -> p i a s"),
-                    op=OP.mult,
-                )
-                prob = nxt[:].rearrange("p i a s -> p i (a s)")
-            return prob
+                paths = prob.unsqueeze(2).to_broadcast([P, n, 2, TILES])
+                gates = gate[:, :, n - 1 : 2 * n - 1, :].rearrange("p s a i -> p a s i")
+                if level < 3:
+                    nxt = keep.tile([P, n, 2, TILES], F32, name=f"prob{level}")
+                    nc.gpsimd.tensor_tensor(out=nxt[:], in0=paths, in1=gates, op=OP.mult)
+                    prob = nxt[:].rearrange("p a s i -> p (a s) i")
+                else:
+                    nc.gpsimd.tensor_tensor(
+                        out=leaf[:].rearrange("p c (a s) j -> p a s c j", s=2),
+                        in0=paths.rearrange("p a s (c j) -> p a s c j", j=8),
+                        in1=gates.rearrange("p a s (c j) -> p a s c j", j=8),
+                        op=OP.mult,
+                    )
 
         def spread_p(q):
-            prep[q] = prep_pool.tile([P, 512], F32, name="prep")
+            prep[q] = keep.tile([P, 4, LEAVES, 8], F32, name="prep")
             nc.scalar.copy(
-                out=prep[q][:].rearrange("p (c r) -> p c r", r=8),
-                in_=leaf[:, 4 * q : 4 * (q + 1), :].rearrange("p i l -> p (i l)").unsqueeze(2).to_broadcast([P, 64, 8]),
+                out=prep[q][:],
+                in_=leaf[:, 0, :, 4 * q : 4 * (q + 1)].rearrange("p l j -> p j l").unsqueeze(3).to_broadcast([P, 4, LEAVES, 8]),
             )
 
         def turn_p(q):
-            p_bank[q] = o_psum.tile([P, 512], F32, name="ob")
+            p_bank[q] = take_bank([P, 512], F32)
             for c in range(4):
-                cols = slice(P * c, P * (c + 1))
-                nc.tensor.transpose(p_bank[q][:, cols], prep[q][:, cols], ident[:])
+                rows = prep[q][:, c, :, :].rearrange("p l r -> p (l r)")
+                nc.tensor.transpose(p_bank[q][1][:, P * c : P * (c + 1)], rows, ident[:])
 
         def leave_p(q):
             p_sb[q] = keep.tile([P, 512], F32, name=f"p_sb{q}")
-            nc.scalar.copy(out=p_sb[q][:], in_=p_bank[q][:])
+            nc.scalar.copy(out=p_sb[q][:], in_=p_bank[q][1][:])
+            free_banks.append(p_bank[q][0])
 
         p_far = keep.tile([P, 8, 3 * P], F32, name="p_far")
 
         def park_p():
-            bank = o_psum.tile([P, 3 * P], F32, name="ob")
+            b, bank = take_bank([P, 3 * P], F32)
             for c in range(3):
-                rows = leaf[:, 8 * (c + 1) : 8 * (c + 2), :].rearrange("p i l -> p (i l)")
+                rows = leaf[:, c + 1, :, :].rearrange("p l j -> p (l j)")
                 nc.tensor.transpose(bank[:, P * c : P * (c + 1)], rows, ident[:])
             turned = keep.tile([P, 3 * P], F32, name="turned")
             nc.scalar.copy(out=turned[:], in_=bank[:])
+            free_banks.append(b)
             parked = out_v[:, TILES - 1, 0 : 3 * P]
             nc.sync.dma_start(out=parked, in_=turned[:])
+            load_x(16, 20)
             for r in range(8):
                 start = 4 * (r % 2) + r // 2
-                nc.sync.dma_start(out=p_far[start:P:8, :, :], in_=parked.rearrange("(i l) n -> l i n", l=LEAVES))
+                nc.sync.dma_start(out=p_far[start:P:8, :, :], in_=parked.rearrange("(l j) n -> l j n", j=8))
+            for a in range(20, TILES, 4):
+                load_x(a, a + 4)
 
-        def p_of(m):
-            first, n = GROUPS[m]
+        def p_of(first, n):
             if first < 8:
                 near = p_sb[first // 4][:].rearrange("p (j n) -> p j n", j=4)
                 return near[:, first % 4 : first % 4 + n, :]
-            c, i = first // 8 - 1, first % 8
-            return p_far[:, i : i + n, P * c : P * (c + 1)]
+            c, j = first // 8 - 1, first % 8
+            return p_far[:, j : j + n, P * c : P * (c + 1)]
 
         w1_c = keep.tile([P, 2, LF], U32, name="w1_c", align_bytes=64)
         w1_s = keep.tile([P, 2, LF], U8, name="w1_s", align_bytes=64)
@@ -173,7 +179,7 @@ def tile_fastfeedforwardnetwork_pa_t_kernel(tc, x_bytes, x_scale, node_logits, n
         w_bank, w_g = {}, {}
 
         def weave_w(n):
-            w_bank[n] = o_psum.tile([P, 1024], BF16, name="ob")
+            w_bank[n] = take_bank([P, 1024], BF16)
             for s in range(2):
                 if n < 4:
                     t = 2 * (n % 2) + s
@@ -182,13 +188,14 @@ def tile_fastfeedforwardnetwork_pa_t_kernel(tc, x_bytes, x_scale, node_logits, n
                     e0 = 256 * (n - 4) + P * s
                     src = w2_raw[:, :, e0 : e0 + P].rearrange("p j e -> p e j")
                 nc.tensor.matmul(
-                    out=w_bank[n][:, 512 * s : 512 * (s + 1)], lhsT=ident16[:], rhs=src, start=True, stop=True
+                    out=w_bank[n][1][:, 512 * s : 512 * (s + 1)], lhsT=ident16[:], rhs=src, start=True, stop=True
                 )
 
-        def leave_w(n):
+        def leave_w(n, tag):
             if n % 2 == 0:
-                w_g[n // 2] = keep.tile([P, 2048], BF16, name=f"w_g{n // 2}", align_bytes=64)
-            nc.scalar.copy(out=w_g[n // 2][:, 1024 * (n % 2) : 1024 * (n % 2 + 1)], in_=w_bank[n][:])
+                w_g[n // 2] = keep.tile([P, 2048], BF16, name=tag, align_bytes=64)
+            nc.scalar.copy(out=w_g[n // 2][:, 1024 * (n % 2) : 1024 * (n % 2 + 1)], in_=w_bank[n][1][:])
+            free_banks.append(w_bank[n][0])
 
         def quant_w(h):
             if h < 2:
@@ -198,323 +205,319 @@ def tile_fastfeedforwardnetwork_pa_t_kernel(tc, x_bytes, x_scale, node_logits, n
                 codes, scales = w2_c[:, cols], w2_s[:, cols]
             nc.vector.quantize_mx(out=codes.bitcast(FP8X4), scales=scales, in_=w_g[h][:])
 
-        xs, xt, xg, xq, a_bank, hp, h1, hg, hq, o_bank, o_sb = ({} for unused in range(11))
+        xs, xt, xg, xq, a_plane, a_bank, hp, h1, hg, hq, o_bank = ({} for unused in range(11))
 
         def widen(copy, first, count, pool=xs_pool, tag="xs"):
             wide = pool.tile([P, 512 * count], BF16, name=tag, align_bytes=64)
-            t, c = x8[first // 2]
-            c += 512 * (first % 2)
-            copy(out=wide[:], in_=t[:, c : c + 512 * count].bitcast(FP8))
+            copy(out=wide[:], in_=x8[:, 512 * first : 512 * (first + count)].bitcast(FP8))
             for n in range(count):
                 xs[first + n] = wide[:, 512 * n : 512 * (n + 1)]
 
-        def turn_x(i, pool=xt_psum, tag="xt"):
-            xt[i] = pool.tile([P, 2, 2, P], F32, name=tag)
+        def turn_x(i):
+            xt[i] = take_bank([P, 2, 2, P], F32)
             for g in range(2):
                 words = xs[2 * i + g].bitcast(F32)
                 for u in range(2):
-                    nc.tensor.transpose(xt[i][:, u, g, :], words[:, u:256:2], ident[:])
+                    nc.tensor.transpose(xt[i][1][:, u, g, :], words[:, u:256:2], ident[:])
 
-        def scale_x(m, j):
-            first, n = GROUPS[m]
+        def scale_x(first, n, j, tag=None):
             if j == 0:
-                xg[m] = xg_pool.tile([P, 2, n, 512], BF16, name=f"xg{m % 4}", align_bytes=64)
+                xg[first] = keep.tile([P, 2, n, 512], BF16, name=tag, align_bytes=64)
             nc.vector.tensor_tensor(
-                out=xg[m][:, :, j, :].rearrange("p g (a n u e) -> p g a n u e", n=16, u=2, e=2),
-                in0=xt[first + j][:].bitcast(BF16).rearrange("p u g (a n e) -> p g a n u e", n=16, e=2),
+                out=xg[first][:, :, j, :].rearrange("p g (a n u e) -> p g a n u e", n=16, u=2, e=2),
+                in0=xt[first + j][1][:].bitcast(BF16).rearrange("p u g (a n e) -> p g a n u e", n=16, e=2),
                 in1=scale_row[:]
                 .rearrange("p g (n u e) -> p g n u e", u=2, e=2)
                 .unsqueeze(2)
                 .to_broadcast([P, 2, 8, 16, 2, 2]),
                 op=OP.mult,
             )
+            free_banks.append(xt[first + j][0])
 
-        def quant_x(m):
-            n = GROUPS[m][1]
-            xq[m] = (
-                xq_pool.tile([P, 256 * n], U32, name="xq_c", align_bytes=64),
-                xq_pool.tile([P, 256 * n], U8, name="xq_s", align_bytes=64),
-            )
+        def quant_x(first, n):
+            codes = two.tile([P, 256 * n], U32, name="xq_c", align_bytes=64)
+            scales = two.tile([P, 256 * n], U8, name="xq_s", align_bytes=64)
             nc.vector.quantize_mx(
-                out=xq[m][0][:].bitcast(FP8X4), scales=xq[m][1][:], in_=xg[m][:].rearrange("p g j c -> p (g j c)")
+                out=codes[:].bitcast(FP8X4), scales=scales[:], in_=xg[first][:].rearrange("p g j c -> p (g j c)")
             )
+            for j in range(n):
+                xq[first + j] = (codes, scales, P * n, P * j)
 
-        def mm1(m, pool=a_psum, tag="a"):
-            n = GROUPS[m][1]
-            width = P * n
+        def mm1(first, n):
+            codes, scales, width, at = xq[first]
             for t in range(4):
-                if t % 2 == 0:
-                    bank = pool.tile([P, 512], F32, name=tag)
-                a_bank[m, t] = bank[:, t % 2 * width : (t % 2 + 1) * width]
+                if n == 4 or t % 2 == 0:
+                    a_bank[first, t], bank = take_bank([P, 512], F32)
+                    used = 0
+                a_plane[first, t] = bank[:, used : used + P * n]
+                used += P * n
                 for g in range(2):
+                    cols = slice(width * g + at, width * g + at + P * n)
                     nc.tensor.matmul_mx(
-                        out=a_bank[m, t],
+                        out=a_plane[first, t],
                         lhsT=w1_c[:, g, P * t : P * (t + 1)].bitcast(FP8X4),
                         lhsT_scale=w1_s[:, g, P * t : P * (t + 1)],
-                        rhs=xq[m][0][:, width * g : width * (g + 1)].bitcast(FP8X4),
-                        rhs_scale=xq[m][1][:, width * g : width * (g + 1)],
+                        rhs=codes[:, cols].bitcast(FP8X4),
+                        rhs_scale=scales[:, cols],
                         start=(g == 0),
                         stop=(g == 1),
                     )
 
-        def weigh_h(m):
-            n = GROUPS[m][1]
-            hp[m] = h_pool.tile([P, 4, P * n], BF16, name="hp", align_bytes=64)
+        def plane_read(first, n, t):
+            if n == 4:
+                free_banks.append(a_bank[first, t])
+            elif t % 2 == 1:
+                free_banks.append(a_bank[first, t - 1])
+
+        def weigh_h(first, n):
+            hp[first] = two.tile([P, 4, P * n], BF16, name="hp", align_bytes=64)
             for t in range(4):
                 nc.vector.scalar_tensor_tensor(
-                    out=hp[m][:, t, :].rearrange("p (j n) -> p j n", j=n),
-                    in0=a_bank[m, t].rearrange("p (j n) -> p j n", j=n),
+                    out=hp[first][:, t, :].rearrange("p (j n) -> p j n", j=n),
+                    in0=a_plane[first, t].rearrange("p (j n) -> p j n", j=n),
                     scalar=bias_h[:, t : t + 1],
-                    in1=p_of(m),
+                    in1=p_of(first, n),
                     op0=OP.add,
                     op1=OP.mult,
                 )
+                plane_read(first, n, t)
 
-        def relu_h(engine, m, pool=hg_pool, tag="hg"):
-            hg[m] = pool.tile([P, 512 * GROUPS[m][1]], BF16, name=tag, align_bytes=64)
+        def relu_h(engine, first, n, tag):
+            hg[first] = keep.tile([P, 512 * n], BF16, name=tag, align_bytes=64)
             engine.tensor_scalar(
-                out=hg[m][:].rearrange("p (n t) -> p n t", t=4),
-                in0=hp[m][:].rearrange("p t n -> p n t"),
+                out=hg[first][:].rearrange("p (n t) -> p n t", t=4),
+                in0=hp[first][:].rearrange("p t n -> p n t"),
                 scalar1=BF16_MAX,
                 scalar2=0.0,
                 op0=OP.min,
                 op1=OP.max,
             )
 
-        def relu_on_scalar(m):
-            hg[m] = hg_pool.tile([P, 512 * GROUPS[m][1]], BF16, name="hg", align_bytes=64)
+        def relu_on_scalar(first, n):
+            hg[first] = keep.tile([P, 512 * n], BF16, name=f"hg{first // 2 % 2}", align_bytes=64)
             nc.scalar.activation(
-                out=hg[m][:].rearrange("p (n t) -> p n t", t=4), in_=hp[m][:].rearrange("p t n -> p n t"), func=ACT.Relu
+                out=hg[first][:].rearrange("p (n t) -> p n t", t=4),
+                in_=hp[first][:].rearrange("p t n -> p n t"),
+                func=ACT.Relu,
             )
 
-        def leave_h(m):
-            h1[m] = h1_pool.tile([P, 4, P * GROUPS[m][1]], F32, name="h1")
+        def leave_h(first, n=2):
+            h1[first] = keep.tile([P, 4, P * n], F32, name="h1")
             for t in range(4):
-                nc.scalar.activation(out=h1[m][:, t, :], in_=a_bank[m, t], func=ACT.Relu, bias=bias_h[:, t : t + 1])
+                nc.scalar.activation(
+                    out=h1[first][:, t, :], in_=a_plane[first, t], func=ACT.Relu, bias=bias_h[:, t : t + 1]
+                )
+                plane_read(first, n, t)
 
-        def weigh_on_gpsimd(m, pool, tag):
-            n = GROUPS[m][1]
-            hg[m] = pool.tile([P, 512 * n], BF16, name=tag, align_bytes=64)
+        def weigh_on_gpsimd(first, tag, pool, n=2):
+            hg[first] = pool.tile([P, 512 * n], BF16, name=tag, align_bytes=64)
             nc.gpsimd.tensor_tensor(
-                out=hg[m][:].rearrange("p (j n t) -> p j n t", j=n, t=4),
-                in0=h1[m][:].rearrange("p t (j n) -> p j n t", j=n),
-                in1=p_of(m).unsqueeze(3).to_broadcast([P, n, P, 4]),
+                out=hg[first][:].rearrange("p (j n t) -> p j n t", j=n, t=4),
+                in0=h1[first][:].rearrange("p t (j n) -> p j n t", j=n),
+                in1=p_of(first, n).unsqueeze(3).to_broadcast([P, n, P, 4]),
                 op=OP.mult,
             )
 
-        def quant_h(m):
-            n = GROUPS[m][1]
-            hq[m] = (
-                hq_pool.tile([P, P * n], U32, name="hq_c", align_bytes=64),
-                hq_pool.tile([P, P * n], U8, name="hq_s", align_bytes=64),
-            )
-            nc.vector.quantize_mx(out=hq[m][0][:].bitcast(FP8X4), scales=hq[m][1][:], in_=hg[m][:])
+        def quant_h(first, n):
+            codes = hq_pool.tile([P, P * n], U32, name="hq_c", align_bytes=64)
+            scales = hq_pool.tile([P, P * n], U8, name="hq_s", align_bytes=64)
+            nc.vector.quantize_mx(out=codes[:].bitcast(FP8X4), scales=scales[:], in_=hg[first][:])
+            for j in range(n):
+                hq[first + j] = (codes[:, P * j : P * (j + 1)], scales[:, P * j : P * (j + 1)])
 
-        def mm2(m, j, pool=o_psum, tag="ob"):
+        def mm2(i):
             for e in range(2):
-                o_bank[m, j, e] = pool.tile([P, 512], F32, name=tag)
+                o_bank[i, e] = take_bank([P, 512], F32)
                 nc.tensor.matmul_mx(
-                    out=o_bank[m, j, e][:],
-                    lhsT=hq[m][0][:, P * j : P * (j + 1)].bitcast(FP8X4),
-                    lhsT_scale=hq[m][1][:, P * j : P * (j + 1)],
+                    out=o_bank[i, e][1][:],
+                    lhsT=hq[i][0].bitcast(FP8X4),
+                    lhsT_scale=hq[i][1],
                     rhs=w2_c[:, 512 * e : 512 * (e + 1)].bitcast(FP8X4),
                     rhs_scale=w2_s[:, 512 * e : 512 * (e + 1)],
                     start=True,
                     stop=True,
                 )
 
-        def leave_o(m, j, copies=(nc.scalar.copy, nc.scalar.copy), halves=False):
-            i = GROUPS[m][0] + j
-            o_sb[i] = o_pool.tile([P, E], F32, name="osb")
+        def leave_o(i, copies=(nc.scalar.copy, nc.scalar.copy), halves=False):
+            o_sb = o_pool.tile([P, E], F32, name="osb")
             for e in range(2):
                 cols = slice(512 * e, 512 * (e + 1))
-                copies[e](out=o_sb[i][:, cols], in_=o_bank[m, j, e][:])
+                copies[e](out=o_sb[:, cols], in_=o_bank[i, e][1][:])
+                free_banks.append(o_bank[i, e][0])
                 if halves:
-                    nc.sync.dma_start(out=out_v[:, i, cols], in_=o_sb[i][:, cols])
+                    nc.sync.dma_start(out=out_v[:, i, cols], in_=o_sb[:, cols])
             if not halves:
-                nc.sync.dma_start(out=out_v[:, i, :], in_=o_sb[i][:])
+                nc.sync.dma_start(out=out_v[:, i, :], in_=o_sb[:])
 
-        def gpsimd_halves(k):
-            free = k >= 5 and GROUPS[k][1] == 2 and k - 2 not in SHARED and k - 1 not in SHARED
-            return 2 if free else 0
+        left = list(range(2 * TILES))
 
-        taken = [2 * GROUPS[k][0] + 8 + n for k in range(len(GROUPS)) for n in range(gpsimd_halves(k))]
-        left = [h for h in range(20, 2 * TILES) if h not in taken and not 24 <= h < 28]
+        def cast(copy, count, pool=xs_pool, tag="xs"):
+            first, count = left[0], min(count, len(left))
+            widen(copy, first, count, pool, tag)
+            for h in range(first, first + count):
+                left.remove(h)
 
-        def scalar_casts(count):
-            while count > 0 and left:
-                run = 2 if left[0] % 2 == 0 else 1
-                widen(nc.scalar.copy, left[0], run)
-                for n in range(run):
-                    left.remove(left[0])
-                count -= run
+        def outputs(tiles):
+            for i in tiles:
+                mm2(i)
+                leave_o(i)
 
         scale_row = keep.tile([P, 2, 64], F32, name="scale_row")
-        widen(nc.vector.tensor_copy, 0, 2)
+        cast(nc.vector.tensor_copy, 2)
         turn_x(0)
         gates_sum()
         nc.vector.tensor_copy(
             out=scale_row[:].rearrange("p g (n t) -> p g n t", t=4),
             in_=scale[:].unsqueeze(2).to_broadcast([P, 2, 16, 4]),
         )
-        widen(nc.vector.tensor_copy, 2, 2)
+        cast(nc.vector.tensor_copy, 2)
         turn_x(1)
-        widen(nc.gpsimd.tensor_copy, 4, 2, keep, "xs2")
-        turn_x(2, a_psum, "a")
+        cast(nc.gpsimd.tensor_copy, 2)
+        turn_x(2)
         gates_sigmoid()
-        for i in range(3, 7):
-            widen(nc.scalar.copy, 2 * i, 2)
-        leaf = leaf_probabilities()
-        turn_x(3, a_psum, "a")
-        scale_x(0, 0)
-        scale_x(0, 1)
+        cast(nc.scalar.copy, 2)
+        cast(nc.scalar.copy, 2)
+        leaf_probabilities()
+        turn_x(3)
+        scale_x(0, 4, 0, "xg0")
+        turn_x(4)
         weave_w(0)
         weave_w(1)
-        turn_x(4)
-        turn_x(5)
-        leave_w(0)
+        scale_x(0, 4, 1)
+        cast(nc.scalar.copy, 2)
         spread_p(0)
-        leave_w(1)
+        leave_w(0, "xg2")
+        leave_w(1, "xg2")
+        scale_x(0, 4, 2)
+        turn_x(5)
         weave_w(2)
         weave_w(3)
-        widen(nc.scalar.copy, 16, 2)
-        leave_w(2)
-        leave_w(3)
-        scale_x(1, 0)
-        scale_x(1, 1)
-        quant_x(0)
-        widen(nc.gpsimd.tensor_copy, 14, 2, xg_pool, "xg0")
-        scale_x(2, 0)
+        scale_x(0, 4, 3)
+        scale_x(4, 4, 0, "xg1")
+        quant_x(0, 4)
+        quant_w(0)
+        cast(nc.scalar.copy, 2)
+        leave_w(2, "xg3")
+        leave_w(3, "xg3")
+        scale_x(4, 4, 1)
+        cast(nc.vector.tensor_copy, 2)
+        quant_w(1)
         turn_x(6)
         park_p()
         turn_p(0)
         leave_p(0)
-        scale_x(2, 1)
         turn_x(7)
-        weave_w(4)
-        widen(nc.scalar.copy, 18, 2)
-        leave_w(4)
+        mm1(0, 4)
+        cast(nc.scalar.copy, 2)
+        cast(nc.scalar.copy, 2)
+        cast(nc.gpsimd.tensor_copy, 5, keep, "xg3")
+        scale_x(4, 4, 2)
+        weigh_h(0, 4)
+        relu_h(nc.gpsimd, 0, 4, "xg0")
         spread_p(1)
-        quant_w(0)
-        quant_x(1)
-        quant_w(1)
-        widen(nc.gpsimd.tensor_copy, 24, 4, keep, "w_g1")
-        mm1(0)
-        mm1(1, o_psum, "ob")
-        scale_x(3, 0)
-        weave_w(5)
-        weave_w(6)
-        scalar_casts(4)
-        leave_w(5)
-        leave_w(6)
-        weigh_h(0)
-        relu_h(nc.gpsimd, 0)
-        weigh_h(1)
-        weave_w(7)
-        leave_w(7)
         turn_x(8)
-        turn_p(1)
-        scalar_casts(2)
-        leave_p(1)
-        scalar_casts(4)
-        scale_x(3, 1)
         turn_x(9)
-        quant_x(2)
-        quant_x(3)
+        scale_x(4, 4, 3)
+        cast(nc.scalar.copy, 1)
+        cast(nc.scalar.copy, 2)
+        for n in range(4, 8):
+            weave_w(n)
+            leave_w(n, "w_g2" if n < 6 else "xg4")
+            if n == 5:
+                scale_x(8, 2, 0, "xg2")
+        turn_p(1)
+        turn_x(10)
+        turn_x(11)
+        leave_p(1)
+        cast(nc.scalar.copy, 2)
+        scale_x(8, 2, 1)
+        quant_x(4, 4)
         quant_w(2)
         quant_w(3)
-        quant_h(0)
-        mm1(2)
-        mm2(0, 0)
-        leave_o(0, 0)
-        relu_h(nc.gpsimd, 1, keep, "w_g3")
-        scalar_casts(2)
-        scale_x(4, 0)
-        turn_x(10)
-        weigh_h(2)
-        mm1(3)
-        relu_h(nc.gpsimd, 2)
-        scale_x(4, 1)
-        turn_x(11)
-        mm2(0, 1)
-        leave_o(0, 1)
-        scalar_casts(4)
-        weigh_h(3)
-        quant_x(4)
-        quant_h(1)
-        quant_h(2)
-        end = len(GROUPS) - 1
-        for k in range(5, end):
+        quant_h(0, 4)
+        quant_x(8, 2)
+        mm1(4, 4)
+        cast(nc.gpsimd.tensor_copy, 3, keep, "xg2")
+        weigh_h(4, 4)
+        relu_h(nc.gpsimd, 4, 4, "xg1")
+        cast(nc.scalar.copy, 1)
+        cast(nc.scalar.copy, 2)
+        outputs([0])
+        mm1(8, 2)
+        scale_x(10, 2, 0, "xg6")
+        outputs([1])
+        cast(nc.scalar.copy, 2)
+        weigh_h(8, 2)
+        turn_x(12)
+        turn_x(13)
+        outputs([2])
+        relu_on_scalar(8, 2)
+        scale_x(10, 2, 1)
+        outputs([3])
+        quant_x(10, 2)
+        quant_h(4, 4)
+
+        ready = [4, 5, 6, 7]
+        for k in range(6, len(GROUPS) - 1):
             first, count = GROUPS[k]
-            gate_tag = f"xg{(k - 1) % 4}"
+            before, older = GROUPS[k - 1], GROUPS[k - 2]
+            gate_tag = f"xg{k % 8}"
             short = k - 1 in SHARED
-            if short:
-                mm1(k - 1, o_psum, "ob")
-                leave_h(k - 1)
-            else:
-                mm1(k - 1)
-            if k == 5:
-                mm2(1, 0)
-                leave_o(1, 0)
-                mm2(1, 1)
-                leave_o(1, 1)
+            mm1(*before)
+            on_gpsimd = k - 2 in SHARED or not left
             if k - 2 in SHARED:
-                weigh_on_gpsimd(k - 2, xg_pool, f"xg{(k - 2) % 4}")
-            elif gpsimd_halves(k):
-                widen(nc.gpsimd.tensor_copy, 2 * first + 8, gpsimd_halves(k), xg_pool, gate_tag)
-                relu_h(nc.gpsimd, k - 2)
+                weigh_on_gpsimd(older[0], f"hg{(k - 3) % 2}", keep)
+            elif left:
+                cast(nc.gpsimd.tensor_copy, SHORT_HALVES if short else LONG_HALVES, keep, gate_tag)
             else:
-                relu_h(nc.gpsimd, k - 2, xg_pool, gate_tag)
-            early = short or k == 5
-            for j in range(2):
-                if j < count:
-                    scale_x(k, j)
-                if early and j < count and first + j + 2 < TILES:
-                    turn_x(first + j + 2)
-                if not early and count == 2 and j == 1:
-                    turn_x(first + 2)
-                    turn_x(first + 3)
-                if j < GROUPS[k - 3][1]:
-                    mm2(k - 3, j)
-                    leave_o(k - 3, j)
-                if j == 0 and not early:
-                    scalar_casts(2 if k in SHARED else CASTS)
-                if not early and count == 1 and j == 0 and first + 2 < TILES:
-                    turn_x(first + 2)
+                relu_h(nc.gpsimd, *older, gate_tag)
+            scale_x(first, count, 0, f"xg{(k + 1) % 8}")
+            if not on_gpsimd and older[0] not in hg:
+                relu_on_scalar(*older)
+            if left and k in SCALAR_CASTS:
+                cast(nc.scalar.copy, 2)
             if short:
-                scalar_casts(2)
-                quant_h(k - 2)
-                quant_x(k)
+                leave_h(before[0])
+            half = (len(ready) + 1) // 2
+            outputs(ready[:half])
+            for i in range(first + 2, min(first + 2 + count, TILES)):
+                turn_x(i)
+            if count == 2:
+                scale_x(first, count, 1)
+            if not short:
+                weigh_h(*before)
+            outputs(ready[half:])
+            if short:
+                quant_h(*older)
+                quant_x(first, count)
             else:
-                weigh_h(k - 1)
-                quant_x(k)
-                quant_h(k - 2)
-        mm1(end - 1)
-        relu_h(nc.gpsimd, end - 2, xg_pool, f"xg{(end - 1) % 4}")
-        mm2(end - 3, 0)
-        leave_o(end - 3, 0)
-        scale_x(end, 0)
-        quant_h(end - 2)
-        mm2(end - 2, 0)
-        leave_o(end - 2, 0)
-        weigh_h(end - 1)
-        quant_x(end)
-        relu_h(nc.vector, end - 1)
-        mm1(end)
-        quant_h(end - 1)
-        weigh_h(end)
-        relu_h(nc.vector, end)
-        mm2(end - 1, 0)
-        leave_o(end - 1, 0, halves=True)
-        quant_h(end)
+                quant_x(first, count)
+                quant_h(*older)
+            ready = list(range(older[0], older[0] + older[1]))
+        mm1(30, 1)
+        relu_h(nc.gpsimd, 29, 1, "xg1")
+        outputs([28])
+        scale_x(31, 1, 0, "xg2")
+        quant_h(29, 1)
+        outputs([29])
+        weigh_h(30, 1)
+        quant_x(31, 1)
+        relu_h(nc.vector, 30, 1, "xg3")
+        mm1(31, 1)
+        quant_h(30, 1)
+        weigh_h(31, 1)
+        relu_h(nc.vector, 31, 1, "xg4")
+        mm2(30)
+        leave_o(30, halves=True)
+        quant_h(31, 1)
         last = o_pool.tile([P, E], F32, name="osb")
         for e in range(4):
             cols = slice(256 * e, 256 * (e + 1))
-            bank = xt_psum.tile([P, 256], F32, name="xt") if e < 2 else a_psum.tile([P, 256], F32, name="a")
+            b, bank = take_bank([P, 256], F32)
             nc.tensor.matmul_mx(
                 out=bank[:],
-                lhsT=hq[end][0][:].bitcast(FP8X4),
-                lhsT_scale=hq[end][1][:],
+                lhsT=hq[31][0].bitcast(FP8X4),
+                lhsT_scale=hq[31][1],
                 rhs=w2_c[:, cols].bitcast(FP8X4),
                 rhs_scale=w2_s[:, cols],
                 start=True,

@@ -26,7 +26,6 @@ GROUPS = [(2 * k, 2) for k in range(14)] + [(i, 1) for i in range(28, TILES)]
 SHARED = (7, 9, 11)
 LONG_HALVES = 5
 SHORT_HALVES = 3
-SCALAR_CASTS = (11, 13)
 
 
 def tile_fastfeedforwardnetwork_pa_t_kernel(tc, x_bytes, x_scale, node_logits, node_b, w1, b1, w2, out):
@@ -40,7 +39,7 @@ def tile_fastfeedforwardnetwork_pa_t_kernel(tc, x_bytes, x_scale, node_logits, n
 
     with ExitStack() as ctx:
         keep = ctx.enter_context(tc.tile_pool(name="keep", bufs=1))
-        xs_pool = ctx.enter_context(tc.tile_pool(name="xs", bufs=10))
+        xs_pool = ctx.enter_context(tc.tile_pool(name="xs", bufs=12))
         two = ctx.enter_context(tc.tile_pool(name="two", bufs=2))
         hq_pool = ctx.enter_context(tc.tile_pool(name="hq", bufs=3))
         o_pool = ctx.enter_context(tc.tile_pool(name="o", bufs=8))
@@ -87,6 +86,7 @@ def tile_fastfeedforwardnetwork_pa_t_kernel(tc, x_bytes, x_scale, node_logits, n
         w2_raw = keep.tile([P, 4, E], BF16, name="w2_raw")
         nc.sync.dma_start(out=w2_raw[:], in_=w2_v)
         load_x(12, 16)
+        load_x(16, 20)
 
         ident = keep.tile([P, P], F32, name="ident")
         make_identity(nc, ident[:])
@@ -100,9 +100,9 @@ def tile_fastfeedforwardnetwork_pa_t_kernel(tc, x_bytes, x_scale, node_logits, n
 
         def gates_sum():
             nc.vector.tensor_tensor(
-                out=z[:],
-                in0=logits[:].rearrange("p (i v) -> p v i", v=NODES),
-                in1=bias_n[:].unsqueeze(2).to_broadcast([P, NODES, TILES]),
+                out=z[:].rearrange("p v (c j) -> p v c j", c=4),
+                in0=logits[:].rearrange("p (j c v) -> p v c j", c=4, v=NODES),
+                in1=bias_n[:].unsqueeze(2).unsqueeze(3).to_broadcast([P, NODES, 4, 8]),
                 op=OP.add,
             )
 
@@ -123,8 +123,8 @@ def tile_fastfeedforwardnetwork_pa_t_kernel(tc, x_bytes, x_scale, node_logits, n
                 else:
                     nc.gpsimd.tensor_tensor(
                         out=leaf[:].rearrange("p c (a s) j -> p a s c j", s=2),
-                        in0=paths.rearrange("p a s (c j) -> p a s c j", j=8),
-                        in1=gates.rearrange("p a s (c j) -> p a s c j", j=8),
+                        in0=paths.rearrange("p a s (c j) -> p a s c j", c=4),
+                        in1=gates.rearrange("p a s (c j) -> p a s c j", c=4),
                         op=OP.mult,
                     )
 
@@ -132,7 +132,7 @@ def tile_fastfeedforwardnetwork_pa_t_kernel(tc, x_bytes, x_scale, node_logits, n
             prep[q] = keep.tile([P, 4, LEAVES, 8], F32, name="prep")
             nc.scalar.copy(
                 out=prep[q][:],
-                in_=leaf[:, 0, :, 4 * q : 4 * (q + 1)].rearrange("p l j -> p j l").unsqueeze(3).to_broadcast([P, 4, LEAVES, 8]),
+                in_=leaf[:, :, :, q].unsqueeze(3).to_broadcast([P, 4, LEAVES, 8]),
             )
 
         def turn_p(q):
@@ -146,31 +146,30 @@ def tile_fastfeedforwardnetwork_pa_t_kernel(tc, x_bytes, x_scale, node_logits, n
             nc.scalar.copy(out=p_sb[q][:], in_=p_bank[q][1][:])
             free_banks.append(p_bank[q][0])
 
-        p_far = keep.tile([P, 8, 3 * P], F32, name="p_far")
+        p_far = keep.tile([P, 7, 4 * P], F32, name="p_far")
 
         def park_p():
-            b, bank = take_bank([P, 3 * P], F32)
-            for c in range(3):
-                rows = leaf[:, c + 1, :, :].rearrange("p l j -> p (l j)")
+            b, bank = take_bank([P, 4 * P], F32)
+            for c in range(4):
+                rows = leaf[:, c, :, :].rearrange("p l j -> p (l j)")
                 nc.tensor.transpose(bank[:, P * c : P * (c + 1)], rows, ident[:])
-            turned = keep.tile([P, 3 * P], F32, name="turned")
+            turned = keep.tile([P, 4 * P], F32, name="turned")
             nc.scalar.copy(out=turned[:], in_=bank[:])
             free_banks.append(b)
-            parked = out_v[:, TILES - 1, 0 : 3 * P]
+            parked = out_v[:, TILES - 1, 0 : 4 * P]
             nc.sync.dma_start(out=parked, in_=turned[:])
-            load_x(16, 20)
-            for r in range(8):
-                start = 4 * (r % 2) + r // 2
-                nc.sync.dma_start(out=p_far[start:P:8, :, :], in_=parked.rearrange("(l j) n -> l j n", j=8))
-            for a in range(20, TILES, 4):
+            load_x(20, 24)
+            rows = parked.rearrange("(l j) n -> l j n", j=8)
+            for a, b in ((1, 3), (3, 8)):
+                for r in range(8):
+                    start = 4 * (r % 2) + r // 2
+                    nc.sync.dma_start(out=p_far[start:P:8, a - 1 : b - 1, :], in_=rows[:, a:b, :])
+            for a in range(24, TILES, 4):
                 load_x(a, a + 4)
 
         def p_of(first, n):
-            if first < 8:
-                near = p_sb[first // 4][:].rearrange("p (j n) -> p j n", j=4)
-                return near[:, first % 4 : first % 4 + n, :]
-            c, j = first // 8 - 1, first % 8
-            return p_far[:, j : j + n, P * c : P * (c + 1)]
+            row = p_sb[0][:] if first < 4 else p_far[:, first // 4 - 1, :]
+            return row[:, P * (first % 4) : P * (first % 4 + n)]
 
         w1_c = keep.tile([P, 2, LF], U32, name="w1_c", align_bytes=64)
         w1_s = keep.tile([P, 2, LF], U8, name="w1_s", align_bytes=64)
@@ -273,8 +272,8 @@ def tile_fastfeedforwardnetwork_pa_t_kernel(tc, x_bytes, x_scale, node_logits, n
             hp[first] = two.tile([P, 4, P * n], BF16, name="hp", align_bytes=64)
             for t in range(4):
                 nc.vector.scalar_tensor_tensor(
-                    out=hp[first][:, t, :].rearrange("p (j n) -> p j n", j=n),
-                    in0=a_plane[first, t].rearrange("p (j n) -> p j n", j=n),
+                    out=hp[first][:, t, :],
+                    in0=a_plane[first, t],
                     scalar=bias_h[:, t : t + 1],
                     in1=p_of(first, n),
                     op0=OP.add,
@@ -282,11 +281,11 @@ def tile_fastfeedforwardnetwork_pa_t_kernel(tc, x_bytes, x_scale, node_logits, n
                 )
                 plane_read(first, n, t)
 
-        def relu_h(engine, first, n, tag):
+        def relu_h(engine, first, n, tag, run=1):
             hg[first] = keep.tile([P, 512 * n], BF16, name=tag, align_bytes=64)
             engine.tensor_scalar(
-                out=hg[first][:].rearrange("p (n t) -> p n t", t=4),
-                in0=hp[first][:].rearrange("p t n -> p n t"),
+                out=hg[first][:].rearrange("p (c i t) -> p c t i", i=run, t=4),
+                in0=hp[first][:].rearrange("p t (c i) -> p c t i", i=run),
                 scalar1=BF16_MAX,
                 scalar2=0.0,
                 op0=OP.min,
@@ -296,8 +295,8 @@ def tile_fastfeedforwardnetwork_pa_t_kernel(tc, x_bytes, x_scale, node_logits, n
         def relu_on_scalar(first, n):
             hg[first] = keep.tile([P, 512 * n], BF16, name=f"hg{first // 2 % 2}", align_bytes=64)
             nc.scalar.activation(
-                out=hg[first][:].rearrange("p (n t) -> p n t", t=4),
-                in_=hp[first][:].rearrange("p t n -> p n t"),
+                out=hg[first][:].rearrange("p (c i t) -> p c t i", i=4, t=4),
+                in_=hp[first][:].rearrange("p t (c i) -> p c t i", i=4),
                 func=ACT.Relu,
             )
 
@@ -312,9 +311,9 @@ def tile_fastfeedforwardnetwork_pa_t_kernel(tc, x_bytes, x_scale, node_logits, n
         def weigh_on_gpsimd(first, tag, pool, n=2):
             hg[first] = pool.tile([P, 512 * n], BF16, name=tag, align_bytes=64)
             nc.gpsimd.tensor_tensor(
-                out=hg[first][:].rearrange("p (j n t) -> p j n t", j=n, t=4),
-                in0=h1[first][:].rearrange("p t (j n) -> p j n t", j=n),
-                in1=p_of(first, n).unsqueeze(3).to_broadcast([P, n, P, 4]),
+                out=hg[first][:].rearrange("p (n t) -> p n t", t=4),
+                in0=h1[first][:].rearrange("p t n -> p n t"),
+                in1=p_of(first, n).unsqueeze(2).to_broadcast([P, P * n, 4]),
                 op=OP.mult,
             )
 
@@ -414,7 +413,6 @@ def tile_fastfeedforwardnetwork_pa_t_kernel(tc, x_bytes, x_scale, node_logits, n
         scale_x(4, 4, 2)
         weigh_h(0, 4)
         relu_h(nc.gpsimd, 0, 4, "xg0")
-        spread_p(1)
         turn_x(8)
         turn_x(9)
         scale_x(4, 4, 3)
@@ -425,10 +423,9 @@ def tile_fastfeedforwardnetwork_pa_t_kernel(tc, x_bytes, x_scale, node_logits, n
             leave_w(n, "w_g2" if n < 6 else "xg4")
             if n == 5:
                 scale_x(8, 2, 0, "xg2")
-        turn_p(1)
+                cast(nc.scalar.copy, 2)
         turn_x(10)
         turn_x(11)
-        leave_p(1)
         cast(nc.scalar.copy, 2)
         scale_x(8, 2, 1)
         quant_x(4, 4)
@@ -443,6 +440,7 @@ def tile_fastfeedforwardnetwork_pa_t_kernel(tc, x_bytes, x_scale, node_logits, n
         cast(nc.scalar.copy, 1)
         cast(nc.scalar.copy, 2)
         outputs([0])
+        cast(nc.scalar.copy, 2)
         mm1(8, 2)
         scale_x(10, 2, 0, "xg6")
         outputs([1])
@@ -474,8 +472,6 @@ def tile_fastfeedforwardnetwork_pa_t_kernel(tc, x_bytes, x_scale, node_logits, n
             scale_x(first, count, 0, f"xg{(k + 1) % 8}")
             if not on_gpsimd and older[0] not in hg:
                 relu_on_scalar(*older)
-            if left and k in SCALAR_CASTS:
-                cast(nc.scalar.copy, 2)
             if short:
                 leave_h(before[0])
             half = (len(ready) + 1) // 2
@@ -502,11 +498,11 @@ def tile_fastfeedforwardnetwork_pa_t_kernel(tc, x_bytes, x_scale, node_logits, n
         outputs([29])
         weigh_h(30, 1)
         quant_x(31, 1)
-        relu_h(nc.vector, 30, 1, "xg3")
+        relu_h(nc.vector, 30, 1, "xg3", 4)
         mm1(31, 1)
         quant_h(30, 1)
         weigh_h(31, 1)
-        relu_h(nc.vector, 31, 1, "xg4")
+        relu_h(nc.vector, 31, 1, "xg4", 4)
         mm2(30)
         leave_o(30, halves=True)
         quant_h(31, 1)

@@ -23,9 +23,8 @@ TILES = TOKENS // P
 FLOPS = 2 * TOKENS * D * LF + 2 * TOKENS * LF * E
 BF16_MAX = 3.3895313892515355e38
 GROUPS = [(2 * k, 2) for k in range(14)] + [(i, 1) for i in range(28, TILES)]
-SHARED = (7, 9, 11)
-LONG_HALVES = 5
-SHORT_HALVES = 3
+SHARED = (7, 10)
+SCALAR_CASTS = {6: (1, 0), 7: (1, 1), 9: (1, 1), 12: (1, 1)}
 
 
 def tile_fastfeedforwardnetwork_pa_t_kernel(tc, x_bytes, x_scale, node_logits, node_b, w1, b1, w2, out):
@@ -292,14 +291,6 @@ def tile_fastfeedforwardnetwork_pa_t_kernel(tc, x_bytes, x_scale, node_logits, n
                 op1=OP.max,
             )
 
-        def relu_on_scalar(first, n):
-            hg[first] = keep.tile([P, 512 * n], BF16, name=f"hg{first // 2 % 2}", align_bytes=64)
-            nc.scalar.activation(
-                out=hg[first][:].rearrange("p (c i t) -> p c t i", i=4, t=4),
-                in_=hp[first][:].rearrange("p t (c i) -> p c t i", i=4),
-                func=ACT.Relu,
-            )
-
         def leave_h(first, n=2):
             h1[first] = keep.tile([P, 4, P * n], F32, name="h1")
             for t in range(4):
@@ -423,9 +414,10 @@ def tile_fastfeedforwardnetwork_pa_t_kernel(tc, x_bytes, x_scale, node_logits, n
             leave_w(n, "w_g2" if n < 6 else "xg4")
             if n == 5:
                 scale_x(8, 2, 0, "xg2")
-                cast(nc.scalar.copy, 2)
+                cast(nc.scalar.copy, 1)
         turn_x(10)
         turn_x(11)
+        cast(nc.scalar.copy, 1)
         cast(nc.scalar.copy, 2)
         scale_x(8, 2, 1)
         quant_x(4, 4)
@@ -445,12 +437,11 @@ def tile_fastfeedforwardnetwork_pa_t_kernel(tc, x_bytes, x_scale, node_logits, n
         scale_x(10, 2, 0, "xg6")
         outputs([1])
         cast(nc.scalar.copy, 2)
-        weigh_h(8, 2)
+        scale_x(10, 2, 1)
         turn_x(12)
         turn_x(13)
         outputs([2])
-        relu_on_scalar(8, 2)
-        scale_x(10, 2, 1)
+        weigh_h(8, 2)
         outputs([3])
         quant_x(10, 2)
         quant_h(4, 4)
@@ -462,20 +453,23 @@ def tile_fastfeedforwardnetwork_pa_t_kernel(tc, x_bytes, x_scale, node_logits, n
             gate_tag = f"xg{k % 8}"
             short = k - 1 in SHARED
             mm1(*before)
-            on_gpsimd = k - 2 in SHARED or not left
             if k - 2 in SHARED:
                 weigh_on_gpsimd(older[0], f"hg{(k - 3) % 2}", keep)
-            elif left:
-                cast(nc.gpsimd.tensor_copy, SHORT_HALVES if short else LONG_HALVES, keep, gate_tag)
+            elif left and not short:
+                cast(nc.gpsimd.tensor_copy, 2, keep, gate_tag)
+                relu_h(nc.gpsimd, *older, f"hg{k % 2}")
             else:
                 relu_h(nc.gpsimd, *older, gate_tag)
             scale_x(first, count, 0, f"xg{(k + 1) % 8}")
-            if not on_gpsimd and older[0] not in hg:
-                relu_on_scalar(*older)
             if short:
                 leave_h(before[0])
             half = (len(ready) + 1) // 2
+            early, late = SCALAR_CASTS.get(k, (0, 0))
+            for n in range(early):
+                cast(nc.scalar.copy, 2)
             outputs(ready[:half])
+            for n in range(late):
+                cast(nc.scalar.copy, 2)
             for i in range(first + 2, min(first + 2 + count, TILES)):
                 turn_x(i)
             if count == 2:
@@ -495,11 +489,11 @@ def tile_fastfeedforwardnetwork_pa_t_kernel(tc, x_bytes, x_scale, node_logits, n
         outputs([28])
         scale_x(31, 1, 0, "xg2")
         quant_h(29, 1)
-        outputs([29])
-        weigh_h(30, 1)
         quant_x(31, 1)
-        relu_h(nc.vector, 30, 1, "xg3", 4)
+        weigh_h(30, 1)
+        outputs([29])
         mm1(31, 1)
+        relu_h(nc.vector, 30, 1, "xg3", 4)
         quant_h(30, 1)
         weigh_h(31, 1)
         relu_h(nc.vector, 31, 1, "xg4", 4)

@@ -23,8 +23,8 @@ TILES = TOKENS // P
 FLOPS = 2 * TOKENS * D * LF + 2 * TOKENS * LF * E
 BF16_MAX = 3.3895313892515355e38
 GROUPS = [(2 * k, 2) for k in range(14)] + [(i, 1) for i in range(28, TILES)]
-SHARED = (7, 10)
-SCALAR_CASTS = {6: (1, 0), 7: (1, 1), 9: (1, 1), 12: (1, 1)}
+SHARED = (7, 9, 11)
+SCALAR_CASTS = {6: (1, 0), 7: (1, 1), 9: (1, 1), 11: (1, 1), 13: (1, 1)}
 
 
 def tile_fastfeedforwardnetwork_pa_t_kernel(tc, x_bytes, x_scale, node_logits, node_b, w1, b1, w2, out):
@@ -454,7 +454,7 @@ def tile_fastfeedforwardnetwork_pa_t_kernel(tc, x_bytes, x_scale, node_logits, n
             short = k - 1 in SHARED
             mm1(*before)
             if k - 2 in SHARED:
-                weigh_on_gpsimd(older[0], f"hg{(k - 3) % 2}", keep)
+                weigh_on_gpsimd(older[0], f"xg{(k - 1) % 8}", keep)
             elif left and not short:
                 cast(nc.gpsimd.tensor_copy, 2, keep, gate_tag)
                 relu_h(nc.gpsimd, *older, f"hg{k % 2}")
@@ -489,11 +489,11 @@ def tile_fastfeedforwardnetwork_pa_t_kernel(tc, x_bytes, x_scale, node_logits, n
         outputs([28])
         scale_x(31, 1, 0, "xg2")
         quant_h(29, 1)
-        quant_x(31, 1)
         weigh_h(30, 1)
+        quant_x(31, 1)
         outputs([29])
-        mm1(31, 1)
         relu_h(nc.vector, 30, 1, "xg3", 4)
+        mm1(31, 1)
         quant_h(30, 1)
         weigh_h(31, 1)
         relu_h(nc.vector, 31, 1, "xg4", 4)

@@ -87,10 +87,10 @@ def tile_fastfeedforwardnetwork_pa_t_kernel(tc, x_bytes, x_scale, node_logits, n
         load_x(12, 16)
         load_x(16, 20)
 
-        ident = keep.tile([P, P], F32, name="ident")
-        make_identity(nc, ident[:])
         ident16 = keep.tile([P, P], BF16, name="ident16")
         make_identity(nc, ident16[:])
+        ident = keep.tile([P, P], F32, name="ident")
+        make_identity(nc, ident[:])
 
         z = keep.tile([P, NODES, TILES], F32, name="z")
         gate = keep.tile([P, 2, NODES, TILES], F32, name="gate")
@@ -352,9 +352,19 @@ def tile_fastfeedforwardnetwork_pa_t_kernel(tc, x_bytes, x_scale, node_logits, n
                 mm2(i)
                 leave_o(i)
 
+        def warm_up(count):
+            b, bank = take_bank([P, 4, P], F32)
+            for n in range(count):
+                nc.tensor.matmul(
+                    out=bank[:], lhsT=ident16[:], rhs=ident16[:].unsqueeze(1).to_broadcast([P, 4, P]), start=True, stop=True
+                )
+            free_banks.append(b)
+
         scale_row = keep.tile([P, 2, 64], F32, name="scale_row")
+        warm_up(3)
         cast(nc.vector.tensor_copy, 2)
         turn_x(0)
+        warm_up(2)
         gates_sum()
         nc.vector.tensor_copy(
             out=scale_row[:].rearrange("p g (n t) -> p g n t", t=4),
@@ -362,6 +372,7 @@ def tile_fastfeedforwardnetwork_pa_t_kernel(tc, x_bytes, x_scale, node_logits, n
         )
         cast(nc.vector.tensor_copy, 2)
         turn_x(1)
+        warm_up(1)
         cast(nc.gpsimd.tensor_copy, 2)
         turn_x(2)
         gates_sigmoid()

@@ -24,7 +24,7 @@ FLOPS = 2 * TOKENS * D * LF + 2 * TOKENS * LF * E
 BF16_MAX = 3.3895313892515355e38
 GROUPS = [(2 * k, 2) for k in range(14)] + [(i, 1) for i in range(28, TILES)]
 SHARED = (7, 9, 11)
-SCALAR_CASTS = {6: (1, 0), 7: (1, 1), 9: (1, 1), 11: (1, 1), 13: (1, 1)}
+SCALAR_CASTS = {6: (1, 0), 7: (1, 1), 9: (1, 1), 11: (1, 1)}
 
 
 def tile_fastfeedforwardnetwork_pa_t_kernel(tc, x_bytes, x_scale, node_logits, node_b, w1, b1, w2, out):
@@ -38,7 +38,7 @@ def tile_fastfeedforwardnetwork_pa_t_kernel(tc, x_bytes, x_scale, node_logits, n
 
     with ExitStack() as ctx:
         keep = ctx.enter_context(tc.tile_pool(name="keep", bufs=1))
-        xs_pool = ctx.enter_context(tc.tile_pool(name="xs", bufs=12))
+        xs_pool = ctx.enter_context(tc.tile_pool(name="xs", bufs=15))
         two = ctx.enter_context(tc.tile_pool(name="two", bufs=2))
         hq_pool = ctx.enter_context(tc.tile_pool(name="hq", bufs=3))
         o_pool = ctx.enter_context(tc.tile_pool(name="o", bufs=8))
@@ -75,15 +75,15 @@ def tile_fastfeedforwardnetwork_pa_t_kernel(tc, x_bytes, x_scale, node_logits, n
             )
 
         load_x(1, 3)
-        load_x(3, 5)
+        load_x(3, 6)
         load_w1(0)
-        load_x(5, 8)
+        load_x(6, 8)
         load_w1(1)
         bias_h = keep.tile([P, 4], BF16, name="bias_h")
         nc.sync.dma_start(out=bias_h[:], in_=b1_v)
-        load_x(8, 12)
         w2_raw = keep.tile([P, 4, E], BF16, name="w2_raw")
         nc.sync.dma_start(out=w2_raw[:], in_=w2_v)
+        load_x(8, 12)
         load_x(12, 16)
         load_x(16, 20)
 
@@ -241,9 +241,9 @@ def tile_fastfeedforwardnetwork_pa_t_kernel(tc, x_bytes, x_scale, node_logits, n
             for j in range(n):
                 xq[first + j] = (codes, scales, P * n, P * j)
 
-        def mm1(first, n):
+        def mm1(first, n, order=(0, 1, 2, 3)):
             codes, scales, width, at = xq[first]
-            for t in range(4):
+            for t in order:
                 if n == 4 or t % 2 == 0:
                     a_bank[first, t], bank = take_bank([P, 512], F32)
                     used = 0
@@ -372,7 +372,7 @@ def tile_fastfeedforwardnetwork_pa_t_kernel(tc, x_bytes, x_scale, node_logits, n
         )
         cast(nc.vector.tensor_copy, 2)
         turn_x(1)
-        warm_up(1)
+        warm_up(2)
         cast(nc.gpsimd.tensor_copy, 2)
         turn_x(2)
         gates_sigmoid()
@@ -381,10 +381,11 @@ def tile_fastfeedforwardnetwork_pa_t_kernel(tc, x_bytes, x_scale, node_logits, n
         leaf_probabilities()
         turn_x(3)
         scale_x(0, 4, 0, "xg0")
-        turn_x(4)
         weave_w(0)
+        turn_x(4)
         weave_w(1)
         scale_x(0, 4, 1)
+        cast(nc.scalar.copy, 2)
         cast(nc.scalar.copy, 2)
         spread_p(0)
         leave_w(0, "xg2")
@@ -401,29 +402,31 @@ def tile_fastfeedforwardnetwork_pa_t_kernel(tc, x_bytes, x_scale, node_logits, n
         leave_w(2, "xg3")
         leave_w(3, "xg3")
         scale_x(4, 4, 1)
-        cast(nc.vector.tensor_copy, 2)
         quant_w(1)
         turn_x(6)
-        park_p()
         turn_p(0)
         leave_p(0)
-        turn_x(7)
+        park_p()
+        weave_w(4)
         mm1(0, 4)
+        cast(nc.scalar.copy, 2)
         cast(nc.scalar.copy, 2)
         cast(nc.scalar.copy, 2)
         cast(nc.gpsimd.tensor_copy, 5, keep, "xg3")
         scale_x(4, 4, 2)
         weigh_h(0, 4)
         relu_h(nc.gpsimd, 0, 4, "xg0")
+        turn_x(7)
         turn_x(8)
-        turn_x(9)
+        leave_w(4, "w_g2")
         scale_x(4, 4, 3)
         cast(nc.scalar.copy, 1)
         cast(nc.scalar.copy, 2)
-        for n in range(4, 8):
+        for n in range(5, 8):
             weave_w(n)
             leave_w(n, "w_g2" if n < 6 else "xg4")
             if n == 5:
+                turn_x(9)
                 scale_x(8, 2, 0, "xg2")
                 cast(nc.scalar.copy, 1)
         turn_x(10)
@@ -437,10 +440,10 @@ def tile_fastfeedforwardnetwork_pa_t_kernel(tc, x_bytes, x_scale, node_logits, n
         quant_h(0, 4)
         quant_x(8, 2)
         mm1(4, 4)
-        cast(nc.gpsimd.tensor_copy, 3, keep, "xg2")
+        cast(nc.gpsimd.tensor_copy, 4, keep, "xg2")
         weigh_h(4, 4)
         relu_h(nc.gpsimd, 4, 4, "xg1")
-        cast(nc.scalar.copy, 1)
+        cast(nc.scalar.copy, 2)
         cast(nc.scalar.copy, 2)
         outputs([0])
         cast(nc.scalar.copy, 2)
@@ -463,7 +466,7 @@ def tile_fastfeedforwardnetwork_pa_t_kernel(tc, x_bytes, x_scale, node_logits, n
             before, older = GROUPS[k - 1], GROUPS[k - 2]
             gate_tag = f"xg{k % 8}"
             short = k - 1 in SHARED
-            mm1(*before)
+            mm1(*before, (2, 3, 0, 1) if count == 2 else (0, 1, 2, 3))
             if k - 2 in SHARED:
                 weigh_on_gpsimd(older[0], f"xg{(k - 1) % 8}", keep)
             elif left and not short:

from contextlib import ExitStack

import concourse.mybir as mybir
from concourse.masks import make_identity

F32 = mybir.dt.float32
BF16 = mybir.dt.bfloat16
U32 = mybir.dt.uint32
U8 = mybir.dt.uint8
FP8 = mybir.dt.float8_e4m3fn
FP8X4 = mybir.dt.float8_e4m3fn_x4
ACT = mybir.ActivationFunctionType
OP = mybir.AluOpType

P = 128
TOKENS = 4096
D = 1024
LF = 512
E = 1024
LEAVES = 16
NODES = 15
TILES = TOKENS // P
FLOPS = 2 * TOKENS * D * LF + 2 * TOKENS * LF * E
BF16_MAX = 3.3895313892515355e38
GROUPS = [(2 * k, 2) for k in range(14)] + [(i, 1) for i in range(28, TILES)]
SHARED = (7, 9, 11)
SCALAR_CASTS = {6: (1, 0), 7: (1, 1), 9: (1, 1), 11: (1, 1)}


def tile_fastfeedforwardnetwork_pa_t_kernel(tc, x_bytes, x_scale, node_logits, node_b, w1, b1, w2, out):
    nc = tc.nc
    x_v = x_bytes.rearrange("b s k -> (b s) k").rearrange("(p i) k -> p i k", i=TILES)
    out_v = out.rearrange("b s e -> (b s) e").rearrange("(p i) e -> p i e", i=TILES)
    logits_v = node_logits.rearrange("b s v -> (b s) v").rearrange("(p i) v -> p (i v)", i=TILES)
    scale_v = x_scale.rearrange("a b (g p t) -> p (a b g) t", p=P, t=4)
    b1_v = b1.rearrange("l f -> (l f)").rearrange("(m t) -> m t", t=4)
    w2_v = w2.rearrange("l f e -> (l f) e").rearrange("(p j) e -> p j e", j=4)

    with ExitStack() as ctx:
        keep = ctx.enter_context(tc.tile_pool(name="keep", bufs=1))
        xs_pool = ctx.enter_context(tc.tile_pool(name="xs", bufs=15))
        two = ctx.enter_context(tc.tile_pool(name="two", bufs=2))
        hq_pool = ctx.enter_context(tc.tile_pool(name="hq", bufs=3))
        o_pool = ctx.enter_context(tc.tile_pool(name="o", bufs=8))
        psum = ctx.enter_context(tc.psum_pool(name="psum", bufs=1))
        ctx.enter_context(tc.manual_schedule())

        free_banks = list(range(8))

        def take_bank(shape, dtype):
            b = free_banks[0]
            free_banks.remove(b)
            return b, psum.tile(shape, dtype, name=f"bank{b}")

        x8 = keep.tile([P, TILES * D], U8, name="x8")

        def load_x(a, b):
            nc.sync.dma_start(out=x8[:, a * D : b * D], in_=x_v[:, a:b, :].rearrange("p i k -> p (i k)"))

        bias_n = keep.tile([P, NODES], BF16, name="bias_n")
        nc.scalar.dma_start(out=bias_n[:], in_=node_b.partition_broadcast(P))
        scale = keep.tile([P, 2, 4], F32, name="scale")
        nc.scalar.dma_start(out=scale[:], in_=scale_v)
        load_x(0, 1)
        logits = keep.tile([P, TILES * NODES], BF16, name="logits")
        nc.sync.dma_start(out=logits[:], in_=logits_v)

        w1_raw = {}

        def load_w1(g):
            w1_raw[g] = keep.tile([P, LEAVES, P], BF16, name=f"w1_raw{g}")
            nc.sync.dma_start(
                out=w1_raw[g][:],
                in_=w1[:, 512 * g : 512 * (g + 1), :].rearrange("l (p j) f -> p l (j f)", j=4),
            )

        load_x(1, 3)
        load_x(3, 6)
        load_w1(0)
        load_x(6, 8)
        load_w1(1)
        bias_h = keep.tile([P, 4], BF16, name="bias_h")
        nc.sync.dma_start(out=bias_h[:], in_=b1_v)
        w2_raw = keep.tile([P, 4, E], BF16, name="w2_raw")
        nc.sync.dma_start(out=w2_raw[:], in_=w2_v)
        load_x(8, 12)
        load_x(12, 16)
        load_x(16, 20)

        ident16 = keep.tile([P, P], BF16, name="ident16")
        make_identity(nc, ident16[:])
        ident = keep.tile([P, P], F32, name="ident")
        make_identity(nc, ident[:])

        z = keep.tile([P, NODES, TILES], F32, name="z")
        gate = keep.tile([P, 2, NODES, TILES], F32, name="gate")
        leaf = keep.tile([P, 4, LEAVES, 8], F32, name="leaf")
        prep, p_bank, p_sb = {}, {}, {}

        def gates_sum():
            nc.vector.tensor_tensor(
                out=z[:].rearrange("p v (c j) -> p v c j", c=4),
                in0=logits[:].rearrange("p (j c v) -> p v c j", c=4, v=NODES),
                in1=bias_n[:].unsqueeze(2).unsqueeze(3).to_broadcast([P, NODES, 4, 8]),
                op=OP.add,
            )

        def gates_sigmoid():
            nc.scalar.activation(out=gate[:, 0, :, :], in_=z[:], func=ACT.Sigmoid)
            nc.scalar.activation(out=gate[:, 1, :, :], in_=z[:], func=ACT.Sigmoid, scale=-1.0)

        def leaf_probabilities():
            prob = gate[:, :, 0, :]
            for level in range(1, 4):
                n = 2**level
                paths = prob.unsqueeze(2).to_broadcast([P, n, 2, TILES])
                gates = gate[:, :, n - 1 : 2 * n - 1, :].rearrange("p s a i -> p a s i")
                if level < 3:
                    nxt = keep.tile([P, n, 2, TILES], F32, name=f"prob{level}")
                    nc.gpsimd.tensor_tensor(out=nxt[:], in0=paths, in1=gates, op=OP.mult)
                    prob = nxt[:].rearrange("p a s i -> p (a s) i")
                else:
                    nc.gpsimd.tensor_tensor(
                        out=leaf[:].rearrange("p c (a s) j -> p a s c j", s=2),
                        in0=paths.rearrange("p a s (c j) -> p a s c j", c=4),
                        in1=gates.rearrange("p a s (c j) -> p a s c j", c=4),
                        op=OP.mult,
                    )

        def spread_p(q):
            prep[q] = keep.tile([P, 4, LEAVES, 8], F32, name="prep")
            nc.scalar.copy(
                out=prep[q][:],
                in_=leaf[:, :, :, q].unsqueeze(3).to_broadcast([P, 4, LEAVES, 8]),
            )

        def turn_p(q):
            p_bank[q] = take_bank([P, 512], F32)
            for c in range(4):
                rows = prep[q][:, c, :, :].rearrange("p l r -> p (l r)")
                nc.tensor.transpose(p_bank[q][1][:, P * c : P * (c + 1)], rows, ident[:])

        def leave_p(q):
            p_sb[q] = keep.tile([P, 512], F32, name=f"p_sb{q}")
            nc.scalar.copy(out=p_sb[q][:], in_=p_bank[q][1][:])
            free_banks.append(p_bank[q][0])

        p_far = keep.tile([P, 7, 4 * P], F32, name="p_far")

        def park_p():
            b, bank = take_bank([P, 4 * P], F32)
            for c in range(4):
                rows = leaf[:, c, :, :].rearrange("p l j -> p (l j)")
                nc.tensor.transpose(bank[:, P * c : P * (c + 1)], rows, ident[:])
            turned = keep.tile([P, 4 * P], F32, name="turned")
            nc.scalar.copy(out=turned[:], in_=bank[:])
            free_banks.append(b)
            parked = out_v[:, TILES - 1, 0 : 4 * P]
            nc.sync.dma_start(out=parked, in_=turned[:])
            load_x(20, 24)
            rows = parked.rearrange("(l j) n -> l j n", j=8)
            for a, b in ((1, 3), (3, 8)):
                for r in range(8):
                    start = 4 * (r % 2) + r // 2
                    nc.sync.dma_start(out=p_far[start:P:8, a - 1 : b - 1, :], in_=rows[:, a:b, :])
            for a in range(24, TILES, 4):
                load_x(a, a + 4)

        def p_of(first, n):
            row = p_sb[0][:] if first < 4 else p_far[:, first // 4 - 1, :]
            return row[:, P * (first % 4) : P * (first % 4 + n)]

        w1_c = keep.tile([P, 2, LF], U32, name="w1_c", align_bytes=64)
        w1_s = keep.tile([P, 2, LF], U8, name="w1_s", align_bytes=64)
        w2_c = keep.tile([P, E], U32, name="w2_c", align_bytes=64)
        w2_s = keep.tile([P, E], U8, name="w2_s", align_bytes=64)
        w_bank, w_g = {}, {}

        def weave_w(n):
            w_bank[n] = take_bank([P, 1024], BF16)
            for s in range(2):
                if n < 4:
                    t = 2 * (n % 2) + s
                    src = w1_raw[n // 2][:].rearrange("p l (j h t) -> p l h j t", h=8, t=4)[:, :, :, :, t]
                else:
                    e0 = 256 * (n - 4) + P * s
                    src = w2_raw[:, :, e0 : e0 + P].rearrange("p j e -> p e j")
                nc.tensor.matmul(
                    out=w_bank[n][1][:, 512 * s : 512 * (s + 1)], lhsT=ident16[:], rhs=src, start=True, stop=True
                )

        def leave_w(n, tag):
            if n % 2 == 0:
                w_g[n // 2] = keep.tile([P, 2048], BF16, name=tag, align_bytes=64)
            nc.scalar.copy(out=w_g[n // 2][:, 1024 * (n % 2) : 1024 * (n % 2 + 1)], in_=w_bank[n][1][:])
            free_banks.append(w_bank[n][0])

        def quant_w(h):
            if h < 2:
                codes, scales = w1_c[:, h, :], w1_s[:, h, :]
            else:
                cols = slice(512 * (h - 2), 512 * (h - 1))
                codes, scales = w2_c[:, cols], w2_s[:, cols]
            nc.vector.quantize_mx(out=codes.bitcast(FP8X4), scales=scales, in_=w_g[h][:])

        xs, xt, xg, xq, a_plane, a_bank, hp, h1, hg, hq, o_bank = ({} for unused in range(11))

        def widen(copy, first, count, pool=xs_pool, tag="xs"):
            wide = pool.tile([P, 512 * count], BF16, name=tag, align_bytes=64)
            copy(out=wide[:], in_=x8[:, 512 * first : 512 * (first + count)].bitcast(FP8))
            for n in range(count):
                xs[first + n] = wide[:, 512 * n : 512 * (n + 1)]

        def turn_x(i):
            xt[i] = take_bank([P, 2, 2, P], F32)
            for g in range(2):
                words = xs[2 * i + g].bitcast(F32)
                for u in range(2):
                    nc.tensor.transpose(xt[i][1][:, u, g, :], words[:, u:256:2], ident[:])

        def scale_x(first, n, j, tag=None):
            if j == 0:
                xg[first] = keep.tile([P, 2, n, 512], BF16, name=tag, align_bytes=64)
            nc.vector.tensor_tensor(
                out=xg[first][:, :, j, :].rearrange("p g (a n u e) -> p g a n u e", n=16, u=2, e=2),
                in0=xt[first + j][1][:].bitcast(BF16).rearrange("p u g (a n e) -> p g a n u e", n=16, e=2),
                in1=scale_row[:]
                .rearrange("p g (n u e) -> p g n u e", u=2, e=2)
                .unsqueeze(2)
                .to_broadcast([P, 2, 8, 16, 2, 2]),
                op=OP.mult,
            )
            free_banks.append(xt[first + j][0])

        def quant_x(first, n):
            codes = two.tile([P, 256 * n], U32, name="xq_c", align_bytes=64)
            scales = two.tile([P, 256 * n], U8, name="xq_s", align_bytes=64)
            nc.vector.quantize_mx(
                out=codes[:].bitcast(FP8X4), scales=scales[:], in_=xg[first][:].rearrange("p g j c -> p (g j c)")
            )
            for j in range(n):
                xq[first + j] = (codes, scales, P * n, P * j)

        def mm1(first, n, order=(0, 1, 2, 3)):
            codes, scales, width, at = xq[first]
            for t in order:
                if n == 4 or t % 2 == 0:
                    a_bank[first, t], bank = take_bank([P, 512], F32)
                    used = 0
                a_plane[first, t] = bank[:, used : used + P * n]
                used += P * n
                for g in range(2):
                    cols = slice(width * g + at, width * g + at + P * n)
                    nc.tensor.matmul_mx(
                        out=a_plane[first, t],
                        lhsT=w1_c[:, g, P * t : P * (t + 1)].bitcast(FP8X4),
                        lhsT_scale=w1_s[:, g, P * t : P * (t + 1)],
                        rhs=codes[:, cols].bitcast(FP8X4),
                        rhs_scale=scales[:, cols],
                        start=(g == 0),
                        stop=(g == 1),
                    )

        def plane_read(first, n, t):
            if n == 4:
                free_banks.append(a_bank[first, t])
            elif t % 2 == 1:
                free_banks.append(a_bank[first, t - 1])

        def weigh_h(first, n):
            hp[first] = two.tile([P, 4, P * n], BF16, name="hp", align_bytes=64)
            for t in range(4):
                nc.vector.scalar_tensor_tensor(
                    out=hp[first][:, t, :],
                    in0=a_plane[first, t],
                    scalar=bias_h[:, t : t + 1],
                    in1=p_of(first, n),
                    op0=OP.add,
                    op1=OP.mult,
                )
                plane_read(first, n, t)

        def relu_h(engine, first, n, tag, run=1):
            hg[first] = keep.tile([P, 512 * n], BF16, name=tag, align_bytes=64)
            engine.tensor_scalar(
                out=hg[first][:].rearrange("p (c i t) -> p c t i", i=run, t=4),
                in0=hp[first][:].rearrange("p t (c i) -> p c t i", i=run),
                scalar1=BF16_MAX,
                scalar2=0.0,
                op0=OP.min,
                op1=OP.max,
            )

        def leave_h(first, n=2):
            h1[first] = keep.tile([P, 4, P * n], F32, name="h1")
            for t in range(4):
                nc.scalar.activation(
                    out=h1[first][:, t, :], in_=a_plane[first, t], func=ACT.Relu, bias=bias_h[:, t : t + 1]
                )
                plane_read(first, n, t)

        def weigh_on_gpsimd(first, tag, pool, n=2):
            hg[first] = pool.tile([P, 512 * n], BF16, name=tag, align_bytes=64)
            nc.gpsimd.tensor_tensor(
                out=hg[first][:].rearrange("p (n t) -> p n t", t=4),
                in0=h1[first][:].rearrange("p t n -> p n t"),
                in1=p_of(first, n).unsqueeze(2).to_broadcast([P, P * n, 4]),
                op=OP.mult,
            )

        def quant_h(first, n):
            codes = hq_pool.tile([P, P * n], U32, name="hq_c", align_bytes=64)
            scales = hq_pool.tile([P, P * n], U8, name="hq_s", align_bytes=64)
            nc.vector.quantize_mx(out=codes[:].bitcast(FP8X4), scales=scales[:], in_=hg[first][:])
            for j in range(n):
                hq[first + j] = (codes[:, P * j : P * (j + 1)], scales[:, P * j : P * (j + 1)])

        def mm2(i):
            for e in range(2):
                o_bank[i, e] = take_bank([P, 512], F32)
                nc.tensor.matmul_mx(
                    out=o_bank[i, e][1][:],
                    lhsT=hq[i][0].bitcast(FP8X4),
                    lhsT_scale=hq[i][1],
                    rhs=w2_c[:, 512 * e : 512 * (e + 1)].bitcast(FP8X4),
                    rhs_scale=w2_s[:, 512 * e : 512 * (e + 1)],
                    start=True,
                    stop=True,
                )

        def leave_o(i, copies=(nc.scalar.copy, nc.scalar.copy), halves=False):
            o_sb = o_pool.tile([P, E], F32, name="osb")
            for e in range(2):
                cols = slice(512 * e, 512 * (e + 1))
                copies[e](out=o_sb[:, cols], in_=o_bank[i, e][1][:])
                free_banks.append(o_bank[i, e][0])
                if halves:
                    nc.sync.dma_start(out=out_v[:, i, cols], in_=o_sb[:, cols])
            if not halves:
                nc.sync.dma_start(out=out_v[:, i, :], in_=o_sb[:])

        left = list(range(2 * TILES))

        def cast(copy, count, pool=xs_pool, tag="xs"):
            first, count = left[0], min(count, len(left))
            widen(copy, first, count, pool, tag)
            for h in range(first, first + count):
                left.remove(h)

        def outputs(tiles):
            for i in tiles:
                mm2(i)
                leave_o(i)

        def warm_up(count):
            b, bank = take_bank([P, 4, P], F32)
            for n in range(count):
                nc.tensor.matmul(
                    out=bank[:], lhsT=ident16[:], rhs=ident16[:].unsqueeze(1).to_broadcast([P, 4, P]), start=True, stop=True
                )
            free_banks.append(b)

        scale_row = keep.tile([P, 2, 64], F32, name="scale_row")
        warm_up(3)
        cast(nc.vector.tensor_copy, 2)
        turn_x(0)
        warm_up(2)
        gates_sum()
        nc.vector.tensor_copy(
            out=scale_row[:].rearrange("p g (n t) -> p g n t", t=4),
            in_=scale[:].unsqueeze(2).to_broadcast([P, 2, 16, 4]),
        )
        cast(nc.vector.tensor_copy, 2)
        turn_x(1)
        warm_up(2)
        cast(nc.gpsimd.tensor_copy, 2)
        turn_x(2)
        gates_sigmoid()
        cast(nc.scalar.copy, 2)
        cast(nc.scalar.copy, 2)
        leaf_probabilities()
        turn_x(3)
        scale_x(0, 4, 0, "xg0")
        weave_w(0)
        turn_x(4)
        weave_w(1)
        scale_x(0, 4, 1)
        cast(nc.scalar.copy, 2)
        cast(nc.scalar.copy, 2)
        spread_p(0)
        leave_w(0, "xg2")
        leave_w(1, "xg2")
        scale_x(0, 4, 2)
        turn_x(5)
        weave_w(2)
        weave_w(3)
        scale_x(0, 4, 3)
        scale_x(4, 4, 0, "xg1")
        quant_x(0, 4)
        quant_w(0)
        cast(nc.scalar.copy, 2)
        leave_w(2, "xg3")
        leave_w(3, "xg3")
        scale_x(4, 4, 1)
        quant_w(1)
        turn_x(6)
        turn_p(0)
        leave_p(0)
        park_p()
        weave_w(4)
        mm1(0, 4)
        cast(nc.scalar.copy, 2)
        cast(nc.scalar.copy, 2)
        cast(nc.scalar.copy, 2)
        cast(nc.gpsimd.tensor_copy, 5, keep, "xg3")
        scale_x(4, 4, 2)
        weigh_h(0, 4)
        relu_h(nc.gpsimd, 0, 4, "xg0")
        turn_x(7)
        turn_x(8)
        leave_w(4, "w_g2")
        scale_x(4, 4, 3)
        cast(nc.scalar.copy, 1)
        cast(nc.scalar.copy, 2)
        for n in range(5, 8):
            weave_w(n)
            leave_w(n, "w_g2" if n < 6 else "xg4")
            if n == 5:
                turn_x(9)
                scale_x(8, 2, 0, "xg2")
                cast(nc.scalar.copy, 1)
        turn_x(10)
        turn_x(11)
        cast(nc.scalar.copy, 1)
        cast(nc.scalar.copy, 2)
        scale_x(8, 2, 1)
        quant_x(4, 4)
        quant_w(2)
        quant_w(3)
        quant_h(0, 4)
        quant_x(8, 2)
        mm1(4, 4)
        cast(nc.gpsimd.tensor_copy, 4, keep, "xg2")
        weigh_h(4, 4)
        relu_h(nc.gpsimd, 4, 4, "xg1")
        cast(nc.scalar.copy, 2)
        cast(nc.scalar.copy, 2)
        outputs([0])
        cast(nc.scalar.copy, 2)
        mm1(8, 2)
        scale_x(10, 2, 0, "xg6")
        outputs([1])
        cast(nc.scalar.copy, 2)
        scale_x(10, 2, 1)
        turn_x(12)
        turn_x(13)
        outputs([2])
        weigh_h(8, 2)
        outputs([3])
        quant_x(10, 2)
        quant_h(4, 4)

        ready = [4, 5, 6, 7]
        for k in range(6, len(GROUPS) - 1):
            first, count = GROUPS[k]
            before, older = GROUPS[k - 1], GROUPS[k - 2]
            gate_tag = f"xg{k % 8}"
            short = k - 1 in SHARED
            mm1(*before, (2, 3, 0, 1) if count == 2 else (0, 1, 2, 3))
            if k - 2 in SHARED:
                weigh_on_gpsimd(older[0], f"xg{(k - 1) % 8}", keep)
            elif left and not short:
                cast(nc.gpsimd.tensor_copy, 2, keep, gate_tag)
                relu_h(nc.gpsimd, *older, f"hg{k % 2}")
            else:
                relu_h(nc.gpsimd, *older, gate_tag)
            scale_x(first, count, 0, f"xg{(k + 1) % 8}")
            if short:
                leave_h(before[0])
            half = (len(ready) + 1) // 2
            early, late = SCALAR_CASTS.get(k, (0, 0))
            for n in range(early):
                cast(nc.scalar.copy, 2)
            outputs(ready[:half])
            for n in range(late):
                cast(nc.scalar.copy, 2)
            for i in range(first + 2, min(first + 2 + count, TILES)):
                turn_x(i)
            if count == 2:
                scale_x(first, count, 1)
            if not short:
                weigh_h(*before)
            outputs(ready[half:])
            if short:
                quant_h(*older)
                quant_x(first, count)
            else:
                quant_x(first, count)
                quant_h(*older)
            ready = list(range(older[0], older[0] + older[1]))
        mm1(30, 1)
        relu_h(nc.gpsimd, 29, 1, "xg1")
        outputs([28])
        scale_x(31, 1, 0, "xg2")
        quant_h(29, 1)
        weigh_h(30, 1)
        quant_x(31, 1)
        outputs([29])
        relu_h(nc.vector, 30, 1, "xg3", 4)
        mm1(31, 1)
        quant_h(30, 1)
        weigh_h(31, 1)
        relu_h(nc.vector, 31, 1, "xg4", 4)
        mm2(30)
        leave_o(30, halves=True)
        quant_h(31, 1)
        last = o_pool.tile([P, E], F32, name="osb")
        for e in range(4):
            cols = slice(256 * e, 256 * (e + 1))
            b, bank = take_bank([P, 256], F32)
            nc.tensor.matmul_mx(
                out=bank[:],
                lhsT=hq[31][0].bitcast(FP8X4),
                lhsT_scale=hq[31][1],
                rhs=w2_c[:, cols].bitcast(FP8X4),
                rhs_scale=w2_s[:, cols],
                start=True,
                stop=True,
            )
            copy = nc.vector.tensor_copy if e % 2 == 0 else nc.scalar.copy
            copy(out=last[:, cols], in_=bank[:])
            nc.sync.dma_start(out=out_v[:, TILES - 1, cols], in_=last[:, cols])
